import numpy as np
import ml_dtypes


def mxq(x, axis, fmt="e4m3"):
    dtype, down = {"e4m3": (ml_dtypes.float8_e4m3fn, 7), "e5m2": (ml_dtypes.float8_e5m2, 14)}[fmt]
    v = np.moveaxis(np.asarray(x, np.float32).astype(ml_dtypes.bfloat16).astype(np.float64), axis, -1)
    blocks = v.reshape(v.shape[:-1] + (-1, 32))
    amax = np.abs(blocks).max(-1, keepdims=True)
    byte = np.maximum(np.where(amax > 0, np.frexp(amax)[1] - 1 + 127, 0) - down, 1)
    scale = np.exp2(byte - 127.0)
    codes = (blocks / scale).astype(np.float32).astype(dtype).astype(np.float64)
    return np.moveaxis((codes * scale).reshape(v.shape), -1, axis)


WIDE = False


def mx_kscale(k):
    if not WIDE:
        return np.ones(k)
    levels = np.array([10, -10, 5, -5, 0])
    a = np.random.permutation(np.resize(levels, k // 512 * 4)).reshape(k // 512, 4)
    idx = np.arange(k)
    return np.exp2(a[idx // 512, idx % 128 // 32])


BF16 = ml_dtypes.bfloat16


def bf(x):
    return np.asarray(x, np.float32).astype(BF16)


def f64(x):
    return np.asarray(x).astype(np.float64)


E2M1 = np.array([0.0, 0.5, 1.0, 1.5, 2.0, 3.0, 4.0, 6.0, -0.0, -0.5, -1.0, -1.5, -2.0, -3.0, -4.0, -6.0])


def pack_weight(w, fmt):
    k, n = w.shape
    w = f64(bf(w)).reshape(k // 32, 32, n)
    amax = np.abs(w).max(1)
    if fmt == "e4m3":
        byte = np.frexp(amax)[1] - 1 + 127 - 7
    else:
        mant, ex = np.frexp(amax / 6.0)
        byte = np.where(mant > 0.5, ex, ex - 1) + 127
    byte = np.clip(np.where(amax > 0, byte, 1), 1, 254)
    scaled = (w * np.exp2(127.0 - byte)[:, None, :]).reshape(k, n).astype(np.float32)
    by_word = np.ascontiguousarray(scaled.reshape(k // 512, 128, 4, n).transpose(0, 1, 3, 2))
    if fmt == "e4m3":
        words = by_word.astype(ml_dtypes.float8_e4m3fn).view(np.uint8)
    else:
        c = by_word.astype(ml_dtypes.float4_e2m1fn).view(np.uint8) & 0xF
        words = c[..., 0::2] | (c[..., 1::2] << 4)
    return np.ascontiguousarray(words), np.ascontiguousarray(byte.astype(np.uint8).reshape(k // 512, 16, n))


def unpack_weight(words, scales, fmt):
    g, p, n, _ = words.shape
    if fmt == "e4m3":
        vals = np.ascontiguousarray(words).view(ml_dtypes.float8_e4m3fn).astype(np.float64)
    else:
        nib = np.empty((g, p, n, 4), np.uint8)
        nib[..., 0::2] = words & 0xF
        nib[..., 1::2] = words >> 4
        vals = E2M1[nib]
    vals = vals * np.repeat(np.exp2(scales.astype(np.float64) - 127.0), 8, axis=1)[..., None]
    return vals.transpose(0, 1, 3, 2).reshape(g * 512, n)


B, N, LD, HID = 16, 255, 1024, 512
NE = N + 1
DT, DX = 5e-4, 1e-3
FLUX_SCALE = 0.25
EH = 0.5
ET = 13
FMT = "e4m3"


def erfc_pos(a):
    a = np.minimum(a, 9.0)
    acc = np.zeros_like(a)
    for n in range(ET):
        t2 = ((n + 0.5) * EH) ** 2
        acc += np.exp(-t2) / (t2 + a * a)
    return 2.0 * EH * a * np.exp(-a * a) / np.pi * acc + 2.0 / (1.0 + np.exp(2.0 * np.pi * a / EH))


def erf(z):
    return np.sign(z) * (1.0 - erfc_pos(np.abs(z)))


def gelu(v):
    return 0.5 * v * (1.0 + erf(v / np.sqrt(2.0)))


def setup_inputs():
    s = mx_kscale(HID)
    edge_hid = bf(gelu(np.random.standard_normal((B, NE, HID)) * 1.4) * s)
    u = bf(np.random.random((B, N)))
    enc = bf((1.0 + 0.5 * np.random.standard_normal(LD)) / np.sqrt(LD))
    W2_words, W2_scales = pack_weight(np.random.standard_normal((HID, HID)) * 1.2 / np.sqrt(HID) / s[:, None], FMT)
    b2 = bf(np.random.standard_normal(HID) * 0.5)
    W3_words, W3_scales = pack_weight(np.random.standard_normal((HID, LD)) * 1.8 / np.sqrt(HID), FMT)
    b3 = bf(np.random.standard_normal(LD) * 0.5)
    return {"edge_hid": edge_hid,
            "u": u,
            "enc": enc,
            "W2_words": W2_words,
            "W2_scales": W2_scales,
            "b2": b2,
            "W3_words": W3_words,
            "W3_scales": W3_scales,
            "b3": b3}


def reference(edge_hid, u, enc, W2_words, W2_scales, b2, W3_words, W3_scales, b3):
    u, enc = f64(u), f64(enc)
    h = u[..., None] * enc
    x = gelu((mxq(f64(edge_hid), 2, "e4m3") @ unpack_weight(W2_words, W2_scales, FMT)) + f64(b2))
    flux = np.tanh((mxq(x, 2, "e4m3") @ unpack_weight(W3_words, W3_scales, FMT)) + f64(b3)) * FLUX_SCALE
    h_new = h - (DT / DX) * (flux[:, 1:] - flux[:, :-1])
    dec = enc / (np.sum(enc * enc) + 1e-12)
    return np.sum(h_new * dec, axis=-1)

@@ -1,0 +1,285 @@
+from contextlib import ExitStack
+
+import concourse.mybir as mybir
+from concourse.masks import make_identity
+
+F32 = mybir.dt.float32
+BF16 = mybir.dt.bfloat16
+I32 = mybir.dt.int32
+U32 = mybir.dt.uint32
+U8 = mybir.dt.uint8
+FP8X4 = mybir.dt.float8_e4m3fn_x4
+ACT = mybir.ActivationFunctionType
+ALU = mybir.AluOpType
+
+P = 128
+GRIDS = 16
+FACES = 256
+CELLS = 255
+HID = 512
+LATENT = 1024
+GROUP = 512
+TILES = GROUP // P
+GROUPS = GRIDS * FACES // GROUP
+CHUNKS = LATENT // P
+PACK = 4
+FLIP_BANKS = 3
+PRODUCT_BANKS = 4
+
+FLOPS = 2 * GRIDS * FACES * HID * (HID + LATENT)
+
+
+def tile_fluxgnn1dlatent_pb_t_kernel(
+    tc, edge_hid, u, enc, W2_words, W2_scales, b2, W3_words, W3_scales, b3, out
+):
+    nc = tc.nc
+    tokens = edge_hid.flatten_outer_dims()
+
+    with ExitStack() as ctx:
+        ctx.enter_context(tc.manual_schedule())
+        keep = ctx.enter_context(tc.tile_pool(name="keep", bufs=1))
+        work = ctx.enter_context(tc.tile_pool(name="work", bufs=2))
+        psum = ctx.enter_context(tc.psum_pool(name="psum", bufs=1))
+
+        e_in = [keep.tile([P, TILES, HID], BF16, name="e_in%d" % g) for g in range(GROUPS)]
+        w2_words = keep.tile([P, HID], U32, name="w2_words", align_bytes=64)
+        w2_plane = keep.tile([P, HID], U8, name="w2_plane", align_bytes=64)
+        w3_words = keep.tile([P, LATENT], U32, name="w3_words", align_bytes=64)
+        w3_plane = keep.tile([P, LATENT], U8, name="w3_plane", align_bytes=64)
+        rows_bf = keep.tile([P, P], BF16, name="rows_bf")
+        rows = keep.tile([P, P], F32, name="rows")
+        cols = keep.tile([P, P], F32, name="cols")
+        ident = keep.tile([P, P], F32, name="ident")
+        pick = keep.tile([P, 2 * P], F32, name="pick")
+        b2_all = keep.tile([P, HID], F32, name="b2_all")
+        u_bf = keep.tile([GRIDS, CELLS], BF16, name="u_bf")
+        u_gain = keep.tile([GRIDS, CELLS], F32, name="u_gain")
+        warm = keep.tile([P, 1], F32, name="warm")
+        warm_out = keep.tile([P, 1], F32, name="warm_out")
+
+        nc.vector.memset(rows_bf[:], 0.0)
+        nc.vector.memset(warm[:], 0.0)
+        nc.vector.memset(w2_plane[:].bitcast(I32), 0)
+        nc.vector.memset(w3_plane[:].bitcast(I32), 0)
+        nc.vector.memset(pick[:], 0.0)
+        nc.vector.memset(pick[:, P : P + 1], 1.0)
+        make_identity(nc, ident[:])
+
+        def load_tokens(g):
+            nc.sync.dma_start(
+                out=e_in[g][:],
+                in_=tokens[g * GROUP : (g + 1) * GROUP, :].rearrange("(n p) k -> p n k", p=P),
+            )
+
+        def load_weight(words_tile, plane_tile, words, scales):
+            nc.sync.dma_start(
+                out=words_tile[:].bitcast(I32),
+                in_=words[0].rearrange("p n t -> p (n t)").bitcast(I32),
+            )
+            for quad in range(4):
+                nc.sync.dma_start(
+                    out=plane_tile[32 * quad : 32 * quad + 4, :].bitcast(I32),
+                    in_=scales[0, 4 * quad : 4 * quad + 4, :].bitcast(I32),
+                )
+
+        nc.scalar.dma_start(out=rows_bf[0:CHUNKS, :], in_=enc.rearrange("(j p) -> j p", p=P))
+        nc.scalar.dma_start(
+            out=rows_bf[CHUNKS : 2 * CHUNKS, :], in_=b3.rearrange("(j p) -> j p", p=P)
+        )
+        nc.scalar.dma_start(
+            out=rows_bf[2 * CHUNKS : 2 * CHUNKS + TILES, :], in_=b2.rearrange("(j p) -> j p", p=P)
+        )
+        nc.scalar.dma_start(out=u_bf[:], in_=u)
+        load_tokens(0)
+        load_weight(w2_words, w2_plane, W2_words, W2_scales)
+        load_tokens(1)
+        load_weight(w3_words, w3_plane, W3_words, W3_scales)
+        for g in range(2, GROUPS):
+            load_tokens(g)
+
+        nc.scalar.activation(out=warm_out[:], in_=warm[:], func=ACT.Gelu)
+
+        nc.vector.tensor_copy(out=rows[:], in_=rows_bf[:])
+        cols_ps = psum.tile([P, P], F32, tag="flip", bufs=FLIP_BANKS)
+        nc.tensor.transpose(cols_ps[:], rows[:], ident[:])
+        nc.vector.tensor_copy(out=cols[:], in_=cols_ps[:])
+        enc_cols = cols[:, 0:CHUNKS]
+        b3_cols = cols[:, CHUNKS : 2 * CHUNKS]
+        enc_sq = keep.tile([P, CHUNKS], F32, name="enc_sq")
+        enc_sq_sum = keep.tile([P, 1], F32, name="enc_sq_sum")
+        nc.vector.tensor_tensor(out=enc_sq[:], in0=enc_cols, in1=enc_cols, op=ALU.mult)
+        nc.vector.tensor_reduce(
+            out=enc_sq_sum[:], in_=enc_sq[:], axis=mybir.AxisListType.X, op=ALU.add
+        )
+
+        def features_to_partitions(src, grouped, copy_out):
+            src_words = src[:].bitcast(F32)
+            grouped_words = grouped[:].bitcast(F32)
+            for half in range(2):
+                bank = psum.tile([P, 2, 2 * P], F32, tag="flip", bufs=FLIP_BANKS)
+                for n in range(2):
+                    for w in range(2):
+                        nc.tensor.transpose(
+                            bank[:, w, n * P : (n + 1) * P],
+                            src_words[:, 2 * half + n, w : HID // 2 : 2],
+                            ident[:],
+                        )
+                copy_out(
+                    out=grouped_words[:, half * 2 * P : (half + 1) * 2 * P, :],
+                    in_=bank[:].rearrange("p w r -> p r w"),
+                )
+
+        def quantise(grouped, codes, plane):
+            nc.vector.quantize_mx(
+                out=codes[:].bitcast(FP8X4),
+                scales=plane[:],
+                in_=grouped[:].rearrange("p r t -> p (r t)"),
+            )
+
+        def new_operand(name):
+            grouped = work.tile([P, GROUP, PACK], BF16, tag=name + "_grouped", name=name + "_grouped", align_bytes=64)
+            codes = work.tile([P, GROUP], U32, tag=name + "_codes", name=name + "_codes", align_bytes=64)
+            plane = work.tile([P, GROUP], U8, tag=name + "_plane", name=name + "_plane", align_bytes=64)
+            return grouped, codes, plane
+
+        e_mx = {}
+        x_mx = {}
+        pre_act = {}
+        x_bf = {}
+        weighted = {}
+
+        def flip_edge_hid(g):
+            e_mx[g] = new_operand("e")
+            features_to_partitions(e_in[g], e_mx[g][0], nc.scalar.copy)
+
+        def flip_x(g):
+            x_mx[g] = new_operand("x")
+            features_to_partitions(x_bf[g], x_mx[g][0], nc.vector.tensor_copy)
+
+        def layer1_product(g, n):
+            if n == 0:
+                pre_act[g] = work.tile([P, TILES, HID], F32, tag="pre_act", name="pre_act")
+                x_bf[g] = work.tile([P, TILES, HID], BF16, tag="x_bf", name="x_bf")
+            product = psum.tile([P, HID], F32, tag="product", bufs=PRODUCT_BANKS)
+            nc.tensor.matmul_mx(
+                out=product[:],
+                lhsT=e_mx[g][1][:, n * P : (n + 1) * P].bitcast(FP8X4),
+                lhsT_scale=e_mx[g][2][:, n * P : (n + 1) * P],
+                rhs=w2_words[:].bitcast(FP8X4),
+                rhs_scale=w2_plane[:],
+                start=True,
+                stop=True,
+            )
+            nc.vector.tensor_tensor(out=pre_act[g][:, n, :], in0=product[:], in1=b2_all[:], op=ALU.add)
+
+        def layer1_gelu(g, n):
+            nc.scalar.activation(out=x_bf[g][:, n, :], in_=pre_act[g][:, n, :], func=ACT.Gelu)
+
+        def layer2(g, j):
+            if j == 0:
+                weighted[g] = work.tile([P, GROUP], F32, tag="weighted", name="weighted")
+            product = psum.tile([P, GROUP], F32, tag="product", bufs=PRODUCT_BANKS)
+            nc.tensor.matmul_mx(
+                out=product[:],
+                lhsT=w3_words[:, j * P : (j + 1) * P].bitcast(FP8X4),
+                lhsT_scale=w3_plane[:, j * P : (j + 1) * P],
+                rhs=x_mx[g][1][:].bitcast(FP8X4),
+                rhs_scale=x_mx[g][2][:],
+                start=True,
+                stop=True,
+            )
+            tanh = work.tile([P, GROUP], F32, tag="tanh", name="tanh", bufs=4)
+            nc.scalar.activation(out=tanh[:], in_=product[:], func=ACT.Tanh, bias=b3_cols[:, j : j + 1])
+            if j == 0:
+                nc.vector.tensor_scalar(
+                    out=weighted[g][:], in0=tanh[:], scalar1=dec_cols[:, 0:1], scalar2=None, op0=ALU.mult
+                )
+            else:
+                nc.vector.scalar_tensor_tensor(
+                    out=weighted[g][:],
+                    in0=tanh[:],
+                    scalar=dec_cols[:, j : j + 1],
+                    in1=weighted[g][:],
+                    op0=ALU.mult,
+                    op1=ALU.add,
+                )
+
+        sums = psum.tile([P, FACES], F32, tag="sums", bufs=1)
+
+        def sum_over_partitions(g):
+            for half in range(GROUP // FACES):
+                b = g * (GROUP // FACES) + half
+                nc.tensor.matmul(
+                    out=sums[:],
+                    lhsT=pick[:, P - b : 2 * P - b],
+                    rhs=weighted[g][:, half * FACES : (half + 1) * FACES],
+                    start=(b == 0),
+                    stop=(b == GRIDS - 1),
+                )
+
+        flip_edge_hid(0)
+        quantise(*e_mx[0])
+
+        b2_ps = psum.tile([P, HID], F32, tag="product", bufs=PRODUCT_BANKS)
+        for n in range(TILES):
+            nc.tensor.matmul(
+                out=b2_ps[:, n * P : (n + 1) * P],
+                lhsT=cols[:, 2 * CHUNKS + n : 2 * CHUNKS + n + 1].to_broadcast([P, P]),
+                rhs=ident[:],
+                start=True,
+                stop=True,
+            )
+        nc.scalar.copy(out=b2_all[:], in_=b2_ps[:])
+        sq_ps = psum.tile([P, P], F32, tag="product", bufs=PRODUCT_BANKS)
+        nc.tensor.matmul(
+            out=sq_ps[:], lhsT=enc_sq_sum[:, 0:1].to_broadcast([P, P]), rhs=ident[:], start=True, stop=True
+        )
+        norm = keep.tile([P, 1], F32, name="norm")
+        norm_eps = keep.tile([P, 1], F32, name="norm_eps")
+        inv_norm = keep.tile([P, 1], F32, name="inv_norm")
+        gain = keep.tile([P, 1], F32, name="gain")
+        dec_cols = keep.tile([P, CHUNKS], F32, name="dec_cols")
+        nc.vector.tensor_reduce(out=norm[:], in_=sq_ps[:], axis=mybir.AxisListType.X, op=ALU.add)
+        nc.vector.tensor_scalar_add(out=norm_eps[:], in0=norm[:], scalar1=1e-12)
+        nc.vector.reciprocal(out=inv_norm[:], in_=norm_eps[:])
+        nc.vector.tensor_tensor(out=gain[:], in0=norm[:], in1=inv_norm[:], op=ALU.mult)
+        nc.vector.tensor_scalar(
+            out=dec_cols[:], in0=enc_cols, scalar1=inv_norm[:, 0:1], scalar2=-0.125, op0=ALU.mult, op1=ALU.mult
+        )
+        nc.vector.tensor_scalar(
+            out=u_gain[:], in0=u_bf[:], scalar1=gain[0:GRIDS, 0:1], scalar2=None, op0=ALU.mult
+        )
+
+        def live(g):
+            return 0 <= g < GROUPS
+
+        def products(step, n):
+            if live(step - 1):
+                layer1_product(step - 1, n)
+            if live(step - 3):
+                layer2(step - 3, 2 * n)
+                layer2(step - 3, 2 * n + 1)
+            if live(step - 1):
+                layer1_gelu(step - 1, n)
+
+        for step in range(1, GROUPS + 4):
+            products(step, 0)
+            products(step, 1)
+            if live(step - 4):
+                sum_over_partitions(step - 4)
+            if live(step):
+                flip_edge_hid(step)
+            if live(step - 2):
+                flip_x(step - 2)
+            if live(step):
+                quantise(*e_mx[step])
+            if live(step - 2):
+                quantise(*x_mx[step - 2])
+            products(step, 2)
+            products(step, 3)
+
+        left = keep.tile([GRIDS, CELLS], F32, name="left")
+        result = keep.tile([GRIDS, CELLS], F32, name="result")
+        nc.vector.tensor_tensor(out=left[:], in0=u_gain[:], in1=sums[0:GRIDS, 0:CELLS], op=ALU.subtract)
+        nc.vector.tensor_tensor(out=result[:], in0=left[:], in1=sums[0:GRIDS, 1 : CELLS + 1], op=ALU.add)
+        nc.sync.dma_start(out=out, in_=result[:])

@@ -11,6 +11,7 @@ U8 = mybir.dt.uint8
 FP8X4 = mybir.dt.float8_e4m3fn_x4
 ACT = mybir.ActivationFunctionType
 ALU = mybir.AluOpType
+ALONG_FREE = mybir.AxisListType.X
 
 P = 128
 GRIDS = 16
@@ -18,13 +19,26 @@ FACES = 256
 CELLS = 255
 HID = 512
 LATENT = 1024
-GROUP = 512
-TILES = GROUP // P
-GROUPS = GRIDS * FACES // GROUP
-CHUNKS = LATENT // P
 PACK = 4
-FLIP_BANKS = 3
-PRODUCT_BANKS = 4
+TILES = GRIDS * FACES // P
+GROUP = 2 * FACES
+PAIR = 2 * GROUP
+GRIDS_IN_PAIR = PAIR // FACES
+CHUNKS = LATENT // P
+JOBS = CHUNKS * GRIDS * FACES // GROUP
+
+FLIP_BANKS = 2
+PRODUCT_BANKS = 5
+
+LAG_QUANTISE_E = 2
+LAG_LAYER1 = 4
+LAG_GELU = 5
+LAG_FLIP_X = 7
+LAG_QUANTISE_X = 8
+LAG_LAYER2 = 16
+LAG_WEIGH = 17
+LAG_SUM = 26
+QUARTERS = 2 * (GRIDS - 1) + LAG_SUM + 1
 
 FLOPS = 2 * GRIDS * FACES * HID * (HID + LATENT)
 
@@ -41,7 +55,7 @@ def tile_fluxgnn1dlatent_pb_t_kernel(
         work = ctx.enter_context(tc.tile_pool(name="work", bufs=2))
         psum = ctx.enter_context(tc.psum_pool(name="psum", bufs=1))
 
-        e_in = [keep.tile([P, TILES, HID], BF16, name="e_in%d" % g) for g in range(GROUPS)]
+        e_in = [keep.tile([P, 2, HID], BF16, name="e_in%d" % b) for b in range(GRIDS)]
         w2_words = keep.tile([P, HID], U32, name="w2_words", align_bytes=64)
         w2_plane = keep.tile([P, HID], U8, name="w2_plane", align_bytes=64)
         w3_words = keep.tile([P, LATENT], U32, name="w3_words", align_bytes=64)
@@ -50,25 +64,31 @@ def tile_fluxgnn1dlatent_pb_t_kernel(
         rows = keep.tile([P, P], F32, name="rows")
         cols = keep.tile([P, P], F32, name="cols")
         ident = keep.tile([P, P], F32, name="ident")
+        ones = keep.tile([P, P], BF16, name="ones")
         pick = keep.tile([P, 2 * P], F32, name="pick")
+        b2_row = keep.tile([P, HID], BF16, name="b2_row")
         b2_all = keep.tile([P, HID], F32, name="b2_all")
         u_bf = keep.tile([GRIDS, CELLS], BF16, name="u_bf")
-        u_gain = keep.tile([GRIDS, CELLS], F32, name="u_gain")
         warm = keep.tile([P, 1], F32, name="warm")
         warm_out = keep.tile([P, 1], F32, name="warm_out")
+        last_bank = psum.tile([P, 2 * FACES], F32, tag="last_bank", bufs=1)
+        sums = last_bank[:, 0:FACES]
+        enc_sq_all = last_bank[:, FACES : FACES + P]
 
         nc.vector.memset(rows_bf[:], 0.0)
-        nc.vector.memset(warm[:], 0.0)
+        nc.vector.memset(b2_row[:], 0.0)
         nc.vector.memset(w2_plane[:].bitcast(I32), 0)
+        nc.vector.memset(warm[:], 0.0)
+        nc.vector.memset(ones[:], 1.0)
         nc.vector.memset(w3_plane[:].bitcast(I32), 0)
-        nc.vector.memset(pick[:], 0.0)
-        nc.vector.memset(pick[:, P : P + 1], 1.0)
         make_identity(nc, ident[:])
+        nc.gpsimd.memset(pick[:], 0.0)
+        nc.gpsimd.memset(pick[:, P : P + 1], 1.0)
 
-        def load_tokens(g):
+        def load_grid(b):
             nc.sync.dma_start(
-                out=e_in[g][:],
-                in_=tokens[g * GROUP : (g + 1) * GROUP, :].rearrange("(n p) k -> p n k", p=P),
+                out=e_in[b][:],
+                in_=tokens[b * FACES : (b + 1) * FACES, :].rearrange("(n p) k -> p n k", p=P),
             )
 
         def load_weight(words_tile, plane_tile, words, scales):
@@ -82,24 +102,188 @@ def tile_fluxgnn1dlatent_pb_t_kernel(
                     in_=scales[0, 4 * quad : 4 * quad + 4, :].bitcast(I32),
                 )
 
+        nc.scalar.dma_start(out=b2_row[0:1, :], in_=b2.unsqueeze(0))
         nc.scalar.dma_start(out=rows_bf[0:CHUNKS, :], in_=enc.rearrange("(j p) -> j p", p=P))
         nc.scalar.dma_start(
             out=rows_bf[CHUNKS : 2 * CHUNKS, :], in_=b3.rearrange("(j p) -> j p", p=P)
         )
-        nc.scalar.dma_start(
-            out=rows_bf[2 * CHUNKS : 2 * CHUNKS + TILES, :], in_=b2.rearrange("(j p) -> j p", p=P)
-        )
         nc.scalar.dma_start(out=u_bf[:], in_=u)
-        load_tokens(0)
+        load_grid(0)
         load_weight(w2_words, w2_plane, W2_words, W2_scales)
-        load_tokens(1)
+        for b in range(1, GRIDS_IN_PAIR):
+            load_grid(b)
         load_weight(w3_words, w3_plane, W3_words, W3_scales)
-        for g in range(2, GROUPS):
-            load_tokens(g)
+        for b in range(GRIDS_IN_PAIR, GRIDS):
+            load_grid(b)
 
         nc.scalar.activation(out=warm_out[:], in_=warm[:], func=ACT.Gelu)
 
+        b2_ps = psum.tile([P, HID], F32, tag="product", bufs=PRODUCT_BANKS)
+        nc.tensor.matmul(out=b2_ps[:], lhsT=ones[:], rhs=b2_row[:], start=True, stop=True)
+        nc.scalar.copy(out=b2_all[:], in_=b2_ps[:])
         nc.vector.tensor_copy(out=rows[:], in_=rows_bf[:])
+
+        e_bank, e_grouped, e_codes, e_plane = {}, {}, {}, {}
+        x_bank, x_grouped, x_codes, x_plane = {}, {}, {}, {}
+        product1, pre_act, x_bf = {}, {}, {}
+        product2, tanh, weighted = {}, {}, {}
+
+        def flip(src):
+            bank = psum.tile([P, 2, FACES], F32, tag="flip", bufs=FLIP_BANKS)
+            words = src[:].bitcast(F32)
+            for n in range(2):
+                for w in range(2):
+                    nc.tensor.transpose(
+                        bank[:, w, n * P : (n + 1) * P], words[:, n, w : HID // 2 : 2], ident[:]
+                    )
+            return bank[:].rearrange("p w r -> p r w")
+
+        def flip_edge_hid(b):
+            if 0 <= b < GRIDS:
+                e_bank[b] = flip(e_in[b])
+
+        def copy_edge_hid(b):
+            if 0 <= b < GRIDS:
+                e_grouped[b] = work.tile([P, FACES, PACK], BF16, tag="e_grouped", name="e_grouped", align_bytes=64)
+                nc.scalar.copy(out=e_grouped[b][:].bitcast(F32), in_=e_bank[b])
+
+        def quantise_edge_hid(b):
+            if 0 <= b < GRIDS:
+                e_codes[b] = work.tile([P, FACES], U32, tag="e_codes", name="e_codes", bufs=3, align_bytes=64)
+                e_plane[b] = work.tile([P, FACES], U8, tag="e_plane", name="e_plane", bufs=3, align_bytes=64)
+                nc.vector.quantize_mx(
+                    out=e_codes[b][:].bitcast(FP8X4),
+                    scales=e_plane[b][:],
+                    in_=e_grouped[b][:].rearrange("p r t -> p (r t)"),
+                )
+
+        def layer1_product(t):
+            if 0 <= t < TILES:
+                b, n = divmod(t, 2)
+                product1[t] = psum.tile([P, HID], F32, tag="product", name="product1", bufs=PRODUCT_BANKS)
+                nc.tensor.matmul_mx(
+                    out=product1[t][:],
+                    lhsT=e_codes[b][:, n * P : (n + 1) * P].bitcast(FP8X4),
+                    lhsT_scale=e_plane[b][:, n * P : (n + 1) * P],
+                    rhs=w2_words[:].bitcast(FP8X4),
+                    rhs_scale=w2_plane[:],
+                    start=True,
+                    stop=True,
+                )
+
+        def add_bias(t):
+            if 0 <= t < TILES:
+                pre_act[t] = work.tile([P, HID], F32, tag="pre_act", name="pre_act", bufs=3)
+                nc.vector.tensor_tensor(out=pre_act[t][:], in0=product1[t][:], in1=b2_all[:], op=ALU.add)
+
+        def gelu(t):
+            if 0 <= t < TILES:
+                b, n = divmod(t, 2)
+                if n == 0:
+                    x_bf[b] = work.tile([P, 2, HID], BF16, tag="x_bf", name="x_bf", bufs=3)
+                nc.scalar.activation(out=x_bf[b][:, n, :], in_=pre_act[t][:], func=ACT.Gelu)
+
+        def flip_x(b):
+            if 0 <= b < GRIDS:
+                x_bank[b] = flip(x_bf[b])
+
+        def copy_x(b):
+            if 0 <= b < GRIDS:
+                x_grouped[b] = work.tile([P, FACES, PACK], BF16, tag="x_grouped", name="x_grouped", align_bytes=64)
+                nc.vector.tensor_copy(out=x_grouped[b][:].bitcast(F32), in_=x_bank[b])
+
+        def quantise_x(b):
+            if 0 <= b < GRIDS:
+                pair, place = divmod(b, GRIDS_IN_PAIR)
+                if place == 0:
+                    x_codes[pair] = work.tile([P, PAIR], U32, tag="x_codes", name="x_codes", align_bytes=64)
+                    x_plane[pair] = work.tile([P, PAIR], U8, tag="x_plane", name="x_plane", align_bytes=64)
+                nc.vector.quantize_mx(
+                    out=x_codes[pair][:, place * FACES : (place + 1) * FACES].bitcast(FP8X4),
+                    scales=x_plane[pair][:, place * FACES : (place + 1) * FACES],
+                    in_=x_grouped[b][:].rearrange("p r t -> p (r t)"),
+                )
+
+        def job(k):
+            pair, rest = divmod(k, 2 * CHUNKS)
+            j, member = divmod(rest, 2)
+            return pair, j, slice(member * GROUP, (member + 1) * GROUP)
+
+        def layer2_product(k):
+            if 0 <= k < JOBS:
+                pair, j, group = job(k)
+                product2[k] = psum.tile([P, GROUP], F32, tag="product", name="product2", bufs=PRODUCT_BANKS)
+                nc.tensor.matmul_mx(
+                    out=product2[k][:],
+                    lhsT=w3_words[:, j * P : (j + 1) * P].bitcast(FP8X4),
+                    lhsT_scale=w3_plane[:, j * P : (j + 1) * P],
+                    rhs=x_codes[pair][:, group].bitcast(FP8X4),
+                    rhs_scale=x_plane[pair][:, group],
+                    start=True,
+                    stop=True,
+                )
+
+        def tanh_of(k):
+            if 0 <= k < JOBS:
+                pair, j, group = job(k)
+                tanh[k] = work.tile([P, GROUP], F32, tag="tanh", name="tanh", bufs=5)
+                nc.scalar.activation(out=tanh[k][:], in_=product2[k][:], func=ACT.Tanh, bias=b3_cols[:, j : j + 1])
+
+        def weigh(k):
+            if 0 <= k < JOBS:
+                pair, j, group = job(k)
+                if k % (2 * CHUNKS) == 0:
+                    weighted[pair] = work.tile([P, PAIR], F32, tag="weighted", name="weighted")
+                if j == 0:
+                    nc.vector.tensor_scalar(
+                        out=weighted[pair][:, group], in0=tanh[k][:], scalar1=enc_cols[:, 0:1], scalar2=None, op0=ALU.mult
+                    )
+                else:
+                    nc.vector.scalar_tensor_tensor(
+                        out=weighted[pair][:, group],
+                        in0=tanh[k][:],
+                        scalar=enc_cols[:, j : j + 1],
+                        in1=weighted[pair][:, group],
+                        op0=ALU.mult,
+                        op1=ALU.add,
+                    )
+
+        def sum_over_partitions(b):
+            if 0 <= b < GRIDS:
+                pair, place = divmod(b, GRIDS_IN_PAIR)
+                nc.tensor.matmul(
+                    out=sums,
+                    lhsT=pick[:, P - b : 2 * P - b],
+                    rhs=weighted[pair][:, place * FACES : (place + 1) * FACES],
+                    start=(b == 0),
+                    stop=(b == GRIDS - 1),
+                )
+
+        def quarter(q):
+            def grid_of(lag):
+                return (q - lag) // 2 if (q - lag) % 2 == 0 else -1
+
+            layer1_product(q - LAG_LAYER1)
+            layer2_product(2 * (q - LAG_LAYER2))
+            layer2_product(2 * (q - LAG_LAYER2) + 1)
+            flip_edge_hid(grid_of(0))
+            flip_x(grid_of(LAG_FLIP_X))
+            sum_over_partitions(grid_of(LAG_SUM))
+
+            gelu(q - LAG_GELU)
+            tanh_of(2 * (q - LAG_LAYER2))
+            tanh_of(2 * (q - LAG_LAYER2) + 1)
+            copy_edge_hid(grid_of(0))
+
+            add_bias(q - LAG_LAYER1)
+            weigh(2 * (q - LAG_WEIGH))
+            weigh(2 * (q - LAG_WEIGH) + 1)
+            copy_x(grid_of(LAG_FLIP_X))
+            quantise_edge_hid(grid_of(LAG_QUANTISE_E))
+            quantise_x(grid_of(LAG_QUANTISE_X))
+
+        quarter(0)
+
         cols_ps = psum.tile([P, P], F32, tag="flip", bufs=FLIP_BANKS)
         nc.tensor.transpose(cols_ps[:], rows[:], ident[:])
         nc.vector.tensor_copy(out=cols[:], in_=cols_ps[:])
@@ -108,178 +292,50 @@ def tile_fluxgnn1dlatent_pb_t_kernel(
         enc_sq = keep.tile([P, CHUNKS], F32, name="enc_sq")
         enc_sq_sum = keep.tile([P, 1], F32, name="enc_sq_sum")
         nc.vector.tensor_tensor(out=enc_sq[:], in0=enc_cols, in1=enc_cols, op=ALU.mult)
-        nc.vector.tensor_reduce(
-            out=enc_sq_sum[:], in_=enc_sq[:], axis=mybir.AxisListType.X, op=ALU.add
-        )
+        nc.vector.tensor_reduce(out=enc_sq_sum[:], in_=enc_sq[:], axis=ALONG_FREE, op=ALU.add)
 
-        def features_to_partitions(src, grouped, copy_out):
-            src_words = src[:].bitcast(F32)
-            grouped_words = grouped[:].bitcast(F32)
-            for half in range(2):
-                bank = psum.tile([P, 2, 2 * P], F32, tag="flip", bufs=FLIP_BANKS)
-                for n in range(2):
-                    for w in range(2):
-                        nc.tensor.transpose(
-                            bank[:, w, n * P : (n + 1) * P],
-                            src_words[:, 2 * half + n, w : HID // 2 : 2],
-                            ident[:],
-                        )
-                copy_out(
-                    out=grouped_words[:, half * 2 * P : (half + 1) * 2 * P, :],
-                    in_=bank[:].rearrange("p w r -> p r w"),
-                )
+        quarter(1)
+        quarter(2)
 
-        def quantise(grouped, codes, plane):
-            nc.vector.quantize_mx(
-                out=codes[:].bitcast(FP8X4),
-                scales=plane[:],
-                in_=grouped[:].rearrange("p r t -> p (r t)"),
-            )
-
-        def new_operand(name):
-            grouped = work.tile([P, GROUP, PACK], BF16, tag=name + "_grouped", name=name + "_grouped", align_bytes=64)
-            codes = work.tile([P, GROUP], U32, tag=name + "_codes", name=name + "_codes", align_bytes=64)
-            plane = work.tile([P, GROUP], U8, tag=name + "_plane", name=name + "_plane", align_bytes=64)
-            return grouped, codes, plane
-
-        e_mx = {}
-        x_mx = {}
-        pre_act = {}
-        x_bf = {}
-        weighted = {}
-
-        def flip_edge_hid(g):
-            e_mx[g] = new_operand("e")
-            features_to_partitions(e_in[g], e_mx[g][0], nc.scalar.copy)
-
-        def flip_x(g):
-            x_mx[g] = new_operand("x")
-            features_to_partitions(x_bf[g], x_mx[g][0], nc.vector.tensor_copy)
-
-        def layer1_product(g, n):
-            if n == 0:
-                pre_act[g] = work.tile([P, TILES, HID], F32, tag="pre_act", name="pre_act")
-                x_bf[g] = work.tile([P, TILES, HID], BF16, tag="x_bf", name="x_bf")
-            product = psum.tile([P, HID], F32, tag="product", bufs=PRODUCT_BANKS)
-            nc.tensor.matmul_mx(
-                out=product[:],
-                lhsT=e_mx[g][1][:, n * P : (n + 1) * P].bitcast(FP8X4),
-                lhsT_scale=e_mx[g][2][:, n * P : (n + 1) * P],
-                rhs=w2_words[:].bitcast(FP8X4),
-                rhs_scale=w2_plane[:],
-                start=True,
-                stop=True,
-            )
-            nc.vector.tensor_tensor(out=pre_act[g][:, n, :], in0=product[:], in1=b2_all[:], op=ALU.add)
-
-        def layer1_gelu(g, n):
-            nc.scalar.activation(out=x_bf[g][:, n, :], in_=pre_act[g][:, n, :], func=ACT.Gelu)
-
-        def layer2(g, j):
-            if j == 0:
-                weighted[g] = work.tile([P, GROUP], F32, tag="weighted", name="weighted")
-            product = psum.tile([P, GROUP], F32, tag="product", bufs=PRODUCT_BANKS)
-            nc.tensor.matmul_mx(
-                out=product[:],
-                lhsT=w3_words[:, j * P : (j + 1) * P].bitcast(FP8X4),
-                lhsT_scale=w3_plane[:, j * P : (j + 1) * P],
-                rhs=x_mx[g][1][:].bitcast(FP8X4),
-                rhs_scale=x_mx[g][2][:],
-                start=True,
-                stop=True,
-            )
-            tanh = work.tile([P, GROUP], F32, tag="tanh", name="tanh", bufs=4)
-            nc.scalar.activation(out=tanh[:], in_=product[:], func=ACT.Tanh, bias=b3_cols[:, j : j + 1])
-            if j == 0:
-                nc.vector.tensor_scalar(
-                    out=weighted[g][:], in0=tanh[:], scalar1=dec_cols[:, 0:1], scalar2=None, op0=ALU.mult
-                )
-            else:
-                nc.vector.scalar_tensor_tensor(
-                    out=weighted[g][:],
-                    in0=tanh[:],
-                    scalar=dec_cols[:, j : j + 1],
-                    in1=weighted[g][:],
-                    op0=ALU.mult,
-                    op1=ALU.add,
-                )
-
-        sums = psum.tile([P, FACES], F32, tag="sums", bufs=1)
-
-        def sum_over_partitions(g):
-            for half in range(GROUP // FACES):
-                b = g * (GROUP // FACES) + half
-                nc.tensor.matmul(
-                    out=sums[:],
-                    lhsT=pick[:, P - b : 2 * P - b],
-                    rhs=weighted[g][:, half * FACES : (half + 1) * FACES],
-                    start=(b == 0),
-                    stop=(b == GRIDS - 1),
-                )
-
-        flip_edge_hid(0)
-        quantise(*e_mx[0])
-
-        b2_ps = psum.tile([P, HID], F32, tag="product", bufs=PRODUCT_BANKS)
-        for n in range(TILES):
-            nc.tensor.matmul(
-                out=b2_ps[:, n * P : (n + 1) * P],
-                lhsT=cols[:, 2 * CHUNKS + n : 2 * CHUNKS + n + 1].to_broadcast([P, P]),
-                rhs=ident[:],
-                start=True,
-                stop=True,
-            )
-        nc.scalar.copy(out=b2_all[:], in_=b2_ps[:])
-        sq_ps = psum.tile([P, P], F32, tag="product", bufs=PRODUCT_BANKS)
         nc.tensor.matmul(
-            out=sq_ps[:], lhsT=enc_sq_sum[:, 0:1].to_broadcast([P, P]), rhs=ident[:], start=True, stop=True
+            out=enc_sq_all, lhsT=enc_sq_sum[:, 0:1].to_broadcast([P, P]), rhs=ident[:], start=True, stop=True
         )
         norm = keep.tile([P, 1], F32, name="norm")
         norm_eps = keep.tile([P, 1], F32, name="norm_eps")
         inv_norm = keep.tile([P, 1], F32, name="inv_norm")
         gain = keep.tile([P, 1], F32, name="gain")
-        dec_cols = keep.tile([P, CHUNKS], F32, name="dec_cols")
-        nc.vector.tensor_reduce(out=norm[:], in_=sq_ps[:], axis=mybir.AxisListType.X, op=ALU.add)
+        right_scale = keep.tile([P, 1], F32, name="right_scale")
+        left_scale = keep.tile([P, 1], F32, name="left_scale")
+        u_gain = keep.tile([GRIDS, CELLS], F32, name="u_gain")
+        nc.vector.tensor_reduce(out=norm[:], in_=enc_sq_all, axis=ALONG_FREE, op=ALU.add)
         nc.vector.tensor_scalar_add(out=norm_eps[:], in0=norm[:], scalar1=1e-12)
         nc.vector.reciprocal(out=inv_norm[:], in_=norm_eps[:])
         nc.vector.tensor_tensor(out=gain[:], in0=norm[:], in1=inv_norm[:], op=ALU.mult)
-        nc.vector.tensor_scalar(
-            out=dec_cols[:], in0=enc_cols, scalar1=inv_norm[:, 0:1], scalar2=-0.125, op0=ALU.mult, op1=ALU.mult
-        )
+        nc.vector.tensor_scalar_mul(out=right_scale[:], in0=inv_norm[:], scalar1=-0.125)
+        nc.vector.tensor_scalar_mul(out=left_scale[:], in0=inv_norm[:], scalar1=0.125)
         nc.vector.tensor_scalar(
             out=u_gain[:], in0=u_bf[:], scalar1=gain[0:GRIDS, 0:1], scalar2=None, op0=ALU.mult
         )
 
-        def live(g):
-            return 0 <= g < GROUPS
-
-        def products(step, n):
-            if live(step - 1):
-                layer1_product(step - 1, n)
-            if live(step - 3):
-                layer2(step - 3, 2 * n)
-                layer2(step - 3, 2 * n + 1)
-            if live(step - 1):
-                layer1_gelu(step - 1, n)
-
-        for step in range(1, GROUPS + 4):
-            products(step, 0)
-            products(step, 1)
-            if live(step - 4):
-                sum_over_partitions(step - 4)
-            if live(step):
-                flip_edge_hid(step)
-            if live(step - 2):
-                flip_x(step - 2)
-            if live(step):
-                quantise(*e_mx[step])
-            if live(step - 2):
-                quantise(*x_mx[step - 2])
-            products(step, 2)
-            products(step, 3)
+        for q in range(3, QUARTERS):
+            quarter(q)
 
         left = keep.tile([GRIDS, CELLS], F32, name="left")
         result = keep.tile([GRIDS, CELLS], F32, name="result")
-        nc.vector.tensor_tensor(out=left[:], in0=u_gain[:], in1=sums[0:GRIDS, 0:CELLS], op=ALU.subtract)
-        nc.vector.tensor_tensor(out=result[:], in0=left[:], in1=sums[0:GRIDS, 1 : CELLS + 1], op=ALU.add)
+        nc.vector.scalar_tensor_tensor(
+            out=left[:],
+            in0=last_bank[0:GRIDS, 0:CELLS],
+            scalar=left_scale[0:GRIDS, 0:1],
+            in1=u_gain[:],
+            op0=ALU.mult,
+            op1=ALU.add,
+        )
+        nc.vector.scalar_tensor_tensor(
+            out=result[:],
+            in0=last_bank[0:GRIDS, 1 : CELLS + 1],
+            scalar=right_scale[0:GRIDS, 0:1],
+            in1=left[:],
+            op0=ALU.mult,
+            op1=ALU.add,
+        )
         nc.sync.dma_start(out=out, in_=result[:])

@@ -27,17 +27,17 @@ GRIDS_IN_PAIR = PAIR // FACES
 CHUNKS = LATENT // P
 JOBS = CHUNKS * GRIDS * FACES // GROUP
 
-FLIP_BANKS = 2
-PRODUCT_BANKS = 5
+FLIP_BANKS = 3
+PRODUCT_BANKS = 4
 
 LAG_QUANTISE_E = 2
-LAG_LAYER1 = 4
-LAG_GELU = 5
-LAG_FLIP_X = 7
-LAG_QUANTISE_X = 8
-LAG_LAYER2 = 16
-LAG_WEIGH = 17
-LAG_SUM = 26
+LAG_LAYER1 = 5
+LAG_GELU = 6
+LAG_FLIP_X = 9
+LAG_QUANTISE_X = 10
+LAG_LAYER2 = 18
+LAG_WEIGH = 19
+LAG_SUM = 28
 QUARTERS = 2 * (GRIDS - 1) + LAG_SUM + 1
 
 FLOPS = 2 * GRIDS * FACES * HID * (HID + LATENT)
@@ -187,10 +187,10 @@ def tile_fluxgnn1dlatent_pb_t_kernel(
             if 0 <= b < GRIDS:
                 x_bank[b] = flip(x_bf[b])
 
-        def copy_x(b):
-            if 0 <= b < GRIDS:
+        def copy_x(b, copy, parity):
+            if 0 <= b < GRIDS and b % 2 == parity:
                 x_grouped[b] = work.tile([P, FACES, PACK], BF16, tag="x_grouped", name="x_grouped", align_bytes=64)
-                nc.vector.tensor_copy(out=x_grouped[b][:].bitcast(F32), in_=x_bank[b])
+                copy(out=x_grouped[b][:].bitcast(F32), in_=x_bank[b])
 
         def quantise_x(b):
             if 0 <= b < GRIDS:
@@ -274,11 +274,12 @@ def tile_fluxgnn1dlatent_pb_t_kernel(
             tanh_of(2 * (q - LAG_LAYER2))
             tanh_of(2 * (q - LAG_LAYER2) + 1)
             copy_edge_hid(grid_of(0))
+            copy_x(grid_of(LAG_FLIP_X), nc.scalar.copy, 0)
 
             add_bias(q - LAG_LAYER1)
             weigh(2 * (q - LAG_WEIGH))
             weigh(2 * (q - LAG_WEIGH) + 1)
-            copy_x(grid_of(LAG_FLIP_X))
+            copy_x(grid_of(LAG_FLIP_X), nc.vector.tensor_copy, 1)
             quantise_edge_hid(grid_of(LAG_QUANTISE_E))
             quantise_x(grid_of(LAG_QUANTISE_X))
 

@@ -20,25 +20,38 @@ CELLS = 255
 HID = 512
 LATENT = 1024
 PACK = 4
-TILES = GRIDS * FACES // P
 GROUP = 2 * FACES
-PAIR = 2 * GROUP
-GRIDS_IN_PAIR = PAIR // FACES
+GROUPS = GRIDS // 2
 CHUNKS = LATENT // P
-JOBS = CHUNKS * GRIDS * FACES // GROUP
 
-FLIP_BANKS = 3
-PRODUCT_BANKS = 4
+FLIP_BANKS = 2
+PRODUCT_BANKS = 5
 
-LAG_QUANTISE_E = 2
-LAG_LAYER1 = 5
-LAG_GELU = 6
-LAG_FLIP_X = 9
-LAG_QUANTISE_X = 10
-LAG_LAYER2 = 18
-LAG_WEIGH = 19
-LAG_SUM = 28
-QUARTERS = 2 * (GRIDS - 1) + LAG_SUM + 1
+FLIP_1 = 1
+COPY_0 = 1
+COPY_1 = 2
+QE_0 = 2
+QE_1 = 3
+LAG_LAYER1 = 4
+LAG_GELU = 4
+INT_0 = 8
+INT_1 = 9
+QX_0 = 9
+QX_1 = 10
+LAG_LAYER2 = 12
+LAG_TANH = 12
+LAG_WEIGH = 13
+LAG_SUM_DIRECT = 14
+LAG_SUM = 19
+S_FIRST = 2
+VORD = 0
+SORD = 0
+TORD = 1
+S_MOD = 99
+TANH_BUFS = 10
+WBUFS = 3
+LAST_DIRECT = 2
+XTRA = 1
 
 FLOPS = 2 * GRIDS * FACES * HID * (HID + LATENT)
 
@@ -56,6 +69,8 @@ def tile_fluxgnn1dlatent_pb_t_kernel(
         psum = ctx.enter_context(tc.psum_pool(name="psum", bufs=1))
 
         e_in = [keep.tile([P, 2, HID], BF16, name="e_in%d" % b) for b in range(GRIDS)]
+        w2_raw_words = keep.tile([P, HID], U32, name="w2_raw_words", align_bytes=64)
+        w2_raw_plane = keep.tile([P, HID], U8, name="w2_raw_plane", align_bytes=64)
         w2_words = keep.tile([P, HID], U32, name="w2_words", align_bytes=64)
         w2_plane = keep.tile([P, HID], U8, name="w2_plane", align_bytes=64)
         w3_words = keep.tile([P, LATENT], U32, name="w3_words", align_bytes=64)
@@ -64,26 +79,20 @@ def tile_fluxgnn1dlatent_pb_t_kernel(
         rows = keep.tile([P, P], F32, name="rows")
         cols = keep.tile([P, P], F32, name="cols")
         ident = keep.tile([P, P], F32, name="ident")
-        ones = keep.tile([P, P], BF16, name="ones")
         pick = keep.tile([P, 2 * P], F32, name="pick")
-        b2_row = keep.tile([P, HID], BF16, name="b2_row")
-        b2_all = keep.tile([P, HID], F32, name="b2_all")
-        u_bf = keep.tile([GRIDS, CELLS], BF16, name="u_bf")
+        pick_enc = keep.tile([P, CHUNKS * 2 * P], F32, name="pick_enc")
+        b2_bf = keep.tile([P, PACK], BF16, name="b2_bf")
+        b2_cols = keep.tile([P, PACK], F32, name="b2_cols")
+        u_bf = keep.tile([GROUPS, 2, CELLS], BF16, name="u_bf")
         warm = keep.tile([P, 1], F32, name="warm")
         warm_out = keep.tile([P, 1], F32, name="warm_out")
-        last_bank = psum.tile([P, 2 * FACES], F32, tag="last_bank", bufs=1)
-        sums = last_bank[:, 0:FACES]
-        enc_sq_all = last_bank[:, FACES : FACES + P]
+        sums = psum.tile([P, GROUP], F32, tag="sums", bufs=1)
 
-        nc.vector.memset(rows_bf[:], 0.0)
-        nc.vector.memset(b2_row[:], 0.0)
-        nc.vector.memset(w2_plane[:].bitcast(I32), 0)
+        nc.vector.memset(w2_raw_plane[:].bitcast(I32), 0)
         nc.vector.memset(warm[:], 0.0)
-        nc.vector.memset(ones[:], 1.0)
+        nc.vector.memset(rows_bf[:], 0.0)
         nc.vector.memset(w3_plane[:].bitcast(I32), 0)
         make_identity(nc, ident[:])
-        nc.gpsimd.memset(pick[:], 0.0)
-        nc.gpsimd.memset(pick[:, P : P + 1], 1.0)
 
         def load_grid(b):
             nc.sync.dma_start(
@@ -102,204 +111,253 @@ def tile_fluxgnn1dlatent_pb_t_kernel(
                     in_=scales[0, 4 * quad : 4 * quad + 4, :].bitcast(I32),
                 )
 
-        nc.scalar.dma_start(out=b2_row[0:1, :], in_=b2.unsqueeze(0))
+        nc.scalar.dma_start(out=b2_bf[:], in_=b2.rearrange("(p t) -> p t", t=PACK))
         nc.scalar.dma_start(out=rows_bf[0:CHUNKS, :], in_=enc.rearrange("(j p) -> j p", p=P))
         nc.scalar.dma_start(
             out=rows_bf[CHUNKS : 2 * CHUNKS, :], in_=b3.rearrange("(j p) -> j p", p=P)
         )
-        nc.scalar.dma_start(out=u_bf[:], in_=u)
+        nc.scalar.dma_start(out=u_bf[:], in_=u.rearrange("(g h) i -> g h i", h=2))
         load_grid(0)
-        load_weight(w2_words, w2_plane, W2_words, W2_scales)
-        for b in range(1, GRIDS_IN_PAIR):
-            load_grid(b)
+        load_weight(w2_raw_words, w2_raw_plane, W2_words, W2_scales)
+        load_grid(1)
+        load_grid(2)
+        load_grid(3)
         load_weight(w3_words, w3_plane, W3_words, W3_scales)
-        for b in range(GRIDS_IN_PAIR, GRIDS):
+        for b in range(4, GRIDS):
             load_grid(b)
 
         nc.scalar.activation(out=warm_out[:], in_=warm[:], func=ACT.Gelu)
 
-        b2_ps = psum.tile([P, HID], F32, tag="product", bufs=PRODUCT_BANKS)
-        nc.tensor.matmul(out=b2_ps[:], lhsT=ones[:], rhs=b2_row[:], start=True, stop=True)
-        nc.scalar.copy(out=b2_all[:], in_=b2_ps[:])
+        nc.gpsimd.tensor_copy(
+            out=w2_plane[:].rearrange("p (t m) -> p m t", t=PACK),
+            in_=w2_raw_plane[:].rearrange("p (m t) -> p m t", t=PACK),
+        )
+        nc.vector.tensor_copy(
+            out=w2_words[:].bitcast(I32).rearrange("p (t m) -> p t m", t=PACK),
+            in_=w2_raw_words[:].bitcast(I32).rearrange("p (m t) -> p t m", t=PACK),
+        )
+        nc.vector.tensor_copy(out=b2_cols[:], in_=b2_bf[:])
         nc.vector.tensor_copy(out=rows[:], in_=rows_bf[:])
+        nc.gpsimd.memset(pick[:], 0.0)
+        nc.gpsimd.memset(pick[:, P : P + 1], 1.0)
+        nc.gpsimd.memset(pick_enc[:], 0.0)
 
         e_bank, e_grouped, e_codes, e_plane = {}, {}, {}, {}
-        x_bank, x_grouped, x_codes, x_plane = {}, {}, {}, {}
-        product1, pre_act, x_bf = {}, {}, {}
+        product1, x_raw = {}, {}
+        x_grouped, x_codes, x_plane = {}, {}, {}
         product2, tanh, weighted = {}, {}, {}
-
-        def flip(src):
-            bank = psum.tile([P, 2, FACES], F32, tag="flip", bufs=FLIP_BANKS)
-            words = src[:].bitcast(F32)
-            for n in range(2):
-                for w in range(2):
-                    nc.tensor.transpose(
-                        bank[:, w, n * P : (n + 1) * P], words[:, n, w : HID // 2 : 2], ident[:]
-                    )
-            return bank[:].rearrange("p w r -> p r w")
 
         def flip_edge_hid(b):
             if 0 <= b < GRIDS:
-                e_bank[b] = flip(e_in[b])
+                e_bank[b] = psum.tile([P, 2, FACES], F32, tag="flip", name="e_bank", bufs=FLIP_BANKS)
+                words = e_in[b][:].bitcast(F32)
+                for n in range(2):
+                    for w in range(2):
+                        nc.tensor.transpose(
+                            e_bank[b][:, w, n * P : (n + 1) * P], words[:, n, w : HID // 2 : 2], ident[:]
+                        )
 
-        def copy_edge_hid(b):
+        def copy_edge_hid(b, copy):
             if 0 <= b < GRIDS:
                 e_grouped[b] = work.tile([P, FACES, PACK], BF16, tag="e_grouped", name="e_grouped", align_bytes=64)
-                nc.scalar.copy(out=e_grouped[b][:].bitcast(F32), in_=e_bank[b])
+                copy(
+                    out=e_grouped[b][:].bitcast(F32), in_=e_bank[b][:].rearrange("p w r -> p r w")
+                )
 
         def quantise_edge_hid(b):
             if 0 <= b < GRIDS:
-                e_codes[b] = work.tile([P, FACES], U32, tag="e_codes", name="e_codes", bufs=3, align_bytes=64)
-                e_plane[b] = work.tile([P, FACES], U8, tag="e_plane", name="e_plane", bufs=3, align_bytes=64)
+                g, h = divmod(b, 2)
+                if h == 0:
+                    e_codes[g] = work.tile([P, GROUP], U32, tag="e_codes", name="e_codes", bufs=3, align_bytes=64)
+                    e_plane[g] = work.tile([P, GROUP], U8, tag="e_plane", name="e_plane", bufs=3, align_bytes=64)
                 nc.vector.quantize_mx(
-                    out=e_codes[b][:].bitcast(FP8X4),
-                    scales=e_plane[b][:],
+                    out=e_codes[g][:, h * FACES : (h + 1) * FACES].bitcast(FP8X4),
+                    scales=e_plane[g][:, h * FACES : (h + 1) * FACES],
                     in_=e_grouped[b][:].rearrange("p r t -> p (r t)"),
                 )
 
-        def layer1_product(t):
-            if 0 <= t < TILES:
-                b, n = divmod(t, 2)
-                product1[t] = psum.tile([P, HID], F32, tag="product", name="product1", bufs=PRODUCT_BANKS)
+        def layer1_product(k):
+            g, t = divmod(k, PACK)
+            if 0 <= g < GROUPS:
+                product1[k] = psum.tile([P, GROUP], F32, tag="product", name="product1", bufs=PRODUCT_BANKS)
                 nc.tensor.matmul_mx(
-                    out=product1[t][:],
-                    lhsT=e_codes[b][:, n * P : (n + 1) * P].bitcast(FP8X4),
-                    lhsT_scale=e_plane[b][:, n * P : (n + 1) * P],
-                    rhs=w2_words[:].bitcast(FP8X4),
-                    rhs_scale=w2_plane[:],
+                    out=product1[k][:],
+                    lhsT=w2_words[:, t * P : (t + 1) * P].bitcast(FP8X4),
+                    lhsT_scale=w2_plane[:, t * P : (t + 1) * P],
+                    rhs=e_codes[g][:].bitcast(FP8X4),
+                    rhs_scale=e_plane[g][:],
                     start=True,
                     stop=True,
                 )
 
-        def add_bias(t):
-            if 0 <= t < TILES:
-                pre_act[t] = work.tile([P, HID], F32, tag="pre_act", name="pre_act", bufs=3)
-                nc.vector.tensor_tensor(out=pre_act[t][:], in0=product1[t][:], in1=b2_all[:], op=ALU.add)
+        def gelu(k):
+            g, t = divmod(k, PACK)
+            if 0 <= g < GROUPS:
+                if t == 0:
+                    x_raw[g] = work.tile([P, PACK, GROUP], BF16, tag="x_raw", name="x_raw", bufs=3)
+                nc.scalar.activation(
+                    out=x_raw[g][:, t, :], in_=product1[k][:], func=ACT.Gelu, bias=b2_cols[:, t : t + 1]
+                )
 
-        def gelu(t):
-            if 0 <= t < TILES:
-                b, n = divmod(t, 2)
-                if n == 0:
-                    x_bf[b] = work.tile([P, 2, HID], BF16, tag="x_bf", name="x_bf", bufs=3)
-                nc.scalar.activation(out=x_bf[b][:, n, :], in_=pre_act[t][:], func=ACT.Gelu)
-
-        def flip_x(b):
+        def interleave(b):
             if 0 <= b < GRIDS:
-                x_bank[b] = flip(x_bf[b])
-
-        def copy_x(b, copy, parity):
-            if 0 <= b < GRIDS and b % 2 == parity:
-                x_grouped[b] = work.tile([P, FACES, PACK], BF16, tag="x_grouped", name="x_grouped", align_bytes=64)
-                copy(out=x_grouped[b][:].bitcast(F32), in_=x_bank[b])
+                g, h = divmod(b, 2)
+                x_grouped[b] = work.tile([P, FACES, PACK], BF16, tag="x_grouped", name="x_grouped", bufs=3, align_bytes=64)
+                nc.vector.tensor_copy(
+                    out=x_grouped[b][:],
+                    in_=x_raw[g][:, :, h * FACES : (h + 1) * FACES].rearrange("p t r -> p r t"),
+                )
 
         def quantise_x(b):
             if 0 <= b < GRIDS:
-                pair, place = divmod(b, GRIDS_IN_PAIR)
-                if place == 0:
-                    x_codes[pair] = work.tile([P, PAIR], U32, tag="x_codes", name="x_codes", align_bytes=64)
-                    x_plane[pair] = work.tile([P, PAIR], U8, tag="x_plane", name="x_plane", align_bytes=64)
+                g, h = divmod(b, 2)
+                if h == 0:
+                    x_codes[g] = work.tile([P, GROUP], U32, tag="x_codes", name="x_codes", bufs=3, align_bytes=64)
+                    x_plane[g] = work.tile([P, GROUP], U8, tag="x_plane", name="x_plane", bufs=3, align_bytes=64)
                 nc.vector.quantize_mx(
-                    out=x_codes[pair][:, place * FACES : (place + 1) * FACES].bitcast(FP8X4),
-                    scales=x_plane[pair][:, place * FACES : (place + 1) * FACES],
+                    out=x_codes[g][:, h * FACES : (h + 1) * FACES].bitcast(FP8X4),
+                    scales=x_plane[g][:, h * FACES : (h + 1) * FACES],
                     in_=x_grouped[b][:].rearrange("p r t -> p (r t)"),
                 )
 
-        def job(k):
-            pair, rest = divmod(k, 2 * CHUNKS)
-            j, member = divmod(rest, 2)
-            return pair, j, slice(member * GROUP, (member + 1) * GROUP)
-
         def layer2_product(k):
-            if 0 <= k < JOBS:
-                pair, j, group = job(k)
+            g, j = divmod(k, CHUNKS)
+            if 0 <= g < GROUPS:
                 product2[k] = psum.tile([P, GROUP], F32, tag="product", name="product2", bufs=PRODUCT_BANKS)
                 nc.tensor.matmul_mx(
                     out=product2[k][:],
                     lhsT=w3_words[:, j * P : (j + 1) * P].bitcast(FP8X4),
                     lhsT_scale=w3_plane[:, j * P : (j + 1) * P],
-                    rhs=x_codes[pair][:, group].bitcast(FP8X4),
-                    rhs_scale=x_plane[pair][:, group],
+                    rhs=x_codes[g][:].bitcast(FP8X4),
+                    rhs_scale=x_plane[g][:],
                     start=True,
                     stop=True,
                 )
 
         def tanh_of(k):
-            if 0 <= k < JOBS:
-                pair, j, group = job(k)
-                tanh[k] = work.tile([P, GROUP], F32, tag="tanh", name="tanh", bufs=5)
+            g, j = divmod(k, CHUNKS)
+            if 0 <= g < GROUPS:
+                tanh[k] = work.tile([P, GROUP], F32, tag="tanh", name="tanh", bufs=TANH_BUFS)
                 nc.scalar.activation(out=tanh[k][:], in_=product2[k][:], func=ACT.Tanh, bias=b3_cols[:, j : j + 1])
 
+        def direct(k):
+            g, j = divmod(k, CHUNKS)
+            if g == GROUPS - 1:
+                return j % 2 == 1 and j < 2 * LAST_DIRECT
+            return j == 0 or (j == 4 and g % 4 < XTRA)
+
         def weigh(k):
-            if 0 <= k < JOBS:
-                pair, j, group = job(k)
-                if k % (2 * CHUNKS) == 0:
-                    weighted[pair] = work.tile([P, PAIR], F32, tag="weighted", name="weighted")
-                if j == 0:
+            g, j = divmod(k, CHUNKS)
+            if 0 <= g < GROUPS and not direct(k):
+                if g not in weighted:
+                    weighted[g] = work.tile([P, GROUP], F32, tag="weighted", name="weighted", bufs=WBUFS)
                     nc.vector.tensor_scalar(
-                        out=weighted[pair][:, group], in0=tanh[k][:], scalar1=enc_cols[:, 0:1], scalar2=None, op0=ALU.mult
+                        out=weighted[g][:], in0=tanh[k][:], scalar1=enc_cols[:, j : j + 1], scalar2=None, op0=ALU.mult
                     )
                 else:
-                    nc.vector.scalar_tensor_tensor(
-                        out=weighted[pair][:, group],
-                        in0=tanh[k][:],
-                        scalar=enc_cols[:, j : j + 1],
-                        in1=weighted[pair][:, group],
-                        op0=ALU.mult,
-                        op1=ALU.add,
-                    )
+                    halves = 2 if k == GROUPS * CHUNKS - 1 else 1
+                    for h in range(halves):
+                        c = slice(h * GROUP // halves, (h + 1) * GROUP // halves)
+                        nc.vector.scalar_tensor_tensor(
+                            out=weighted[g][:, c],
+                            in0=tanh[k][:, c],
+                            scalar=enc_cols[:, j : j + 1],
+                            in1=weighted[g][:, c],
+                            op0=ALU.mult,
+                            op1=ALU.add,
+                        )
 
-        def sum_over_partitions(b):
-            if 0 <= b < GRIDS:
-                pair, place = divmod(b, GRIDS_IN_PAIR)
+        def sum_direct(k):
+            g, j = divmod(k, CHUNKS)
+            if 0 <= g < GROUPS and direct(k):
                 nc.tensor.matmul(
-                    out=sums,
-                    lhsT=pick[:, P - b : 2 * P - b],
-                    rhs=weighted[pair][:, place * FACES : (place + 1) * FACES],
-                    start=(b == 0),
-                    stop=(b == GRIDS - 1),
+                    out=sums[:],
+                    lhsT=pick_enc[:, j * 2 * P + P - g : j * 2 * P + 2 * P - g],
+                    rhs=tanh[k][:],
+                    start=(k == 0),
+                    stop=False,
                 )
 
-        def quarter(q):
-            def grid_of(lag):
-                return (q - lag) // 2 if (q - lag) % 2 == 0 else -1
+        def sum_weighted(g):
+            if 0 <= g < GROUPS:
+                halves = 2 if g == GROUPS - 1 else 1
+                for h in range(halves):
+                    c = slice(h * GROUP // halves, (h + 1) * GROUP // halves)
+                    nc.tensor.matmul(
+                        out=sums[:, c],
+                        lhsT=pick[:, P - g : 2 * P - g],
+                        rhs=weighted[g][:, c],
+                        start=False,
+                        stop=(g == GROUPS - 1 and h == halves - 1),
+                    )
 
+        def on_scalar(b):
+            return (0 <= b < S_FIRST and b % 2 == 0) or (b >= S_FIRST and b % S_MOD == 0)
+
+        def quarter(q):
+            def group_of(lag):
+                return (q - lag) // 4 if (q - lag) % 4 == 0 else -99
+
+            def grids(lag0, lag1):
+                return [2 * group_of(lag0), 2 * group_of(lag1) + 1]
+
+            if TORD == 1:
+                for b in grids(0, FLIP_1):
+                    flip_edge_hid(b)
             layer1_product(q - LAG_LAYER1)
             layer2_product(2 * (q - LAG_LAYER2))
             layer2_product(2 * (q - LAG_LAYER2) + 1)
-            flip_edge_hid(grid_of(0))
-            flip_x(grid_of(LAG_FLIP_X))
-            sum_over_partitions(grid_of(LAG_SUM))
+            if TORD == 0:
+                for b in grids(0, FLIP_1):
+                    flip_edge_hid(b)
+            sum_direct(2 * (q - LAG_SUM_DIRECT))
+            sum_direct(2 * (q - LAG_SUM_DIRECT) + 1)
+            sum_weighted(group_of(LAG_SUM))
 
-            gelu(q - LAG_GELU)
-            tanh_of(2 * (q - LAG_LAYER2))
-            tanh_of(2 * (q - LAG_LAYER2) + 1)
-            copy_edge_hid(grid_of(0))
-            copy_x(grid_of(LAG_FLIP_X), nc.scalar.copy, 0)
+            if SORD == 0: gelu(q - LAG_GELU)
+            tanh_of(2 * (q - LAG_TANH))
+            if SORD == 1: gelu(q - LAG_GELU)
+            tanh_of(2 * (q - LAG_TANH) + 1)
+            if SORD == 2: gelu(q - LAG_GELU)
+            for b in grids(COPY_0, COPY_1):
+                if on_scalar(b):
+                    copy_edge_hid(b, nc.scalar.copy)
 
-            add_bias(q - LAG_LAYER1)
-            weigh(2 * (q - LAG_WEIGH))
+            if VORD == 1:
+                weigh(2 * (q - LAG_WEIGH))
+            for b in grids(COPY_0, COPY_1):
+                if not on_scalar(b):
+                    copy_edge_hid(b, nc.vector.tensor_copy)
+            for b in grids(INT_0, INT_1):
+                interleave(b)
+            if VORD == 0:
+                weigh(2 * (q - LAG_WEIGH))
+            for b in grids(QE_0, QE_1):
+                quantise_edge_hid(b)
+            for b in grids(QX_0, QX_1):
+                quantise_x(b)
             weigh(2 * (q - LAG_WEIGH) + 1)
-            copy_x(grid_of(LAG_FLIP_X), nc.vector.tensor_copy, 1)
-            quantise_edge_hid(grid_of(LAG_QUANTISE_E))
-            quantise_x(grid_of(LAG_QUANTISE_X))
 
         quarter(0)
 
-        cols_ps = psum.tile([P, P], F32, tag="flip", bufs=FLIP_BANKS)
+        cols_ps = psum.tile([P, P], F32, tag="product", name="cols_ps", bufs=PRODUCT_BANKS)
         nc.tensor.transpose(cols_ps[:], rows[:], ident[:])
+        quarter(1)
         nc.vector.tensor_copy(out=cols[:], in_=cols_ps[:])
         enc_cols = cols[:, 0:CHUNKS]
         b3_cols = cols[:, CHUNKS : 2 * CHUNKS]
+        for j in (0, 1, 3, 4, 5):
+            nc.gpsimd.tensor_copy(out=pick_enc[:, j * 2 * P + P : j * 2 * P + P + 1], in_=enc_cols[:, j : j + 1])
+        for q in range(2, 17):
+            quarter(q)
+
         enc_sq = keep.tile([P, CHUNKS], F32, name="enc_sq")
         enc_sq_sum = keep.tile([P, 1], F32, name="enc_sq_sum")
         nc.vector.tensor_tensor(out=enc_sq[:], in0=enc_cols, in1=enc_cols, op=ALU.mult)
         nc.vector.tensor_reduce(out=enc_sq_sum[:], in_=enc_sq[:], axis=ALONG_FREE, op=ALU.add)
-
-        quarter(1)
-        quarter(2)
-
+        enc_sq_all = psum.tile([P, P], F32, tag="product", name="enc_sq_all", bufs=PRODUCT_BANKS)
         nc.tensor.matmul(
-            out=enc_sq_all, lhsT=enc_sq_sum[:, 0:1].to_broadcast([P, P]), rhs=ident[:], start=True, stop=True
+            out=enc_sq_all[:], lhsT=enc_sq_sum[:, 0:1].to_broadcast([P, P]), rhs=ident[:], start=True, stop=True
         )
         norm = keep.tile([P, 1], F32, name="norm")
         norm_eps = keep.tile([P, 1], F32, name="norm_eps")
@@ -307,36 +365,41 @@ def tile_fluxgnn1dlatent_pb_t_kernel(
         gain = keep.tile([P, 1], F32, name="gain")
         right_scale = keep.tile([P, 1], F32, name="right_scale")
         left_scale = keep.tile([P, 1], F32, name="left_scale")
-        u_gain = keep.tile([GRIDS, CELLS], F32, name="u_gain")
-        nc.vector.tensor_reduce(out=norm[:], in_=enc_sq_all, axis=ALONG_FREE, op=ALU.add)
-        nc.vector.tensor_scalar_add(out=norm_eps[:], in0=norm[:], scalar1=1e-12)
+        u_gain = keep.tile([GROUPS, 2, CELLS], F32, name="u_gain")
+        nc.vector.tensor_reduce(out=norm[:], in_=enc_sq_all[:], axis=ALONG_FREE, op=ALU.add)
+        nc.gpsimd.tensor_scalar(
+            out=norm_eps[:], in0=norm[:], scalar1=1e-12, scalar2=None, op0=ALU.add
+        )
+        quarter(17)
         nc.vector.reciprocal(out=inv_norm[:], in_=norm_eps[:])
-        nc.vector.tensor_tensor(out=gain[:], in0=norm[:], in1=inv_norm[:], op=ALU.mult)
-        nc.vector.tensor_scalar_mul(out=right_scale[:], in0=inv_norm[:], scalar1=-0.125)
-        nc.vector.tensor_scalar_mul(out=left_scale[:], in0=inv_norm[:], scalar1=0.125)
-        nc.vector.tensor_scalar(
-            out=u_gain[:], in0=u_bf[:], scalar1=gain[0:GRIDS, 0:1], scalar2=None, op0=ALU.mult
+        nc.gpsimd.tensor_tensor(out=gain[:], in0=norm[:], in1=inv_norm[:], op=ALU.mult)
+        nc.gpsimd.tensor_scalar(out=right_scale[:], in0=inv_norm[:], scalar1=-0.125, scalar2=None, op0=ALU.mult)
+        nc.gpsimd.tensor_scalar(out=left_scale[:], in0=inv_norm[:], scalar1=0.125, scalar2=None, op0=ALU.mult)
+        nc.gpsimd.tensor_scalar(
+            out=u_gain[:], in0=u_bf[:], scalar1=gain[0:GROUPS, 0:1], scalar2=None, op0=ALU.mult
         )
 
-        for q in range(3, QUARTERS):
+        for q in range(18, 4 * (GROUPS - 1) + LAG_SUM + 1):
             quarter(q)
 
-        left = keep.tile([GRIDS, CELLS], F32, name="left")
-        result = keep.tile([GRIDS, CELLS], F32, name="result")
-        nc.vector.scalar_tensor_tensor(
-            out=left[:],
-            in0=last_bank[0:GRIDS, 0:CELLS],
-            scalar=left_scale[0:GRIDS, 0:1],
-            in1=u_gain[:],
-            op0=ALU.mult,
-            op1=ALU.add,
-        )
-        nc.vector.scalar_tensor_tensor(
-            out=result[:],
-            in0=last_bank[0:GRIDS, 1 : CELLS + 1],
-            scalar=right_scale[0:GRIDS, 0:1],
-            in1=left[:],
-            op0=ALU.mult,
-            op1=ALU.add,
-        )
-        nc.sync.dma_start(out=out, in_=result[:])
+        left = keep.tile([GROUPS, 2, CELLS], F32, name="left")
+        result = keep.tile([GROUPS, 2, CELLS], F32, name="result")
+        for h in range(2):
+            grid_sums = sums[0:GROUPS, h * FACES : (h + 1) * FACES]
+            nc.vector.scalar_tensor_tensor(
+                out=left[:, h, :],
+                in0=grid_sums[:, 0:CELLS],
+                scalar=left_scale[0:GROUPS, 0:1],
+                in1=u_gain[:, h, :],
+                op0=ALU.mult,
+                op1=ALU.add,
+            )
+            nc.vector.scalar_tensor_tensor(
+                out=result[:, h, :],
+                in0=grid_sums[:, 1 : CELLS + 1],
+                scalar=right_scale[0:GROUPS, 0:1],
+                in1=left[:, h, :],
+                op0=ALU.mult,
+                op1=ALU.add,
+            )
+        nc.sync.dma_start(out=out.rearrange("(g h) i -> g h i", h=2), in_=result[:])

@@ -27,7 +27,7 @@ CHUNKS = LATENT // P
 FLIP_BANKS = 2
 PRODUCT_BANKS = 5
 
-FLIP_1 = 1
+FLIP_1 = 0
 COPY_0 = 1
 COPY_1 = 2
 QE_0 = 2
@@ -47,8 +47,12 @@ S_FIRST = 2
 VORD = 0
 SORD = 0
 TORD = 1
-S_MOD = 99
+S_MOD = 4
+S_REM = 1
+S_FROM = 4
+CPOS = 0
 TANH_BUFS = 10
+DIRECT_CHUNKS = [0, 4, 1, 3]
 WBUFS = 3
 LAST_DIRECT = 2
 XTRA = 1
@@ -80,7 +84,7 @@ def tile_fluxgnn1dlatent_pb_t_kernel(
         cols = keep.tile([P, P], F32, name="cols")
         ident = keep.tile([P, P], F32, name="ident")
         pick = keep.tile([P, 2 * P], F32, name="pick")
-        pick_enc = keep.tile([P, CHUNKS * 2 * P], F32, name="pick_enc")
+        pick_enc = keep.tile([P, 5 * P], F32, name="pick_enc")
         b2_bf = keep.tile([P, PACK], BF16, name="b2_bf")
         b2_cols = keep.tile([P, PACK], F32, name="b2_cols")
         u_bf = keep.tile([GROUPS, 2, CELLS], BF16, name="u_bf")
@@ -93,6 +97,9 @@ def tile_fluxgnn1dlatent_pb_t_kernel(
         nc.vector.memset(rows_bf[:], 0.0)
         nc.vector.memset(w3_plane[:].bitcast(I32), 0)
         make_identity(nc, ident[:])
+        nc.vector.memset(pick[:], 0.0)
+        nc.vector.memset(pick[:, P : P + 1], 1.0)
+        nc.vector.memset(pick_enc[:], 0.0)
 
         def load_grid(b):
             nc.sync.dma_start(
@@ -128,19 +135,16 @@ def tile_fluxgnn1dlatent_pb_t_kernel(
 
         nc.scalar.activation(out=warm_out[:], in_=warm[:], func=ACT.Gelu)
 
-        nc.gpsimd.tensor_copy(
-            out=w2_plane[:].rearrange("p (t m) -> p m t", t=PACK),
-            in_=w2_raw_plane[:].rearrange("p (m t) -> p m t", t=PACK),
-        )
+        for t in range(PACK):
+            nc.vector.tensor_copy(
+                out=w2_plane[:, t * P : (t + 1) * P], in_=w2_raw_plane[:, t : HID : PACK]
+            )
         nc.vector.tensor_copy(
             out=w2_words[:].bitcast(I32).rearrange("p (t m) -> p t m", t=PACK),
             in_=w2_raw_words[:].bitcast(I32).rearrange("p (m t) -> p t m", t=PACK),
         )
         nc.vector.tensor_copy(out=b2_cols[:], in_=b2_bf[:])
         nc.vector.tensor_copy(out=rows[:], in_=rows_bf[:])
-        nc.gpsimd.memset(pick[:], 0.0)
-        nc.gpsimd.memset(pick[:, P : P + 1], 1.0)
-        nc.gpsimd.memset(pick_enc[:], 0.0)
 
         e_bank, e_grouped, e_codes, e_plane = {}, {}, {}, {}
         product1, x_raw = {}, {}
@@ -272,7 +276,7 @@ def tile_fluxgnn1dlatent_pb_t_kernel(
             if 0 <= g < GROUPS and direct(k):
                 nc.tensor.matmul(
                     out=sums[:],
-                    lhsT=pick_enc[:, j * 2 * P + P - g : j * 2 * P + 2 * P - g],
+                    lhsT=pick_enc[:, (DIRECT_CHUNKS.index(j) + 1) * P - g : (DIRECT_CHUNKS.index(j) + 2) * P - g],
                     rhs=tanh[k][:],
                     start=(k == 0),
                     stop=False,
@@ -292,7 +296,7 @@ def tile_fluxgnn1dlatent_pb_t_kernel(
                     )
 
         def on_scalar(b):
-            return (0 <= b < S_FIRST and b % 2 == 0) or (b >= S_FIRST and b % S_MOD == 0)
+            return 0 <= b < S_FIRST or (b >= S_FROM and b % S_MOD == S_REM)
 
         def quarter(q):
             def group_of(lag):
@@ -314,14 +318,19 @@ def tile_fluxgnn1dlatent_pb_t_kernel(
             sum_direct(2 * (q - LAG_SUM_DIRECT) + 1)
             sum_weighted(group_of(LAG_SUM))
 
+            if CPOS == 1:
+                for b in grids(COPY_0, COPY_1):
+                    if on_scalar(b):
+                        copy_edge_hid(b, nc.scalar.copy)
             if SORD == 0: gelu(q - LAG_GELU)
             tanh_of(2 * (q - LAG_TANH))
             if SORD == 1: gelu(q - LAG_GELU)
             tanh_of(2 * (q - LAG_TANH) + 1)
             if SORD == 2: gelu(q - LAG_GELU)
-            for b in grids(COPY_0, COPY_1):
-                if on_scalar(b):
-                    copy_edge_hid(b, nc.scalar.copy)
+            if CPOS == 0:
+                for b in grids(COPY_0, COPY_1):
+                    if on_scalar(b):
+                        copy_edge_hid(b, nc.scalar.copy)
 
             if VORD == 1:
                 weigh(2 * (q - LAG_WEIGH))
@@ -346,8 +355,8 @@ def tile_fluxgnn1dlatent_pb_t_kernel(
         nc.vector.tensor_copy(out=cols[:], in_=cols_ps[:])
         enc_cols = cols[:, 0:CHUNKS]
         b3_cols = cols[:, CHUNKS : 2 * CHUNKS]
-        for j in (0, 1, 3, 4, 5):
-            nc.gpsimd.tensor_copy(out=pick_enc[:, j * 2 * P + P : j * 2 * P + P + 1], in_=enc_cols[:, j : j + 1])
+        for n, j in enumerate(DIRECT_CHUNKS):
+            nc.vector.tensor_copy(out=pick_enc[:, (n + 1) * P : (n + 1) * P + 1], in_=enc_cols[:, j : j + 1])
         for q in range(2, 17):
             quarter(q)
 
@@ -367,21 +376,19 @@ def tile_fluxgnn1dlatent_pb_t_kernel(
         left_scale = keep.tile([P, 1], F32, name="left_scale")
         u_gain = keep.tile([GROUPS, 2, CELLS], F32, name="u_gain")
         nc.vector.tensor_reduce(out=norm[:], in_=enc_sq_all[:], axis=ALONG_FREE, op=ALU.add)
-        nc.gpsimd.tensor_scalar(
-            out=norm_eps[:], in0=norm[:], scalar1=1e-12, scalar2=None, op0=ALU.add
-        )
+        nc.vector.tensor_scalar_add(out=norm_eps[:], in0=norm[:], scalar1=1e-12)
         quarter(17)
         nc.vector.reciprocal(out=inv_norm[:], in_=norm_eps[:])
-        nc.gpsimd.tensor_tensor(out=gain[:], in0=norm[:], in1=inv_norm[:], op=ALU.mult)
-        nc.gpsimd.tensor_scalar(out=right_scale[:], in0=inv_norm[:], scalar1=-0.125, scalar2=None, op0=ALU.mult)
-        nc.gpsimd.tensor_scalar(out=left_scale[:], in0=inv_norm[:], scalar1=0.125, scalar2=None, op0=ALU.mult)
-        nc.gpsimd.tensor_scalar(
-            out=u_gain[:], in0=u_bf[:], scalar1=gain[0:GROUPS, 0:1], scalar2=None, op0=ALU.mult
-        )
+        nc.vector.tensor_tensor(out=gain[:], in0=norm[:], in1=inv_norm[:], op=ALU.mult)
+        nc.vector.tensor_scalar_mul(out=right_scale[:], in0=inv_norm[:], scalar1=-0.125)
+        nc.vector.tensor_scalar_mul(out=left_scale[:], in0=inv_norm[:], scalar1=0.125)
 
         for q in range(18, 4 * (GROUPS - 1) + LAG_SUM + 1):
             quarter(q)
 
+        nc.vector.tensor_scalar(
+            out=u_gain[:], in0=u_bf[:], scalar1=gain[0:GROUPS, 0:1], scalar2=None, op0=ALU.mult
+        )
         left = keep.tile([GROUPS, 2, CELLS], F32, name="left")
         result = keep.tile([GROUPS, 2, CELLS], F32, name="result")
         for h in range(2):

@@ -47,15 +47,18 @@ S_FIRST = 2
 VORD = 0
 SORD = 0
 TORD = 1
-S_MOD = 4
+S_MOD = 2
 S_REM = 1
 S_FROM = 4
 CPOS = 0
 TANH_BUFS = 10
-DIRECT_CHUNKS = [0, 4, 1, 3]
+DIRECT_CHUNKS = [0, 4, 1, 3, 5]
 WBUFS = 3
 LAST_DIRECT = 2
-XTRA = 1
+XTRA = 0
+BASE_DIRECT = 0
+X4 = []
+HALF_FROM = 0
 
 FLOPS = 2 * GRIDS * FACES * HID * (HID + LATENT)
 
@@ -84,7 +87,7 @@ def tile_fluxgnn1dlatent_pb_t_kernel(
         cols = keep.tile([P, P], F32, name="cols")
         ident = keep.tile([P, P], F32, name="ident")
         pick = keep.tile([P, 2 * P], F32, name="pick")
-        pick_enc = keep.tile([P, 5 * P], F32, name="pick_enc")
+        pick_enc = keep.tile([P, 6 * P], F32, name="pick_enc")
         b2_bf = keep.tile([P, PACK], BF16, name="b2_bf")
         b2_cols = keep.tile([P, PACK], F32, name="b2_cols")
         u_bf = keep.tile([GROUPS, 2, CELLS], BF16, name="u_bf")
@@ -248,7 +251,7 @@ def tile_fluxgnn1dlatent_pb_t_kernel(
             g, j = divmod(k, CHUNKS)
             if g == GROUPS - 1:
                 return j % 2 == 1 and j < 2 * LAST_DIRECT
-            return j == 0 or (j == 4 and g % 4 < XTRA)
+            return j < BASE_DIRECT or (j == 4 and (g % 4 < XTRA or g in X4))
 
         def weigh(k):
             g, j = divmod(k, CHUNKS)
@@ -259,7 +262,7 @@ def tile_fluxgnn1dlatent_pb_t_kernel(
                         out=weighted[g][:], in0=tanh[k][:], scalar1=enc_cols[:, j : j + 1], scalar2=None, op0=ALU.mult
                     )
                 else:
-                    halves = 2 if k == GROUPS * CHUNKS - 1 else 1
+                    halves = 2 if k == GROUPS * CHUNKS - 1 or g >= HALF_FROM else 1
                     for h in range(halves):
                         c = slice(h * GROUP // halves, (h + 1) * GROUP // halves)
                         nc.vector.scalar_tensor_tensor(
@@ -291,7 +294,7 @@ def tile_fluxgnn1dlatent_pb_t_kernel(
                         out=sums[:, c],
                         lhsT=pick[:, P - g : 2 * P - g],
                         rhs=weighted[g][:, c],
-                        start=False,
+                        start=(g == 0 and BASE_DIRECT == 0),
                         stop=(g == GROUPS - 1 and h == halves - 1),
                     )
 

@@ -211,8 +211,8 @@ def tile_fluxgnn1dlatent_pb_t_kernel(
                 g, h = divmod(b, 2)
                 x_grouped[b] = work.tile([P, FACES, PACK], BF16, tag="x_grouped", name="x_grouped", bufs=3, align_bytes=64)
                 nc.vector.tensor_copy(
-                    out=x_grouped[b][:],
-                    in_=x_raw[g][:, :, h * FACES : (h + 1) * FACES].rearrange("p t r -> p r t"),
+                    out=x_grouped[b][:].rearrange("p (c i) t -> p c t i", i=4),
+                    in_=x_raw[g][:, :, h * FACES : (h + 1) * FACES].rearrange("p t (c i) -> p c t i", i=4),
                 )
 
         def quantise_x(b):

@@ -27,34 +27,36 @@ CHUNKS = LATENT // P
 FLIP_BANKS = 2
 PRODUCT_BANKS = 5
 
-FLIP_1 = 0
-COPY_0 = 1
-COPY_1 = 2
-QE_0 = 2
-QE_1 = 3
-LAG_LAYER1 = 4
-LAG_GELU = 4
-INT_0 = 8
-INT_1 = 9
-QX_0 = 9
-QX_1 = 10
-LAG_LAYER2 = 12
-LAG_TANH = 12
-LAG_WEIGH = 13
-LAG_SUM_DIRECT = 14
-LAG_SUM = 19
+FLIP_1 = 1
+LAG_COPY = 1
+EG_BUFS = 2
+HALF_PH = []
+LAG_QE = 2
+LAG_LAYER1 = 6
+LAG_GELU = 6
+INT_0 = 10
+INT_1 = 12
+LAG_QX = 12
+LAG_LAYER2 = 15
+LAG_TANH = 15
+LAG_WEIGH = 16
+LAG_SUM_DIRECT = 17
+LAG_SUM = 22
+MAIN = 1
 S_FIRST = 2
+Q0 = 8
+HS2 = 0
 VORD = 0
 SORD = 0
-TORD = 1
+TORD = 0
 S_MOD = 2
 S_REM = 1
 S_FROM = 4
-CPOS = 0
-TANH_BUFS = 10
+CPOS = 1
+TANH_BUFS = 12
 DIRECT_CHUNKS = [0, 4, 1, 3, 5]
 WBUFS = 3
-LAST_DIRECT = 2
+LAST_DIRECT = 1
 XTRA = 0
 BASE_DIRECT = 0
 X4 = []
@@ -152,7 +154,7 @@ def tile_fluxgnn1dlatent_pb_t_kernel(
         e_bank, e_grouped, e_codes, e_plane = {}, {}, {}, {}
         product1, x_raw = {}, {}
         x_grouped, x_codes, x_plane = {}, {}, {}
-        product2, tanh, weighted = {}, {}, {}
+        product2, tanh, weighted, last_sums = {}, {}, {}, {}
 
         def flip_edge_hid(b):
             if 0 <= b < GRIDS:
@@ -166,65 +168,69 @@ def tile_fluxgnn1dlatent_pb_t_kernel(
 
         def copy_edge_hid(b, copy):
             if 0 <= b < GRIDS:
-                e_grouped[b] = work.tile([P, FACES, PACK], BF16, tag="e_grouped", name="e_grouped", align_bytes=64)
+                g, h = divmod(b, 2)
+                if g not in e_grouped:
+                    e_grouped[g] = work.tile([P, GROUP, PACK], BF16, tag="e_grouped", name="e_grouped", bufs=EG_BUFS, align_bytes=64)
                 copy(
-                    out=e_grouped[b][:].bitcast(F32), in_=e_bank[b][:].rearrange("p w r -> p r w")
+                    out=e_grouped[g][:, h * FACES : (h + 1) * FACES, :].rearrange("p r t -> p (r t)").bitcast(F32).rearrange("p (r w) -> p r w", w=2),
+                    in_=e_bank[b][:].rearrange("p w r -> p r w"),
                 )
 
-        def quantise_edge_hid(b):
-            if 0 <= b < GRIDS:
-                g, h = divmod(b, 2)
-                if h == 0:
+        def quantise_edge_hid(g, h=None):
+            if 0 <= g < GROUPS:
+                if h != 1:
                     e_codes[g] = work.tile([P, GROUP], U32, tag="e_codes", name="e_codes", bufs=3, align_bytes=64)
                     e_plane[g] = work.tile([P, GROUP], U8, tag="e_plane", name="e_plane", bufs=3, align_bytes=64)
+                c = slice(0, GROUP) if h is None else slice(h * FACES, (h + 1) * FACES)
                 nc.vector.quantize_mx(
-                    out=e_codes[g][:, h * FACES : (h + 1) * FACES].bitcast(FP8X4),
-                    scales=e_plane[g][:, h * FACES : (h + 1) * FACES],
-                    in_=e_grouped[b][:].rearrange("p r t -> p (r t)"),
+                    out=e_codes[g][:, c].bitcast(FP8X4),
+                    scales=e_plane[g][:, c],
+                    in_=e_grouped[g][:, c, :].rearrange("p r t -> p (r t)"),
                 )
 
-        def layer1_product(k):
+        def layer1_product(k, h=None):
             g, t = divmod(k, PACK)
             if 0 <= g < GROUPS:
-                product1[k] = psum.tile([P, GROUP], F32, tag="product", name="product1", bufs=PRODUCT_BANKS)
+                c = slice(0, GROUP) if h is None else slice(h * FACES, (h + 1) * FACES)
+                product1[k, h] = psum.tile([P, c.stop - c.start], F32, tag="product", name="product1", bufs=PRODUCT_BANKS)
                 nc.tensor.matmul_mx(
-                    out=product1[k][:],
+                    out=product1[k, h][:],
                     lhsT=w2_words[:, t * P : (t + 1) * P].bitcast(FP8X4),
                     lhsT_scale=w2_plane[:, t * P : (t + 1) * P],
-                    rhs=e_codes[g][:].bitcast(FP8X4),
-                    rhs_scale=e_plane[g][:],
+                    rhs=e_codes[g][:, c].bitcast(FP8X4),
+                    rhs_scale=e_plane[g][:, c],
                     start=True,
                     stop=True,
                 )
 
-        def gelu(k):
+        def gelu(k, h=None):
             g, t = divmod(k, PACK)
             if 0 <= g < GROUPS:
-                if t == 0:
+                if t == 0 and h != 1:
                     x_raw[g] = work.tile([P, PACK, GROUP], BF16, tag="x_raw", name="x_raw", bufs=3)
+                c = slice(0, GROUP) if h is None else slice(h * FACES, (h + 1) * FACES)
                 nc.scalar.activation(
-                    out=x_raw[g][:, t, :], in_=product1[k][:], func=ACT.Gelu, bias=b2_cols[:, t : t + 1]
+                    out=x_raw[g][:, t, c], in_=product1[k, h][:], func=ACT.Gelu, bias=b2_cols[:, t : t + 1]
                 )
 
         def interleave(b):
             if 0 <= b < GRIDS:
                 g, h = divmod(b, 2)
-                x_grouped[b] = work.tile([P, FACES, PACK], BF16, tag="x_grouped", name="x_grouped", bufs=3, align_bytes=64)
+                if h == 0:
+                    x_grouped[g] = work.tile([P, GROUP, PACK], BF16, tag="x_grouped", name="x_grouped", bufs=2, align_bytes=64)
                 nc.vector.tensor_copy(
-                    out=x_grouped[b][:].rearrange("p (c i) t -> p c t i", i=4),
+                    out=x_grouped[g][:, h * FACES : (h + 1) * FACES, :].rearrange("p (c i) t -> p c t i", i=4),
                     in_=x_raw[g][:, :, h * FACES : (h + 1) * FACES].rearrange("p t (c i) -> p c t i", i=4),
                 )
 
-        def quantise_x(b):
-            if 0 <= b < GRIDS:
-                g, h = divmod(b, 2)
-                if h == 0:
-                    x_codes[g] = work.tile([P, GROUP], U32, tag="x_codes", name="x_codes", bufs=3, align_bytes=64)
-                    x_plane[g] = work.tile([P, GROUP], U8, tag="x_plane", name="x_plane", bufs=3, align_bytes=64)
+        def quantise_x(g):
+            if 0 <= g < GROUPS:
+                x_codes[g] = work.tile([P, GROUP], U32, tag="x_codes", name="x_codes", bufs=3, align_bytes=64)
+                x_plane[g] = work.tile([P, GROUP], U8, tag="x_plane", name="x_plane", bufs=3, align_bytes=64)
                 nc.vector.quantize_mx(
-                    out=x_codes[g][:, h * FACES : (h + 1) * FACES].bitcast(FP8X4),
-                    scales=x_plane[g][:, h * FACES : (h + 1) * FACES],
-                    in_=x_grouped[b][:].rearrange("p r t -> p (r t)"),
+                    out=x_codes[g][:].bitcast(FP8X4),
+                    scales=x_plane[g][:],
+                    in_=x_grouped[g][:].rearrange("p r t -> p (r t)"),
                 )
 
         def layer2_product(k):
@@ -253,7 +259,7 @@ def tile_fluxgnn1dlatent_pb_t_kernel(
                 return j % 2 == 1 and j < 2 * LAST_DIRECT
             return j < BASE_DIRECT or (j == 4 and (g % 4 < XTRA or g in X4))
 
-        def weigh(k):
+        def weigh(k, halved):
             g, j = divmod(k, CHUNKS)
             if 0 <= g < GROUPS and not direct(k):
                 if g not in weighted:
@@ -262,7 +268,7 @@ def tile_fluxgnn1dlatent_pb_t_kernel(
                         out=weighted[g][:], in0=tanh[k][:], scalar1=enc_cols[:, j : j + 1], scalar2=None, op0=ALU.mult
                     )
                 else:
-                    halves = 2 if k == GROUPS * CHUNKS - 1 or g >= HALF_FROM else 1
+                    halves = 2 if k == GROUPS * CHUNKS - 1 or g >= HALF_FROM or halved else 1
                     for h in range(halves):
                         c = slice(h * GROUP // halves, (h + 1) * GROUP // halves)
                         nc.vector.scalar_tensor_tensor(
@@ -277,26 +283,49 @@ def tile_fluxgnn1dlatent_pb_t_kernel(
         def sum_direct(k):
             g, j = divmod(k, CHUNKS)
             if 0 <= g < GROUPS and direct(k):
-                nc.tensor.matmul(
-                    out=sums[:],
-                    lhsT=pick_enc[:, (DIRECT_CHUNKS.index(j) + 1) * P - g : (DIRECT_CHUNKS.index(j) + 2) * P - g],
-                    rhs=tanh[k][:],
-                    start=(k == 0),
-                    stop=False,
-                )
+                lhsT = pick_enc[:, (DIRECT_CHUNKS.index(j) + 1) * P - g : (DIRECT_CHUNKS.index(j) + 2) * P - g]
+                if g < GROUPS - 1:
+                    nc.tensor.matmul(out=sums[:], lhsT=lhsT, rhs=tanh[k][:], start=(k == 0), stop=False)
+                else:
+                    for h in range(2):
+                        fresh = h not in last_sums
+                        if fresh:
+                            last_sums[h] = psum.tile([P, FACES], F32, tag="flip", name="last_sums", bufs=FLIP_BANKS)
+                        nc.tensor.matmul(
+                            out=last_sums[h][:],
+                            lhsT=lhsT,
+                            rhs=tanh[k][:, h * FACES : (h + 1) * FACES],
+                            start=fresh,
+                            stop=False,
+                        )
 
         def sum_weighted(g):
             if 0 <= g < GROUPS:
-                halves = 2 if g == GROUPS - 1 else 1
-                for h in range(halves):
-                    c = slice(h * GROUP // halves, (h + 1) * GROUP // halves)
+                lhsT = pick[:, P - g : 2 * P - g]
+                if g < GROUPS - 1:
                     nc.tensor.matmul(
-                        out=sums[:, c],
-                        lhsT=pick[:, P - g : 2 * P - g],
-                        rhs=weighted[g][:, c],
+                        out=sums[:],
+                        lhsT=lhsT,
+                        rhs=weighted[g][:],
                         start=(g == 0 and BASE_DIRECT == 0),
-                        stop=(g == GROUPS - 1 and h == halves - 1),
+                        stop=(g == GROUPS - 2),
                     )
+                else:
+                    for h in range(2):
+                        fresh = h not in last_sums
+                        if fresh:
+                            last_sums[h] = psum.tile([P, FACES], F32, tag="flip", name="last_sums", bufs=FLIP_BANKS)
+                        nc.tensor.matmul(
+                            out=last_sums[h][:],
+                            lhsT=lhsT,
+                            rhs=weighted[g][:, h * FACES : (h + 1) * FACES],
+                            start=fresh,
+                            stop=True,
+                        )
+
+        def gelu_from_group_1(k):
+            if k >= PACK:
+                gelu(k)
 
         def on_scalar(b):
             return 0 <= b < S_FIRST or (b >= S_FROM and b % S_MOD == S_REM)
@@ -308,69 +337,75 @@ def tile_fluxgnn1dlatent_pb_t_kernel(
             def grids(lag0, lag1):
                 return [2 * group_of(lag0), 2 * group_of(lag1) + 1]
 
-            if TORD == 1:
-                for b in grids(0, FLIP_1):
+            if TORD == 1 and q > 0:
+                for b in grids(0, 0):
                     flip_edge_hid(b)
-            layer1_product(q - LAG_LAYER1)
+            if q - LAG_LAYER1 >= PACK:
+                layer1_product(q - LAG_LAYER1)
             layer2_product(2 * (q - LAG_LAYER2))
             layer2_product(2 * (q - LAG_LAYER2) + 1)
-            if TORD == 0:
-                for b in grids(0, FLIP_1):
+            if TORD == 0 and q > 0:
+                for b in grids(0, 0):
                     flip_edge_hid(b)
             sum_direct(2 * (q - LAG_SUM_DIRECT))
             sum_direct(2 * (q - LAG_SUM_DIRECT) + 1)
             sum_weighted(group_of(LAG_SUM))
 
-            if CPOS == 1:
-                for b in grids(COPY_0, COPY_1):
+            if CPOS == 1 and q != LAG_COPY:
+                for b in grids(LAG_COPY, LAG_COPY):
                     if on_scalar(b):
                         copy_edge_hid(b, nc.scalar.copy)
-            if SORD == 0: gelu(q - LAG_GELU)
+            if SORD == 0: gelu_from_group_1(q - LAG_GELU)
             tanh_of(2 * (q - LAG_TANH))
-            if SORD == 1: gelu(q - LAG_GELU)
+            if SORD == 1: gelu_from_group_1(q - LAG_GELU)
             tanh_of(2 * (q - LAG_TANH) + 1)
-            if SORD == 2: gelu(q - LAG_GELU)
-            if CPOS == 0:
-                for b in grids(COPY_0, COPY_1):
+            if SORD == 2: gelu_from_group_1(q - LAG_GELU)
+            if CPOS == 0 and q != LAG_COPY:
+                for b in grids(LAG_COPY, LAG_COPY):
                     if on_scalar(b):
                         copy_edge_hid(b, nc.scalar.copy)
 
             if VORD == 1:
-                weigh(2 * (q - LAG_WEIGH))
-            for b in grids(COPY_0, COPY_1):
+                weigh(2 * (q - LAG_WEIGH), q % 4 in HALF_PH)
+            for b in grids(LAG_COPY, LAG_COPY) if q != LAG_COPY else []:
                 if not on_scalar(b):
                     copy_edge_hid(b, nc.vector.tensor_copy)
             for b in grids(INT_0, INT_1):
                 interleave(b)
             if VORD == 0:
-                weigh(2 * (q - LAG_WEIGH))
-            for b in grids(QE_0, QE_1):
-                quantise_edge_hid(b)
-            for b in grids(QX_0, QX_1):
-                quantise_x(b)
-            weigh(2 * (q - LAG_WEIGH) + 1)
+                weigh(2 * (q - LAG_WEIGH), q % 4 in HALF_PH)
+            if q != LAG_QE:
+                quantise_edge_hid(group_of(LAG_QE))
+            quantise_x(group_of(LAG_QX))
+            weigh(2 * (q - LAG_WEIGH) + 1, q % 4 in HALF_PH)
 
-        quarter(0)
-
+        flip_edge_hid(0)
+        copy_edge_hid(0, nc.scalar.copy)
+        quantise_edge_hid(0, 0)
+        flip_edge_hid(1)
+        copy_edge_hid(1, nc.scalar.copy)
         cols_ps = psum.tile([P, P], F32, tag="product", name="cols_ps", bufs=PRODUCT_BANKS)
         nc.tensor.transpose(cols_ps[:], rows[:], ident[:])
-        quarter(1)
+        flip_edge_hid(2)
+        for t in range(PACK):
+            layer1_product(t, 0)
+            gelu(t, 0)
+        quantise_edge_hid(0, 1)
         nc.vector.tensor_copy(out=cols[:], in_=cols_ps[:])
+        flip_edge_hid(3)
+        for t in range(PACK):
+            layer1_product(t, 1)
+        copy_edge_hid(2, nc.scalar.copy if HS2 else nc.vector.tensor_copy)
+        for t in range(PACK):
+            gelu(t, 1)
+        copy_edge_hid(3, nc.vector.tensor_copy)
         enc_cols = cols[:, 0:CHUNKS]
         b3_cols = cols[:, CHUNKS : 2 * CHUNKS]
         for n, j in enumerate(DIRECT_CHUNKS):
             nc.vector.tensor_copy(out=pick_enc[:, (n + 1) * P : (n + 1) * P + 1], in_=enc_cols[:, j : j + 1])
-        for q in range(2, 17):
-            quarter(q)
-
+        quantise_edge_hid(1)
         enc_sq = keep.tile([P, CHUNKS], F32, name="enc_sq")
         enc_sq_sum = keep.tile([P, 1], F32, name="enc_sq_sum")
-        nc.vector.tensor_tensor(out=enc_sq[:], in0=enc_cols, in1=enc_cols, op=ALU.mult)
-        nc.vector.tensor_reduce(out=enc_sq_sum[:], in_=enc_sq[:], axis=ALONG_FREE, op=ALU.add)
-        enc_sq_all = psum.tile([P, P], F32, tag="product", name="enc_sq_all", bufs=PRODUCT_BANKS)
-        nc.tensor.matmul(
-            out=enc_sq_all[:], lhsT=enc_sq_sum[:, 0:1].to_broadcast([P, P]), rhs=ident[:], start=True, stop=True
-        )
         norm = keep.tile([P, 1], F32, name="norm")
         norm_eps = keep.tile([P, 1], F32, name="norm_eps")
         inv_norm = keep.tile([P, 1], F32, name="inv_norm")
@@ -378,38 +413,61 @@ def tile_fluxgnn1dlatent_pb_t_kernel(
         right_scale = keep.tile([P, 1], F32, name="right_scale")
         left_scale = keep.tile([P, 1], F32, name="left_scale")
         u_gain = keep.tile([GROUPS, 2, CELLS], F32, name="u_gain")
-        nc.vector.tensor_reduce(out=norm[:], in_=enc_sq_all[:], axis=ALONG_FREE, op=ALU.add)
-        nc.vector.tensor_scalar_add(out=norm_eps[:], in0=norm[:], scalar1=1e-12)
-        quarter(17)
-        nc.vector.reciprocal(out=inv_norm[:], in_=norm_eps[:])
-        nc.vector.tensor_tensor(out=gain[:], in0=norm[:], in1=inv_norm[:], op=ALU.mult)
-        nc.vector.tensor_scalar_mul(out=right_scale[:], in0=inv_norm[:], scalar1=-0.125)
-        nc.vector.tensor_scalar_mul(out=left_scale[:], in0=inv_norm[:], scalar1=0.125)
-
-        for q in range(18, 4 * (GROUPS - 1) + LAG_SUM + 1):
-            quarter(q)
-
-        nc.vector.tensor_scalar(
-            out=u_gain[:], in0=u_bf[:], scalar1=gain[0:GROUPS, 0:1], scalar2=None, op0=ALU.mult
-        )
-        left = keep.tile([GROUPS, 2, CELLS], F32, name="left")
         result = keep.tile([GROUPS, 2, CELLS], F32, name="result")
-        for h in range(2):
-            grid_sums = sums[0:GROUPS, h * FACES : (h + 1) * FACES]
+        last_result = keep.tile([GROUPS, 2, CELLS], F32, name="last_result")
+
+        def cells(w_sums, grids_of_groups, to):
+            hs = grids_of_groups
+            left = work.tile([GROUPS, 2, CELLS], F32, tag="left", name="left", bufs=3)
+            by_grid = w_sums.rearrange("g (h i) -> g h i", i=FACES)
             nc.vector.scalar_tensor_tensor(
-                out=left[:, h, :],
-                in0=grid_sums[:, 0:CELLS],
+                out=left[:, hs, :],
+                in0=by_grid[:, :, 0:CELLS],
                 scalar=left_scale[0:GROUPS, 0:1],
-                in1=u_gain[:, h, :],
+                in1=u_gain[:, hs, :],
                 op0=ALU.mult,
                 op1=ALU.add,
             )
             nc.vector.scalar_tensor_tensor(
-                out=result[:, h, :],
-                in0=grid_sums[:, 1 : CELLS + 1],
+                out=to[:, hs, :],
+                in0=by_grid[:, :, 1 : CELLS + 1],
                 scalar=right_scale[0:GROUPS, 0:1],
-                in1=left[:, h, :],
+                in1=left[:, hs, :],
                 op0=ALU.mult,
                 op1=ALU.add,
             )
-        nc.sync.dma_start(out=out.rearrange("(g h) i -> g h i", h=2), in_=result[:])
+
+        for q in range(Q0, 4 * (GROUPS - 1) + LAG_SUM + 1):
+            if q == 14:
+                nc.vector.tensor_tensor(out=enc_sq[:], in0=enc_cols, in1=enc_cols, op=ALU.mult)
+            if q == 15:
+                nc.vector.tensor_reduce(out=enc_sq_sum[:], in_=enc_sq[:], axis=ALONG_FREE, op=ALU.add)
+            if q == 18:
+                enc_sq_all = psum.tile([P, P], F32, tag="product", name="enc_sq_all", bufs=PRODUCT_BANKS)
+                nc.tensor.matmul(
+                    out=enc_sq_all[:], lhsT=enc_sq_sum[:, 0:1].to_broadcast([P, P]), rhs=ident[:], start=True, stop=True
+                )
+            if q == 19:
+                nc.vector.tensor_reduce(out=norm[:], in_=enc_sq_all[:], axis=ALONG_FREE, op=ALU.add)
+            if q == 20:
+                nc.vector.tensor_scalar_add(out=norm_eps[:], in0=norm[:], scalar1=1e-12)
+            if q == 21:
+                nc.vector.reciprocal(out=inv_norm[:], in_=norm_eps[:])
+            if q == 22:
+                nc.vector.tensor_tensor(out=gain[:], in0=norm[:], in1=inv_norm[:], op=ALU.mult)
+                nc.vector.tensor_scalar_mul(out=right_scale[:], in0=inv_norm[:], scalar1=-0.125)
+                nc.vector.tensor_scalar_mul(out=left_scale[:], in0=inv_norm[:], scalar1=0.125)
+            if q == 23:
+                nc.vector.tensor_scalar(
+                    out=u_gain[:], in0=u_bf[:], scalar1=gain[0:GROUPS, 0:1], scalar2=None, op0=ALU.mult
+                )
+            quarter(q)
+            if q == 4 * (GROUPS - 2) + LAG_SUM + MAIN:
+                cells(sums[0:GROUPS, :], slice(0, 2), result)
+                nc.sync.dma_start(
+                    out=out.rearrange("(g h) i -> g h i", h=2)[0 : GROUPS - 1, :, :], in_=result[0 : GROUPS - 1, :, :]
+                )
+        by_group = out.rearrange("(g h) i -> g h i", h=2)
+        for h in range(2):
+            cells(last_sums[h][0:GROUPS, :], slice(h, h + 1), last_result)
+        nc.sync.dma_start(out=by_group[GROUPS - 1 : GROUPS, :, :], in_=last_result[GROUPS - 1 : GROUPS, :, :])

@@ -31,17 +31,17 @@ FLIP_1 = 1
 LAG_COPY = 1
 EG_BUFS = 2
 HALF_PH = []
-LAG_QE = 2
+LAG_QE = 3
 LAG_LAYER1 = 6
 LAG_GELU = 6
 INT_0 = 10
-INT_1 = 12
+INT_1 = 11
 LAG_QX = 12
 LAG_LAYER2 = 15
 LAG_TANH = 15
 LAG_WEIGH = 16
-LAG_SUM_DIRECT = 17
-LAG_SUM = 22
+LAG_SUM_DIRECT = 18
+LAG_SUM = 18
 MAIN = 1
 S_FIRST = 2
 Q0 = 8
@@ -49,18 +49,16 @@ HS2 = 0
 VORD = 0
 SORD = 0
 TORD = 0
-S_MOD = 2
-S_REM = 1
-S_FROM = 4
+S_SET = [5, 7, 9, 11, 13, 15]
 CPOS = 1
 TANH_BUFS = 12
-DIRECT_CHUNKS = [0, 4, 1, 3, 5]
+DIRECT_CHUNKS = [1, 3, 4, 5, 7]
 WBUFS = 3
-LAST_DIRECT = 1
+LAST_SET = [5]
 XTRA = 0
 BASE_DIRECT = 0
 X4 = []
-HALF_FROM = 0
+HALF_FROM = 7
 
 FLOPS = 2 * GRIDS * FACES * HID * (HID + LATENT)
 
@@ -140,16 +138,16 @@ def tile_fluxgnn1dlatent_pb_t_kernel(
 
         nc.scalar.activation(out=warm_out[:], in_=warm[:], func=ACT.Gelu)
 
-        for t in range(PACK):
-            nc.vector.tensor_copy(
-                out=w2_plane[:, t * P : (t + 1) * P], in_=w2_raw_plane[:, t : HID : PACK]
-            )
+        nc.vector.tensor_copy(out=b2_cols[:], in_=b2_bf[:])
+        nc.vector.tensor_copy(out=rows[:], in_=rows_bf[:])
         nc.vector.tensor_copy(
             out=w2_words[:].bitcast(I32).rearrange("p (t m) -> p t m", t=PACK),
             in_=w2_raw_words[:].bitcast(I32).rearrange("p (m t) -> p t m", t=PACK),
         )
-        nc.vector.tensor_copy(out=b2_cols[:], in_=b2_bf[:])
-        nc.vector.tensor_copy(out=rows[:], in_=rows_bf[:])
+        for t in range(PACK):
+            nc.vector.tensor_copy(
+                out=w2_plane[:, t * P : (t + 1) * P], in_=w2_raw_plane[:, t : HID : PACK]
+            )
 
         e_bank, e_grouped, e_codes, e_plane = {}, {}, {}, {}
         product1, x_raw = {}, {}
@@ -225,13 +223,23 @@ def tile_fluxgnn1dlatent_pb_t_kernel(
 
         def quantise_x(g):
             if 0 <= g < GROUPS:
-                x_codes[g] = work.tile([P, GROUP], U32, tag="x_codes", name="x_codes", bufs=3, align_bytes=64)
-                x_plane[g] = work.tile([P, GROUP], U8, tag="x_plane", name="x_plane", bufs=3, align_bytes=64)
+                x_codes[g] = work.tile([P, GROUP], U32, tag="x_codes", name="x_codes", bufs=4, align_bytes=64)
+                x_plane[g] = work.tile([P, GROUP], U8, tag="x_plane", name="x_plane", bufs=4, align_bytes=64)
                 nc.vector.quantize_mx(
                     out=x_codes[g][:].bitcast(FP8X4),
                     scales=x_plane[g][:],
                     in_=x_grouped[g][:].rearrange("p r t -> p (r t)"),
                 )
+
+        def place(k):
+            g, j = divmod(k, CHUNKS)
+            return 2 * CHUNKS * (g // 2) + 2 * j + (CHUNKS + 1) * (g % 2)
+
+        order = sorted(range(GROUPS * CHUNKS), key=place)
+        last_place = [order.index(g * CHUNKS + CHUNKS - 1) for g in range(GROUPS)]
+
+        def job(i):
+            return order[i] if 0 <= i < GROUPS * CHUNKS else -1
 
         def layer2_product(k):
             g, j = divmod(k, CHUNKS)
@@ -256,7 +264,7 @@ def tile_fluxgnn1dlatent_pb_t_kernel(
         def direct(k):
             g, j = divmod(k, CHUNKS)
             if g == GROUPS - 1:
-                return j % 2 == 1 and j < 2 * LAST_DIRECT
+                return j in LAST_SET
             return j < BASE_DIRECT or (j == 4 and (g % 4 < XTRA or g in X4))
 
         def weigh(k, halved):
@@ -268,7 +276,7 @@ def tile_fluxgnn1dlatent_pb_t_kernel(
                         out=weighted[g][:], in0=tanh[k][:], scalar1=enc_cols[:, j : j + 1], scalar2=None, op0=ALU.mult
                     )
                 else:
-                    halves = 2 if k == GROUPS * CHUNKS - 1 or g >= HALF_FROM or halved else 1
+                    halves = 2 if g >= HALF_FROM or halved else 1
                     for h in range(halves):
                         c = slice(h * GROUP // halves, (h + 1) * GROUP // halves)
                         nc.vector.scalar_tensor_tensor(
@@ -285,7 +293,7 @@ def tile_fluxgnn1dlatent_pb_t_kernel(
             if 0 <= g < GROUPS and direct(k):
                 lhsT = pick_enc[:, (DIRECT_CHUNKS.index(j) + 1) * P - g : (DIRECT_CHUNKS.index(j) + 2) * P - g]
                 if g < GROUPS - 1:
-                    nc.tensor.matmul(out=sums[:], lhsT=lhsT, rhs=tanh[k][:], start=(k == 0), stop=False)
+                    nc.tensor.matmul(out=sums[:], lhsT=lhsT, rhs=tanh[k][:], start=(g == 0 and j == 0), stop=False)
                 else:
                     for h in range(2):
                         fresh = h not in last_sums
@@ -296,7 +304,7 @@ def tile_fluxgnn1dlatent_pb_t_kernel(
                             lhsT=lhsT,
                             rhs=tanh[k][:, h * FACES : (h + 1) * FACES],
                             start=fresh,
-                            stop=False,
+                            stop=(j == CHUNKS - 1),
                         )
 
         def sum_weighted(g):
@@ -320,7 +328,7 @@ def tile_fluxgnn1dlatent_pb_t_kernel(
                             lhsT=lhsT,
                             rhs=weighted[g][:, h * FACES : (h + 1) * FACES],
                             start=fresh,
-                            stop=True,
+                            stop=not direct(GROUPS * CHUNKS - 1),
                         )
 
         def gelu_from_group_1(k):
@@ -328,7 +336,7 @@ def tile_fluxgnn1dlatent_pb_t_kernel(
                 gelu(k)
 
         def on_scalar(b):
-            return 0 <= b < S_FIRST or (b >= S_FROM and b % S_MOD == S_REM)
+            return 0 <= b < S_FIRST or b in S_SET
 
         def quarter(q):
             def group_of(lag):
@@ -342,23 +350,26 @@ def tile_fluxgnn1dlatent_pb_t_kernel(
                     flip_edge_hid(b)
             if q - LAG_LAYER1 >= PACK:
                 layer1_product(q - LAG_LAYER1)
-            layer2_product(2 * (q - LAG_LAYER2))
-            layer2_product(2 * (q - LAG_LAYER2) + 1)
+            layer2_product(job(2 * (q - LAG_LAYER2)))
+            layer2_product(job(2 * (q - LAG_LAYER2) + 1))
             if TORD == 0 and q > 0:
                 for b in grids(0, 0):
                     flip_edge_hid(b)
-            sum_direct(2 * (q - LAG_SUM_DIRECT))
-            sum_direct(2 * (q - LAG_SUM_DIRECT) + 1)
-            sum_weighted(group_of(LAG_SUM))
+            sum_direct(job(2 * (q - LAG_SUM_DIRECT)))
+            if 2 * (q - LAG_SUM_DIRECT) + 1 != GROUPS * CHUNKS - 1:
+                sum_direct(job(2 * (q - LAG_SUM_DIRECT) + 1))
+            for g in range(GROUPS - 1):
+                if last_place[g] // 2 == q - LAG_SUM:
+                    sum_weighted(g)
 
             if CPOS == 1 and q != LAG_COPY:
                 for b in grids(LAG_COPY, LAG_COPY):
                     if on_scalar(b):
                         copy_edge_hid(b, nc.scalar.copy)
             if SORD == 0: gelu_from_group_1(q - LAG_GELU)
-            tanh_of(2 * (q - LAG_TANH))
+            tanh_of(job(2 * (q - LAG_TANH)))
             if SORD == 1: gelu_from_group_1(q - LAG_GELU)
-            tanh_of(2 * (q - LAG_TANH) + 1)
+            tanh_of(job(2 * (q - LAG_TANH) + 1))
             if SORD == 2: gelu_from_group_1(q - LAG_GELU)
             if CPOS == 0 and q != LAG_COPY:
                 for b in grids(LAG_COPY, LAG_COPY):
@@ -366,44 +377,43 @@ def tile_fluxgnn1dlatent_pb_t_kernel(
                         copy_edge_hid(b, nc.scalar.copy)
 
             if VORD == 1:
-                weigh(2 * (q - LAG_WEIGH), q % 4 in HALF_PH)
+                weigh(job(2 * (q - LAG_WEIGH)), q % 4 in HALF_PH)
             for b in grids(LAG_COPY, LAG_COPY) if q != LAG_COPY else []:
                 if not on_scalar(b):
                     copy_edge_hid(b, nc.vector.tensor_copy)
             for b in grids(INT_0, INT_1):
                 interleave(b)
             if VORD == 0:
-                weigh(2 * (q - LAG_WEIGH), q % 4 in HALF_PH)
+                weigh(job(2 * (q - LAG_WEIGH)), q % 4 in HALF_PH)
             if q != LAG_QE:
                 quantise_edge_hid(group_of(LAG_QE))
             quantise_x(group_of(LAG_QX))
-            weigh(2 * (q - LAG_WEIGH) + 1, q % 4 in HALF_PH)
+            weigh(job(2 * (q - LAG_WEIGH) + 1), q % 4 in HALF_PH)
 
         flip_edge_hid(0)
         copy_edge_hid(0, nc.scalar.copy)
-        quantise_edge_hid(0, 0)
         flip_edge_hid(1)
         copy_edge_hid(1, nc.scalar.copy)
-        cols_ps = psum.tile([P, P], F32, tag="product", name="cols_ps", bufs=PRODUCT_BANKS)
-        nc.tensor.transpose(cols_ps[:], rows[:], ident[:])
-        flip_edge_hid(2)
+        quantise_edge_hid(0, 0)
         for t in range(PACK):
             layer1_product(t, 0)
             gelu(t, 0)
         quantise_edge_hid(0, 1)
-        nc.vector.tensor_copy(out=cols[:], in_=cols_ps[:])
+        flip_edge_hid(2)
+        copy_edge_hid(2, nc.scalar.copy if HS2 else nc.vector.tensor_copy)
         flip_edge_hid(3)
+        copy_edge_hid(3, nc.vector.tensor_copy)
         for t in range(PACK):
             layer1_product(t, 1)
-        copy_edge_hid(2, nc.scalar.copy if HS2 else nc.vector.tensor_copy)
-        for t in range(PACK):
             gelu(t, 1)
-        copy_edge_hid(3, nc.vector.tensor_copy)
+        cols_ps = psum.tile([P, P], F32, tag="product", name="cols_ps", bufs=PRODUCT_BANKS)
+        nc.tensor.transpose(cols_ps[:], rows[:], ident[:])
+        quantise_edge_hid(1)
+        nc.vector.tensor_copy(out=cols[:], in_=cols_ps[:])
         enc_cols = cols[:, 0:CHUNKS]
         b3_cols = cols[:, CHUNKS : 2 * CHUNKS]
         for n, j in enumerate(DIRECT_CHUNKS):
             nc.vector.tensor_copy(out=pick_enc[:, (n + 1) * P : (n + 1) * P + 1], in_=enc_cols[:, j : j + 1])
-        quantise_edge_hid(1)
         enc_sq = keep.tile([P, CHUNKS], F32, name="enc_sq")
         enc_sq_sum = keep.tile([P, 1], F32, name="enc_sq_sum")
         norm = keep.tile([P, 1], F32, name="norm")
@@ -414,7 +424,7 @@ def tile_fluxgnn1dlatent_pb_t_kernel(
         left_scale = keep.tile([P, 1], F32, name="left_scale")
         u_gain = keep.tile([GROUPS, 2, CELLS], F32, name="u_gain")
         result = keep.tile([GROUPS, 2, CELLS], F32, name="result")
-        last_result = keep.tile([GROUPS, 2, CELLS], F32, name="last_result")
+        last_result = keep.tile([GROUPS, 2, FACES], F32, name="last_result")
 
         def cells(w_sums, grids_of_groups, to):
             hs = grids_of_groups
@@ -429,7 +439,7 @@ def tile_fluxgnn1dlatent_pb_t_kernel(
                 op1=ALU.add,
             )
             nc.vector.scalar_tensor_tensor(
-                out=to[:, hs, :],
+                out=to[:, hs, 0:CELLS],
                 in0=by_grid[:, :, 1 : CELLS + 1],
                 scalar=right_scale[0:GROUPS, 0:1],
                 in1=left[:, hs, :],
@@ -437,7 +447,7 @@ def tile_fluxgnn1dlatent_pb_t_kernel(
                 op1=ALU.add,
             )
 
-        for q in range(Q0, 4 * (GROUPS - 1) + LAG_SUM + 1):
+        for q in range(Q0, max(4 * GROUPS + LAG_WEIGH, last_place[GROUPS - 2] // 2 + LAG_SUM + MAIN + 1)):
             if q == 14:
                 nc.vector.tensor_tensor(out=enc_sq[:], in0=enc_cols, in1=enc_cols, op=ALU.mult)
             if q == 15:
@@ -462,12 +472,14 @@ def tile_fluxgnn1dlatent_pb_t_kernel(
                     out=u_gain[:], in0=u_bf[:], scalar1=gain[0:GROUPS, 0:1], scalar2=None, op0=ALU.mult
                 )
             quarter(q)
-            if q == 4 * (GROUPS - 2) + LAG_SUM + MAIN:
+            if q == last_place[GROUPS - 2] // 2 + LAG_SUM + MAIN:
                 cells(sums[0:GROUPS, :], slice(0, 2), result)
                 nc.sync.dma_start(
                     out=out.rearrange("(g h) i -> g h i", h=2)[0 : GROUPS - 1, :, :], in_=result[0 : GROUPS - 1, :, :]
                 )
+        sum_weighted(GROUPS - 1)
+        sum_direct(GROUPS * CHUNKS - 1)
         by_group = out.rearrange("(g h) i -> g h i", h=2)
         for h in range(2):
             cells(last_sums[h][0:GROUPS, :], slice(h, h + 1), last_result)
-        nc.sync.dma_start(out=by_group[GROUPS - 1 : GROUPS, :, :], in_=last_result[GROUPS - 1 : GROUPS, :, :])
+        nc.sync.dma_start(out=by_group[GROUPS - 1 : GROUPS, :, :], in_=last_result[GROUPS - 1 : GROUPS, :, 0:CELLS])

@@ -22,15 +22,17 @@ LATENT = 1024
 PACK = 4
 GROUP = 2 * FACES
 GROUPS = GRIDS // 2
+LAST = GROUPS - 1
 CHUNKS = LATENT // P
 
 FLIP_BANKS = 2
 PRODUCT_BANKS = 5
 
-FLIP_1 = 1
 LAG_COPY = 1
-EG_BUFS = 2
-HALF_PH = []
+LAG_COPY_S = 1
+LAG_SUM_6 = 18
+TSPLIT = 0
+PIECES = 2
 LAG_QE = 3
 LAG_LAYER1 = 6
 LAG_GELU = 6
@@ -42,23 +44,29 @@ LAG_TANH = 15
 LAG_WEIGH = 16
 LAG_SUM_DIRECT = 18
 LAG_SUM = 18
-MAIN = 1
-S_FIRST = 2
-Q0 = 8
-HS2 = 0
-VORD = 0
-SORD = 0
-TORD = 0
+STAGGER = 4
 S_SET = [5, 7, 9, 11, 13, 15]
+DIRECT = [(7, 3)]
+LATE = 1
+HALF_DIRECT = []
+SUM_GAP = 0
+DH_LAG = 19
+SPLIT = 2
+SPLIT_FROM = 4
 CPOS = 1
+TORD = 0
+FPOS = 0
+Q0 = 8
 TANH_BUFS = 12
-DIRECT_CHUNKS = [1, 3, 4, 5, 7]
-WBUFS = 3
-LAST_SET = [5]
-XTRA = 0
-BASE_DIRECT = 0
-X4 = []
-HALF_FROM = 7
+NORM_Q = 14
+E0_SPLIT = 0
+CELL_Q = 0
+HS2 = 0
+HF = 0
+HV = 0
+EARLY = 4
+E1_FIRST = 0
+CORD = 0
 
 FLOPS = 2 * GRIDS * FACES * HID * (HID + LATENT)
 
@@ -87,7 +95,8 @@ def tile_fluxgnn1dlatent_pb_t_kernel(
         cols = keep.tile([P, P], F32, name="cols")
         ident = keep.tile([P, P], F32, name="ident")
         pick = keep.tile([P, 2 * P], F32, name="pick")
-        pick_enc = keep.tile([P, 6 * P], F32, name="pick_enc")
+        direct_chunks = sorted(set([j for s, j in DIRECT + HALF_DIRECT]))
+        pick_enc = keep.tile([P, (len(direct_chunks) + 1) * P], F32, name="pick_enc")
         b2_bf = keep.tile([P, PACK], BF16, name="b2_bf")
         b2_cols = keep.tile([P, PACK], F32, name="b2_cols")
         u_bf = keep.tile([GROUPS, 2, CELLS], BF16, name="u_bf")
@@ -102,7 +111,8 @@ def tile_fluxgnn1dlatent_pb_t_kernel(
         make_identity(nc, ident[:])
         nc.vector.memset(pick[:], 0.0)
         nc.vector.memset(pick[:, P : P + 1], 1.0)
-        nc.vector.memset(pick_enc[:], 0.0)
+        if direct_chunks:
+            nc.vector.memset(pick_enc[:], 0.0)
 
         def load_grid(b):
             nc.sync.dma_start(
@@ -127,13 +137,22 @@ def tile_fluxgnn1dlatent_pb_t_kernel(
             out=rows_bf[CHUNKS : 2 * CHUNKS, :], in_=b3.rearrange("(j p) -> j p", p=P)
         )
         nc.scalar.dma_start(out=u_bf[:], in_=u.rearrange("(g h) i -> g h i", h=2))
-        load_grid(0)
+        if E0_SPLIT:
+            for n in range(2):
+                nc.sync.dma_start(out=e_in[0][:, n, :], in_=tokens[n * P : (n + 1) * P, :])
+        else:
+            load_grid(0)
+        if E1_FIRST == 1:
+            load_grid(1)
         load_weight(w2_raw_words, w2_raw_plane, W2_words, W2_scales)
-        load_grid(1)
+        if E1_FIRST == 0:
+            load_grid(1)
         load_grid(2)
         load_grid(3)
+        for b in range(4, EARLY):
+            load_grid(b)
         load_weight(w3_words, w3_plane, W3_words, W3_scales)
-        for b in range(4, GRIDS):
+        for b in range(EARLY, GRIDS):
             load_grid(b)
 
         nc.scalar.activation(out=warm_out[:], in_=warm[:], func=ACT.Gelu)
@@ -168,31 +187,28 @@ def tile_fluxgnn1dlatent_pb_t_kernel(
             if 0 <= b < GRIDS:
                 g, h = divmod(b, 2)
                 if g not in e_grouped:
-                    e_grouped[g] = work.tile([P, GROUP, PACK], BF16, tag="e_grouped", name="e_grouped", bufs=EG_BUFS, align_bytes=64)
+                    e_grouped[g] = work.tile([P, GROUP, PACK], BF16, tag="e_grouped", name="e_grouped", align_bytes=64)
                 copy(
                     out=e_grouped[g][:, h * FACES : (h + 1) * FACES, :].rearrange("p r t -> p (r t)").bitcast(F32).rearrange("p (r w) -> p r w", w=2),
                     in_=e_bank[b][:].rearrange("p w r -> p r w"),
                 )
 
-        def quantise_edge_hid(g, h=None):
+        def quantise_edge_hid(g, c):
             if 0 <= g < GROUPS:
-                if h != 1:
+                if g not in e_codes:
                     e_codes[g] = work.tile([P, GROUP], U32, tag="e_codes", name="e_codes", bufs=3, align_bytes=64)
                     e_plane[g] = work.tile([P, GROUP], U8, tag="e_plane", name="e_plane", bufs=3, align_bytes=64)
-                c = slice(0, GROUP) if h is None else slice(h * FACES, (h + 1) * FACES)
                 nc.vector.quantize_mx(
                     out=e_codes[g][:, c].bitcast(FP8X4),
                     scales=e_plane[g][:, c],
                     in_=e_grouped[g][:, c, :].rearrange("p r t -> p (r t)"),
                 )
 
-        def layer1_product(k, h=None):
-            g, t = divmod(k, PACK)
+        def layer1_product(g, t, c):
             if 0 <= g < GROUPS:
-                c = slice(0, GROUP) if h is None else slice(h * FACES, (h + 1) * FACES)
-                product1[k, h] = psum.tile([P, c.stop - c.start], F32, tag="product", name="product1", bufs=PRODUCT_BANKS)
+                product1[g, t, c.start] = psum.tile([P, c.stop - c.start], F32, tag="product", name="product1", bufs=PRODUCT_BANKS)
                 nc.tensor.matmul_mx(
-                    out=product1[k, h][:],
+                    out=product1[g, t, c.start][:],
                     lhsT=w2_words[:, t * P : (t + 1) * P].bitcast(FP8X4),
                     lhsT_scale=w2_plane[:, t * P : (t + 1) * P],
                     rhs=e_codes[g][:, c].bitcast(FP8X4),
@@ -201,21 +217,19 @@ def tile_fluxgnn1dlatent_pb_t_kernel(
                     stop=True,
                 )
 
-        def gelu(k, h=None):
-            g, t = divmod(k, PACK)
+        def gelu(g, t, c):
             if 0 <= g < GROUPS:
-                if t == 0 and h != 1:
+                if g not in x_raw:
                     x_raw[g] = work.tile([P, PACK, GROUP], BF16, tag="x_raw", name="x_raw", bufs=3)
-                c = slice(0, GROUP) if h is None else slice(h * FACES, (h + 1) * FACES)
                 nc.scalar.activation(
-                    out=x_raw[g][:, t, c], in_=product1[k, h][:], func=ACT.Gelu, bias=b2_cols[:, t : t + 1]
+                    out=x_raw[g][:, t, c], in_=product1[g, t, c.start][:], func=ACT.Gelu, bias=b2_cols[:, t : t + 1]
                 )
 
         def interleave(b):
             if 0 <= b < GRIDS:
                 g, h = divmod(b, 2)
                 if h == 0:
-                    x_grouped[g] = work.tile([P, GROUP, PACK], BF16, tag="x_grouped", name="x_grouped", bufs=2, align_bytes=64)
+                    x_grouped[g] = work.tile([P, GROUP, PACK], BF16, tag="x_grouped", name="x_grouped", align_bytes=64)
                 nc.vector.tensor_copy(
                     out=x_grouped[g][:, h * FACES : (h + 1) * FACES, :].rearrange("p (c i) t -> p c t i", i=4),
                     in_=x_raw[g][:, :, h * FACES : (h + 1) * FACES].rearrange("p t (c i) -> p c t i", i=4),
@@ -231,255 +245,299 @@ def tile_fluxgnn1dlatent_pb_t_kernel(
                     in_=x_grouped[g][:].rearrange("p r t -> p (r t)"),
                 )
 
-        def place(k):
-            g, j = divmod(k, CHUNKS)
-            return 2 * CHUNKS * (g // 2) + 2 * j + (CHUNKS + 1) * (g % 2)
+        whole = slice(0, GROUP)
+        streams = [(g, whole) for g in range(LAST)]
+        for h in range(LATE):
+            streams.append((LAST, slice(h * GROUP // LATE, (h + 1) * GROUP // LATE)))
+        order = sorted(
+            [(s, j) for s in range(len(streams)) for j in range(CHUNKS)],
+            key=lambda job: (STAGGER * job[0] + job[1], job[0]),
+        )
+        last_place = [order.index((s, CHUNKS - 1)) for s in range(len(streams))]
 
-        order = sorted(range(GROUPS * CHUNKS), key=place)
-        last_place = [order.index(g * CHUNKS + CHUNKS - 1) for g in range(GROUPS)]
+        covered, summed = [], []
 
-        def job(i):
-            return order[i] if 0 <= i < GROUPS * CHUNKS else -1
-
-        def layer2_product(k):
-            g, j = divmod(k, CHUNKS)
-            if 0 <= g < GROUPS:
-                product2[k] = psum.tile([P, GROUP], F32, tag="product", name="product2", bufs=PRODUCT_BANKS)
+        def layer2_product(i):
+            if 0 <= i < len(order):
+                s, j = order[i]
+                g, c = streams[s]
+                product2[i] = psum.tile([P, c.stop - c.start], F32, tag="product", name="product2", bufs=PRODUCT_BANKS)
                 nc.tensor.matmul_mx(
-                    out=product2[k][:],
+                    out=product2[i][:],
                     lhsT=w3_words[:, j * P : (j + 1) * P].bitcast(FP8X4),
                     lhsT_scale=w3_plane[:, j * P : (j + 1) * P],
-                    rhs=x_codes[g][:].bitcast(FP8X4),
-                    rhs_scale=x_plane[g][:],
+                    rhs=x_codes[g][:, c].bitcast(FP8X4),
+                    rhs_scale=x_plane[g][:, c],
                     start=True,
                     stop=True,
                 )
 
-        def tanh_of(k):
-            g, j = divmod(k, CHUNKS)
-            if 0 <= g < GROUPS:
-                tanh[k] = work.tile([P, GROUP], F32, tag="tanh", name="tanh", bufs=TANH_BUFS)
-                nc.scalar.activation(out=tanh[k][:], in_=product2[k][:], func=ACT.Tanh, bias=b3_cols[:, j : j + 1])
+        def tanh_of(i):
+            if 0 <= i < len(order):
+                s, j = order[i]
+                g, c = streams[s]
+                tanh[i] = work.tile([P, c.stop - c.start], F32, tag="tanh", name="tanh", bufs=TANH_BUFS)
+                n = c.stop - c.start
+                parts = 2 if TSPLIT and i == len(order) - 1 else 1
+                for a in range(parts):
+                    part = slice(a * n // parts, (a + 1) * n // parts)
+                    nc.scalar.activation(
+                        out=tanh[i][:, part], in_=product2[i][:, part], func=ACT.Tanh, bias=b3_cols[:, j : j + 1]
+                    )
 
-        def direct(k):
-            g, j = divmod(k, CHUNKS)
-            if g == GROUPS - 1:
-                return j in LAST_SET
-            return j < BASE_DIRECT or (j == 4 and (g % 4 < XTRA or g in X4))
-
-        def weigh(k, halved):
-            g, j = divmod(k, CHUNKS)
-            if 0 <= g < GROUPS and not direct(k):
-                if g not in weighted:
-                    weighted[g] = work.tile([P, GROUP], F32, tag="weighted", name="weighted", bufs=WBUFS)
+        def weigh(i):
+            if 0 <= i < len(order) and order[i] not in DIRECT:
+                covered.append((order[i], 0))
+                if order[i] not in HALF_DIRECT:
+                    covered.append((order[i], 1))
+                s, j = order[i]
+                g, c = streams[s]
+                if s not in weighted:
+                    weighted[s] = work.tile([P, c.stop - c.start], F32, tag="weighted", name="weighted", bufs=4)
                     nc.vector.tensor_scalar(
-                        out=weighted[g][:], in0=tanh[k][:], scalar1=enc_cols[:, j : j + 1], scalar2=None, op0=ALU.mult
+                        out=weighted[s][:], in0=tanh[i][:], scalar1=enc_cols[:, j : j + 1], scalar2=None, op0=ALU.mult
                     )
                 else:
-                    halves = 2 if g >= HALF_FROM or halved else 1
-                    for h in range(halves):
-                        c = slice(h * GROUP // halves, (h + 1) * GROUP // halves)
+                    n = c.stop - c.start
+                    parts = SPLIT if s >= LAST and j >= SPLIT_FROM else 1
+                    if order[i] in HALF_DIRECT:
+                        n, parts = n // 2, 1
+                    for a in range(parts):
+                        part = slice(a * n // parts, (a + 1) * n // parts)
                         nc.vector.scalar_tensor_tensor(
-                            out=weighted[g][:, c],
-                            in0=tanh[k][:, c],
+                            out=weighted[s][:, part],
+                            in0=tanh[i][:, part],
                             scalar=enc_cols[:, j : j + 1],
-                            in1=weighted[g][:, c],
+                            in1=weighted[s][:, part],
                             op0=ALU.mult,
                             op1=ALU.add,
                         )
 
-        def sum_direct(k):
-            g, j = divmod(k, CHUNKS)
-            if 0 <= g < GROUPS and direct(k):
-                lhsT = pick_enc[:, (DIRECT_CHUNKS.index(j) + 1) * P - g : (DIRECT_CHUNKS.index(j) + 2) * P - g]
-                if g < GROUPS - 1:
-                    nc.tensor.matmul(out=sums[:], lhsT=lhsT, rhs=tanh[k][:], start=(g == 0 and j == 0), stop=False)
-                else:
-                    for h in range(2):
-                        fresh = h not in last_sums
-                        if fresh:
-                            last_sums[h] = psum.tile([P, FACES], F32, tag="flip", name="last_sums", bufs=FLIP_BANKS)
-                        nc.tensor.matmul(
-                            out=last_sums[h][:],
-                            lhsT=lhsT,
-                            rhs=tanh[k][:, h * FACES : (h + 1) * FACES],
-                            start=fresh,
-                            stop=(j == CHUNKS - 1),
-                        )
+        opened = []
+        pieces = [(0, GROUP)] if PIECES == 1 else [(0, FACES), (FACES, FACES)]
 
-        def sum_weighted(g):
-            if 0 <= g < GROUPS:
-                lhsT = pick[:, P - g : 2 * P - g]
-                if g < GROUPS - 1:
-                    nc.tensor.matmul(
-                        out=sums[:],
-                        lhsT=lhsT,
-                        rhs=weighted[g][:],
-                        start=(g == 0 and BASE_DIRECT == 0),
-                        stop=(g == GROUPS - 2),
-                    )
-                else:
-                    for h in range(2):
-                        fresh = h not in last_sums
-                        if fresh:
-                            last_sums[h] = psum.tile([P, FACES], F32, tag="flip", name="last_sums", bufs=FLIP_BANKS)
-                        nc.tensor.matmul(
-                            out=last_sums[h][:],
-                            lhsT=lhsT,
-                            rhs=weighted[g][:, h * FACES : (h + 1) * FACES],
-                            start=fresh,
-                            stop=not direct(GROUPS * CHUNKS - 1),
-                        )
+        def add_to_sums(s, lhsT, rhs, final, cols_of=slice(0, GROUP)):
+            g, c = streams[s]
+            if s < LAST:
+                nc.tensor.matmul(out=sums[:, cols_of], lhsT=lhsT, rhs=rhs[:, cols_of], start=(0 not in opened), stop=final and s == LAST - 1)
+                opened.append(0)
+            else:
+                for a, n in pieces:
+                    fresh = a not in last_sums
+                    if fresh and a < GROUP - P:
+                        last_sums[a] = psum.tile([P, n], F32, tag="flip", name="last_sums", bufs=FLIP_BANKS)
+                    elif fresh:
+                        last_sums[a] = psum.tile([P, n], F32, tag="product", name="last_sums", bufs=PRODUCT_BANKS)
+                    nc.tensor.matmul(out=last_sums[a][:], lhsT=lhsT, rhs=rhs[:, a : a + n], start=fresh, stop=final)
 
-        def gelu_from_group_1(k):
-            if k >= PACK:
-                gelu(k)
+        def sum_direct(i):
+            if 0 <= i < len(order) and order[i] in DIRECT:
+                covered.extend([(order[i], 0), (order[i], 1)])
+                s, j = order[i]
+                g, c = streams[s]
+                n = direct_chunks.index(j) + 1
+                add_to_sums(s, pick_enc[:, n * P - g : (n + 1) * P - g], tanh[i][:], False)
 
-        def on_scalar(b):
-            return 0 <= b < S_FIRST or b in S_SET
+        def sum_half_direct(i):
+            if 0 <= i < len(order) and order[i] in HALF_DIRECT:
+                covered.append((order[i], 1))
+                s, j = order[i]
+                g, c = streams[s]
+                n = direct_chunks.index(j) + 1
+                add_to_sums(s, pick_enc[:, n * P - g : (n + 1) * P - g], tanh[i][:], False, slice(FACES, GROUP))
+
+        def sum_weighted(s, h=None):
+            g, c = streams[s]
+            summed.extend([(s, 0), (s, 1)] if h is None else [(s, h)])
+            if h is None:
+                add_to_sums(s, pick[:, P - g : 2 * P - g], weighted[s][:], True)
+            else:
+                add_to_sums(s, pick[:, P - g : 2 * P - g], weighted[s][:], h == 1, slice(h * FACES, (h + 1) * FACES))
 
         def quarter(q):
             def group_of(lag):
-                return (q - lag) // 4 if (q - lag) % 4 == 0 else -99
+                return (q - lag) // 4 if (q - lag) % 4 == 0 and q - lag > 3 else -1
 
-            def grids(lag0, lag1):
-                return [2 * group_of(lag0), 2 * group_of(lag1) + 1]
-
-            if TORD == 1 and q > 0:
-                for b in grids(0, 0):
-                    flip_edge_hid(b)
+            if TORD == 1:
+                flip_edge_hid(2 * group_of(0))
+                flip_edge_hid(2 * group_of(FPOS) + 1)
             if q - LAG_LAYER1 >= PACK:
-                layer1_product(q - LAG_LAYER1)
-            layer2_product(job(2 * (q - LAG_LAYER2)))
-            layer2_product(job(2 * (q - LAG_LAYER2) + 1))
-            if TORD == 0 and q > 0:
-                for b in grids(0, 0):
-                    flip_edge_hid(b)
-            sum_direct(job(2 * (q - LAG_SUM_DIRECT)))
-            if 2 * (q - LAG_SUM_DIRECT) + 1 != GROUPS * CHUNKS - 1:
-                sum_direct(job(2 * (q - LAG_SUM_DIRECT) + 1))
-            for g in range(GROUPS - 1):
-                if last_place[g] // 2 == q - LAG_SUM:
-                    sum_weighted(g)
+                layer1_product((q - LAG_LAYER1) // PACK, (q - LAG_LAYER1) % PACK, whole)
+            layer2_product(2 * (q - LAG_LAYER2))
+            layer2_product(2 * (q - LAG_LAYER2) + 1)
+            if TORD == 0:
+                flip_edge_hid(2 * group_of(0))
+                flip_edge_hid(2 * group_of(FPOS) + 1)
+            sum_direct(2 * (q - LAG_SUM_DIRECT))
+            sum_direct(2 * (q - LAG_SUM_DIRECT) + 1)
+            for s in range(LAST):
+                if s == LAST - 1:
+                    if last_place[s] // 2 == q - LAG_SUM_6:
+                        sum_weighted(s)
+                elif SUM_GAP == 0 or s == 0:
+                    if last_place[s] // 2 == q - LAG_SUM:
+                        sum_weighted(s)
+                else:
+                    if last_place[s] // 2 == q - LAG_SUM:
+                        sum_weighted(s, 0)
+                    if last_place[s] // 2 == q - LAG_SUM - SUM_GAP:
+                        sum_weighted(s, 1)
+            sum_half_direct(2 * (q - DH_LAG))
+            sum_half_direct(2 * (q - DH_LAG) + 1)
 
-            if CPOS == 1 and q != LAG_COPY:
-                for b in grids(LAG_COPY, LAG_COPY):
-                    if on_scalar(b):
+            copies = [2 * group_of(LAG_COPY), 2 * group_of(LAG_COPY + FPOS) + 1]
+            copies_s = [2 * group_of(LAG_COPY_S), 2 * group_of(LAG_COPY_S + FPOS) + 1]
+            if CPOS == 1:
+                for b in copies_s:
+                    if b in S_SET:
                         copy_edge_hid(b, nc.scalar.copy)
-            if SORD == 0: gelu_from_group_1(q - LAG_GELU)
-            tanh_of(job(2 * (q - LAG_TANH)))
-            if SORD == 1: gelu_from_group_1(q - LAG_GELU)
-            tanh_of(job(2 * (q - LAG_TANH) + 1))
-            if SORD == 2: gelu_from_group_1(q - LAG_GELU)
-            if CPOS == 0 and q != LAG_COPY:
-                for b in grids(LAG_COPY, LAG_COPY):
-                    if on_scalar(b):
+            if q - LAG_GELU >= PACK:
+                gelu((q - LAG_GELU) // PACK, (q - LAG_GELU) % PACK, whole)
+            tanh_of(2 * (q - LAG_TANH))
+            tanh_of(2 * (q - LAG_TANH) + 1)
+            if CPOS == 0:
+                for b in copies_s:
+                    if b in S_SET:
                         copy_edge_hid(b, nc.scalar.copy)
 
-            if VORD == 1:
-                weigh(job(2 * (q - LAG_WEIGH)), q % 4 in HALF_PH)
-            for b in grids(LAG_COPY, LAG_COPY) if q != LAG_COPY else []:
-                if not on_scalar(b):
+            for b in copies:
+                if b not in S_SET:
                     copy_edge_hid(b, nc.vector.tensor_copy)
-            for b in grids(INT_0, INT_1):
-                interleave(b)
-            if VORD == 0:
-                weigh(job(2 * (q - LAG_WEIGH)), q % 4 in HALF_PH)
-            if q != LAG_QE:
-                quantise_edge_hid(group_of(LAG_QE))
-            quantise_x(group_of(LAG_QX))
-            weigh(job(2 * (q - LAG_WEIGH) + 1), q % 4 in HALF_PH)
+            if q >= INT_0:
+                interleave(2 * ((q - INT_0) // 4) if (q - INT_0) % 4 == 0 else -1)
+            if q >= INT_1:
+                interleave(2 * ((q - INT_1) // 4) + 1 if (q - INT_1) % 4 == 0 else -1)
+            weigh(2 * (q - LAG_WEIGH))
+            quantise_edge_hid(group_of(LAG_QE), whole)
+            if q >= LAG_QX and (q - LAG_QX) % 4 == 0:
+                quantise_x((q - LAG_QX) // 4)
+            weigh(2 * (q - LAG_WEIGH) + 1)
 
+        halves = [slice(0, FACES), slice(FACES, GROUP)]
         flip_edge_hid(0)
         copy_edge_hid(0, nc.scalar.copy)
         flip_edge_hid(1)
         copy_edge_hid(1, nc.scalar.copy)
-        quantise_edge_hid(0, 0)
+        quantise_edge_hid(0, halves[0])
+        if HF == 1:
+            flip_edge_hid(2)
         for t in range(PACK):
-            layer1_product(t, 0)
-            gelu(t, 0)
-        quantise_edge_hid(0, 1)
-        flip_edge_hid(2)
+            layer1_product(0, t, halves[0])
+            gelu(0, t, halves[0])
+        if HF == 0:
+            flip_edge_hid(2)
+        if HV == 0:
+            quantise_edge_hid(0, halves[1])
         copy_edge_hid(2, nc.scalar.copy if HS2 else nc.vector.tensor_copy)
+        if HV == 1:
+            quantise_edge_hid(0, halves[1])
         flip_edge_hid(3)
         copy_edge_hid(3, nc.vector.tensor_copy)
         for t in range(PACK):
-            layer1_product(t, 1)
-            gelu(t, 1)
+            layer1_product(0, t, halves[1])
+            gelu(0, t, halves[1])
         cols_ps = psum.tile([P, P], F32, tag="product", name="cols_ps", bufs=PRODUCT_BANKS)
         nc.tensor.transpose(cols_ps[:], rows[:], ident[:])
-        quantise_edge_hid(1)
+        quantise_edge_hid(1, whole)
         nc.vector.tensor_copy(out=cols[:], in_=cols_ps[:])
         enc_cols = cols[:, 0:CHUNKS]
         b3_cols = cols[:, CHUNKS : 2 * CHUNKS]
-        for n, j in enumerate(DIRECT_CHUNKS):
+        for n, j in enumerate(direct_chunks):
             nc.vector.tensor_copy(out=pick_enc[:, (n + 1) * P : (n + 1) * P + 1], in_=enc_cols[:, j : j + 1])
+
         enc_sq = keep.tile([P, CHUNKS], F32, name="enc_sq")
         enc_sq_sum = keep.tile([P, 1], F32, name="enc_sq_sum")
         norm = keep.tile([P, 1], F32, name="norm")
         norm_eps = keep.tile([P, 1], F32, name="norm_eps")
         inv_norm = keep.tile([P, 1], F32, name="inv_norm")
-        gain = keep.tile([P, 1], F32, name="gain")
-        right_scale = keep.tile([P, 1], F32, name="right_scale")
-        left_scale = keep.tile([P, 1], F32, name="left_scale")
-        u_gain = keep.tile([GROUPS, 2, CELLS], F32, name="u_gain")
+        scale = keep.tile([P, 1], F32, name="scale")
+        u_gain = keep.tile([GROUPS, 2, FACES], F32, name="u_gain")
         result = keep.tile([GROUPS, 2, CELLS], F32, name="result")
         last_result = keep.tile([GROUPS, 2, FACES], F32, name="last_result")
-
-        def cells(w_sums, grids_of_groups, to):
-            hs = grids_of_groups
-            left = work.tile([GROUPS, 2, CELLS], F32, tag="left", name="left", bufs=3)
-            by_grid = w_sums.rearrange("g (h i) -> g h i", i=FACES)
-            nc.vector.scalar_tensor_tensor(
-                out=left[:, hs, :],
-                in0=by_grid[:, :, 0:CELLS],
-                scalar=left_scale[0:GROUPS, 0:1],
-                in1=u_gain[:, hs, :],
-                op0=ALU.mult,
-                op1=ALU.add,
-            )
-            nc.vector.scalar_tensor_tensor(
-                out=to[:, hs, 0:CELLS],
-                in0=by_grid[:, :, 1 : CELLS + 1],
-                scalar=right_scale[0:GROUPS, 0:1],
-                in1=left[:, hs, :],
-                op0=ALU.mult,
-                op1=ALU.add,
-            )
-
-        for q in range(Q0, max(4 * GROUPS + LAG_WEIGH, last_place[GROUPS - 2] // 2 + LAG_SUM + MAIN + 1)):
-            if q == 14:
-                nc.vector.tensor_tensor(out=enc_sq[:], in0=enc_cols, in1=enc_cols, op=ALU.mult)
-            if q == 15:
-                nc.vector.tensor_reduce(out=enc_sq_sum[:], in_=enc_sq[:], axis=ALONG_FREE, op=ALU.add)
-            if q == 18:
-                enc_sq_all = psum.tile([P, P], F32, tag="product", name="enc_sq_all", bufs=PRODUCT_BANKS)
-                nc.tensor.matmul(
-                    out=enc_sq_all[:], lhsT=enc_sq_sum[:, 0:1].to_broadcast([P, P]), rhs=ident[:], start=True, stop=True
-                )
-            if q == 19:
-                nc.vector.tensor_reduce(out=norm[:], in_=enc_sq_all[:], axis=ALONG_FREE, op=ALU.add)
-            if q == 20:
-                nc.vector.tensor_scalar_add(out=norm_eps[:], in0=norm[:], scalar1=1e-12)
-            if q == 21:
-                nc.vector.reciprocal(out=inv_norm[:], in_=norm_eps[:])
-            if q == 22:
-                nc.vector.tensor_tensor(out=gain[:], in0=norm[:], in1=inv_norm[:], op=ALU.mult)
-                nc.vector.tensor_scalar_mul(out=right_scale[:], in0=inv_norm[:], scalar1=-0.125)
-                nc.vector.tensor_scalar_mul(out=left_scale[:], in0=inv_norm[:], scalar1=0.125)
-            if q == 23:
-                nc.vector.tensor_scalar(
-                    out=u_gain[:], in0=u_bf[:], scalar1=gain[0:GROUPS, 0:1], scalar2=None, op0=ALU.mult
-                )
-            quarter(q)
-            if q == last_place[GROUPS - 2] // 2 + LAG_SUM + MAIN:
-                cells(sums[0:GROUPS, :], slice(0, 2), result)
-                nc.sync.dma_start(
-                    out=out.rearrange("(g h) i -> g h i", h=2)[0 : GROUPS - 1, :, :], in_=result[0 : GROUPS - 1, :, :]
-                )
-        sum_weighted(GROUPS - 1)
-        sum_direct(GROUPS * CHUNKS - 1)
         by_group = out.rearrange("(g h) i -> g h i", h=2)
-        for h in range(2):
-            cells(last_sums[h][0:GROUPS, :], slice(h, h + 1), last_result)
-        nc.sync.dma_start(out=by_group[GROUPS - 1 : GROUPS, :, :], in_=last_result[GROUPS - 1 : GROUPS, :, 0:CELLS])
+        norm_bank = {}
+
+        def prepare(step):
+            if step == 0:
+                nc.vector.tensor_tensor(out=enc_sq[:], in0=enc_cols, in1=enc_cols, op=ALU.mult)
+            if step == 1:
+                nc.vector.tensor_reduce(out=enc_sq_sum[:], in_=enc_sq[:], axis=ALONG_FREE, op=ALU.add)
+            if step == 4:
+                norm_bank[0] = psum.tile([P, P], F32, tag="product", name="enc_sq_all", bufs=PRODUCT_BANKS)
+                nc.tensor.matmul(
+                    out=norm_bank[0][:], lhsT=enc_sq_sum[:, 0:1].to_broadcast([P, P]), rhs=ident[:], start=True, stop=True
+                )
+            if step == 5:
+                nc.vector.tensor_reduce(out=norm[:], in_=norm_bank[0][:], axis=ALONG_FREE, op=ALU.add)
+            if step == 6:
+                nc.vector.tensor_scalar_add(out=norm_eps[:], in0=norm[:], scalar1=1e-12)
+            if step == 7:
+                nc.vector.reciprocal(out=inv_norm[:], in_=norm_eps[:])
+            if step == 8:
+                nc.vector.tensor_scalar_mul(out=scale[:], in0=inv_norm[:], scalar1=0.125)
+            if step == 9:
+                nc.vector.tensor_scalar(
+                    out=u_gain[:, :, 0:CELLS],
+                    in0=u_bf[:],
+                    scalar1=norm[0:GROUPS, 0:1],
+                    scalar2=inv_norm[0:GROUPS, 0:1],
+                    op0=ALU.mult,
+                    op1=ALU.mult,
+                )
+
+        def cells_right(w, h, a, n, to):
+            hs = slice(0, 2) if h is None else slice(h, h + 1)
+            nc.vector.scalar_tensor_tensor(
+                out=to[:, hs, a : a + n],
+                in0=w.rearrange("g (h i) -> g h i", h=hs.stop - hs.start)[:, :, 1 : n + 1],
+                scalar=scale[0:GROUPS, 0:1],
+                in1=u_gain[:, hs, a : a + n],
+                op0=ALU.mult,
+                op1=ALU.subtract,
+            )
+
+        def cells_left(w, h, a, n, right, to):
+            hs = slice(0, 2) if h is None else slice(h, h + 1)
+            nc.vector.scalar_tensor_tensor(
+                out=to[:, hs, a : a + n],
+                in0=w.rearrange("g (h i) -> g h i", h=hs.stop - hs.start)[:, :, 0:n],
+                scalar=scale[0:GROUPS, 0:1],
+                in1=right[:, hs, a : a + n],
+                op0=ALU.mult,
+                op1=ALU.subtract,
+            )
+
+        right = keep.tile([GROUPS, 2, CELLS], F32, name="right")
+        last_right = keep.tile([GROUPS, 2, FACES], F32, name="last_right")
+        end = (len(order) + 1) // 2 + LAG_WEIGH
+        for q in range(Q0, end):
+            prepare(q - NORM_Q)
+            quarter(q)
+        for i in range(2 * (end - LAG_SUM_DIRECT), len(order)):
+            sum_direct(i)
+        for i in range(2 * (end - DH_LAG), len(order)):
+            sum_half_direct(i)
+        sum_weighted(LAST)
+
+        todo = []
+        for a, n in pieces:
+            h, first = divmod(a, FACES)
+            if PIECES == 1:
+                for h in range(2):
+                    todo.append((last_sums[a][0:GROUPS, h * FACES : (h + 1) * FACES], h, 0, CELLS))
+            else:
+                todo.append((last_sums[a][0:GROUPS, 0 : n], h, first, n - 1))
+        rights = [lambda p=p: cells_right(*p, last_right) for p in todo]
+        lefts = [lambda p=p: cells_left(*p, last_right, last_result) for p in todo]
+        cells_right(sums[0:GROUPS, :], None, 0, CELLS, right)
+        if CORD == 0:
+            rights[0]()
+        cells_left(sums[0:GROUPS, :], None, 0, CELLS, right, result)
+        nc.sync.dma_start(out=by_group[0:LAST, :, :], in_=result[0:LAST, :, :])
+        if CORD == 1:
+            rights[0]()
+        for f in rights[1:] + lefts:
+            f()
+        assert sorted(covered) == sorted([(o, h) for o in order for h in range(2)])
+        assert sorted(summed) == [(s, h) for s in range(GROUPS) for h in range(2)]
+        nc.sync.dma_start(out=by_group[LAST:GROUPS, :, :], in_=last_result[LAST:GROUPS, :, 0:CELLS])

@@ -59,13 +59,15 @@ FPOS = 0
 Q0 = 8
 TANH_BUFS = 12
 NORM_Q = 14
-E0_SPLIT = 0
 CELL_Q = 0
 HS2 = 0
 HF = 0
 HV = 0
-EARLY = 4
-E1_FIRST = 0
+LOADS = ["0", "w2", "s2", "1", "2", "3", "w3", "s3", "4", "5", "6", "7", "8", "9", "10", "11", "12", "13", "14", "15"]
+C1S = 0
+WARM0 = 4
+WARM1 = 4
+WARM2 = 1
 CORD = 0
 
 FLOPS = 2 * GRIDS * FACES * HID * (HID + LATENT)
@@ -102,8 +104,10 @@ def tile_fluxgnn1dlatent_pb_t_kernel(
         u_bf = keep.tile([GROUPS, 2, CELLS], BF16, name="u_bf")
         warm = keep.tile([P, 1], F32, name="warm")
         warm_out = keep.tile([P, 1], F32, name="warm_out")
+        noise = keep.tile([P, GROUP], BF16, name="noise")
         sums = psum.tile([P, GROUP], F32, tag="sums", bufs=1)
 
+        nc.vector.memset(noise[:], 0.0)
         nc.vector.memset(w2_raw_plane[:].bitcast(I32), 0)
         nc.vector.memset(warm[:], 0.0)
         nc.vector.memset(rows_bf[:], 0.0)
@@ -120,11 +124,13 @@ def tile_fluxgnn1dlatent_pb_t_kernel(
                 in_=tokens[b * FACES : (b + 1) * FACES, :].rearrange("(n p) k -> p n k", p=P),
             )
 
-        def load_weight(words_tile, plane_tile, words, scales):
+        def load_words(words_tile, words):
             nc.sync.dma_start(
                 out=words_tile[:].bitcast(I32),
                 in_=words[0].rearrange("p n t -> p (n t)").bitcast(I32),
             )
+
+        def load_plane(plane_tile, scales):
             for quad in range(4):
                 nc.sync.dma_start(
                     out=plane_tile[32 * quad : 32 * quad + 4, :].bitcast(I32),
@@ -137,23 +143,17 @@ def tile_fluxgnn1dlatent_pb_t_kernel(
             out=rows_bf[CHUNKS : 2 * CHUNKS, :], in_=b3.rearrange("(j p) -> j p", p=P)
         )
         nc.scalar.dma_start(out=u_bf[:], in_=u.rearrange("(g h) i -> g h i", h=2))
-        if E0_SPLIT:
-            for n in range(2):
-                nc.sync.dma_start(out=e_in[0][:, n, :], in_=tokens[n * P : (n + 1) * P, :])
-        else:
-            load_grid(0)
-        if E1_FIRST == 1:
-            load_grid(1)
-        load_weight(w2_raw_words, w2_raw_plane, W2_words, W2_scales)
-        if E1_FIRST == 0:
-            load_grid(1)
-        load_grid(2)
-        load_grid(3)
-        for b in range(4, EARLY):
-            load_grid(b)
-        load_weight(w3_words, w3_plane, W3_words, W3_scales)
-        for b in range(EARLY, GRIDS):
-            load_grid(b)
+        for what in LOADS:
+            if what == "w2":
+                load_words(w2_raw_words, W2_words)
+            elif what == "s2":
+                load_plane(w2_raw_plane, W2_scales)
+            elif what == "w3":
+                load_words(w3_words, W3_words)
+            elif what == "s3":
+                load_plane(w3_plane, W3_scales)
+            else:
+                load_grid(int(what))
 
         nc.scalar.activation(out=warm_out[:], in_=warm[:], func=ACT.Gelu)
 
@@ -172,6 +172,12 @@ def tile_fluxgnn1dlatent_pb_t_kernel(
         product1, x_raw = {}, {}
         x_grouped, x_codes, x_plane = {}, {}, {}
         product2, tanh, weighted, last_sums = {}, {}, {}, {}
+
+        def stir(n):
+            if n > 0:
+                bank = psum.tile([P, GROUP], F32, tag="product", name="stirred", bufs=PRODUCT_BANKS)
+                for i in range(n):
+                    nc.tensor.matmul(out=bank[:], lhsT=noise[:, 0:P], rhs=noise[:], start=True, stop=True)
 
         def flip_edge_hid(b):
             if 0 <= b < GRIDS:
@@ -414,11 +420,14 @@ def tile_fluxgnn1dlatent_pb_t_kernel(
             weigh(2 * (q - LAG_WEIGH) + 1)
 
         halves = [slice(0, FACES), slice(FACES, GROUP)]
+        stir(WARM0)
         flip_edge_hid(0)
         copy_edge_hid(0, nc.scalar.copy)
+        stir(WARM1)
         flip_edge_hid(1)
-        copy_edge_hid(1, nc.scalar.copy)
+        stir(WARM2)
         quantise_edge_hid(0, halves[0])
+        copy_edge_hid(1, nc.scalar.copy if C1S else nc.vector.tensor_copy)
         if HF == 1:
             flip_edge_hid(2)
         for t in range(PACK):

@@ -24,51 +24,25 @@ GROUP = 2 * FACES
 GROUPS = GRIDS // 2
 LAST = GROUPS - 1
 CHUNKS = LATENT // P
+BLOCKS = GROUP // P
+ROWS = 2 * GRIDS
 
 FLIP_BANKS = 2
 PRODUCT_BANKS = 5
 
-LAG_COPY = 1
-LAG_COPY_S = 1
-LAG_SUM_6 = 18
-TSPLIT = 0
-PIECES = 2
-LAG_QE = 3
-LAG_LAYER1 = 6
-LAG_GELU = 6
-INT_0 = 10
-INT_1 = 11
-LAG_QX = 12
-LAG_LAYER2 = 15
-LAG_TANH = 15
-LAG_WEIGH = 16
-LAG_SUM_DIRECT = 18
-LAG_SUM = 18
-STAGGER = 4
-S_SET = [5, 7, 9, 11, 13, 15]
-DIRECT = [(7, 3)]
-LATE = 1
-HALF_DIRECT = []
-SUM_GAP = 0
-DH_LAG = 19
-SPLIT = 2
-SPLIT_FROM = 4
-CPOS = 1
-TORD = 0
-FPOS = 0
-Q0 = 8
+SCALED = [4, 5, 6, 7]
+SCALED_LAST = [6, 7]
+RUN_A, RUN_B, REDUCE = 8, 9, 10
+RUN_6A, RUN_6B, REDUCE_6 = 31, 31, 32
+COPIED_BY_SCALAR = [5, 9, 13]
 TANH_BUFS = 12
-NORM_Q = 14
-CELL_Q = 0
-HS2 = 0
-HF = 0
-HV = 0
+SCALED_BUFS = 12
 LOADS = ["0", "w2", "s2", "1", "2", "3", "w3", "s3", "4", "5", "6", "7", "8", "9", "10", "11", "12", "13", "14", "15"]
-C1S = 0
 WARM0 = 4
 WARM1 = 4
 WARM2 = 1
-CORD = 0
+WARM_END = 3
+R6_POS = 0
 
 FLOPS = 2 * GRIDS * FACES * HID * (HID + LATENT)
 
@@ -96,16 +70,14 @@ def tile_fluxgnn1dlatent_pb_t_kernel(
         rows = keep.tile([P, P], F32, name="rows")
         cols = keep.tile([P, P], F32, name="cols")
         ident = keep.tile([P, P], F32, name="ident")
-        pick = keep.tile([P, 2 * P], F32, name="pick")
-        direct_chunks = sorted(set([j for s, j in DIRECT + HALF_DIRECT]))
-        pick_enc = keep.tile([P, (len(direct_chunks) + 1) * P], F32, name="pick_enc")
         b2_bf = keep.tile([P, PACK], BF16, name="b2_bf")
         b2_cols = keep.tile([P, PACK], F32, name="b2_cols")
-        u_bf = keep.tile([GROUPS, 2, CELLS], BF16, name="u_bf")
+        u_rows = keep.tile([ROWS, P], BF16, name="u_rows")
+        w_cols = keep.tile([P, P + GRIDS], F32, name="w_cols")
+        w_late = keep.tile([P, P + GRIDS], F32, name="w_late")
         warm = keep.tile([P, 1], F32, name="warm")
         warm_out = keep.tile([P, 1], F32, name="warm_out")
         noise = keep.tile([P, GROUP], BF16, name="noise")
-        sums = psum.tile([P, GROUP], F32, tag="sums", bufs=1)
 
         nc.vector.memset(noise[:], 0.0)
         nc.vector.memset(w2_raw_plane[:].bitcast(I32), 0)
@@ -113,10 +85,9 @@ def tile_fluxgnn1dlatent_pb_t_kernel(
         nc.vector.memset(rows_bf[:], 0.0)
         nc.vector.memset(w3_plane[:].bitcast(I32), 0)
         make_identity(nc, ident[:])
-        nc.vector.memset(pick[:], 0.0)
-        nc.vector.memset(pick[:, P : P + 1], 1.0)
-        if direct_chunks:
-            nc.vector.memset(pick_enc[:], 0.0)
+        nc.vector.memset(u_rows[:], 0.0)
+        nc.vector.memset(w_cols[:], 0.0)
+        nc.vector.memset(w_late[:], 0.0)
 
         def load_grid(b):
             nc.sync.dma_start(
@@ -142,7 +113,8 @@ def tile_fluxgnn1dlatent_pb_t_kernel(
         nc.scalar.dma_start(
             out=rows_bf[CHUNKS : 2 * CHUNKS, :], in_=b3.rearrange("(j p) -> j p", p=P)
         )
-        nc.scalar.dma_start(out=u_bf[:], in_=u.rearrange("(g h) i -> g h i", h=2))
+        nc.scalar.dma_start(out=u_rows[0:GRIDS, :], in_=u[:, 0:P])
+        nc.scalar.dma_start(out=u_rows[GRIDS:ROWS, 0 : CELLS - P], in_=u[:, P:CELLS])
         for what in LOADS:
             if what == "w2":
                 load_words(w2_raw_words, W2_words)
@@ -171,7 +143,7 @@ def tile_fluxgnn1dlatent_pb_t_kernel(
         e_bank, e_grouped, e_codes, e_plane = {}, {}, {}, {}
         product1, x_raw = {}, {}
         x_grouped, x_codes, x_plane = {}, {}, {}
-        product2, tanh, weighted, last_sums = {}, {}, {}, {}
+        product2, tanh, weighted, scaled, acc = {}, {}, {}, {}, {}
 
         def stir(n):
             if n > 0:
@@ -252,172 +224,144 @@ def tile_fluxgnn1dlatent_pb_t_kernel(
                 )
 
         whole = slice(0, GROUP)
-        streams = [(g, whole) for g in range(LAST)]
-        for h in range(LATE):
-            streams.append((LAST, slice(h * GROUP // LATE, (h + 1) * GROUP // LATE)))
-        order = sorted(
-            [(s, j) for s in range(len(streams)) for j in range(CHUNKS)],
-            key=lambda job: (STAGGER * job[0] + job[1], job[0]),
+
+        jobs = sorted(
+            [(g, j) for g in range(GROUPS) for j in range(CHUNKS)],
+            key=lambda job: (CHUNKS // 2 * job[0] + job[1], job[0]),
         )
-        last_place = [order.index((s, CHUNKS - 1)) for s in range(len(streams))]
+        slots = [jobs[i : i + 2] for i in range(0, len(jobs), 2)]
+        covered = []
 
-        covered, summed = [], []
+        def layer2_product(n):
+            if 0 <= n < len(slots):
+                for g, j in slots[n]:
+                    product2[g, j] = psum.tile([P, GROUP], F32, tag="product", name="product2", bufs=PRODUCT_BANKS)
+                    nc.tensor.matmul_mx(
+                        out=product2[g, j][:],
+                        lhsT=w3_words[:, j * P : (j + 1) * P].bitcast(FP8X4),
+                        lhsT_scale=w3_plane[:, j * P : (j + 1) * P],
+                        rhs=x_codes[g][:].bitcast(FP8X4),
+                        rhs_scale=x_plane[g][:],
+                        start=True,
+                        stop=True,
+                    )
 
-        def layer2_product(i):
-            if 0 <= i < len(order):
-                s, j = order[i]
-                g, c = streams[s]
-                product2[i] = psum.tile([P, c.stop - c.start], F32, tag="product", name="product2", bufs=PRODUCT_BANKS)
-                nc.tensor.matmul_mx(
-                    out=product2[i][:],
-                    lhsT=w3_words[:, j * P : (j + 1) * P].bitcast(FP8X4),
-                    lhsT_scale=w3_plane[:, j * P : (j + 1) * P],
-                    rhs=x_codes[g][:, c].bitcast(FP8X4),
-                    rhs_scale=x_plane[g][:, c],
-                    start=True,
-                    stop=True,
-                )
-
-        def tanh_of(i):
-            if 0 <= i < len(order):
-                s, j = order[i]
-                g, c = streams[s]
-                tanh[i] = work.tile([P, c.stop - c.start], F32, tag="tanh", name="tanh", bufs=TANH_BUFS)
-                n = c.stop - c.start
-                parts = 2 if TSPLIT and i == len(order) - 1 else 1
-                for a in range(parts):
-                    part = slice(a * n // parts, (a + 1) * n // parts)
+        def tanh_of(n):
+            if 0 <= n < len(slots):
+                for g, j in slots[n]:
+                    tanh[g, j] = work.tile([P, GROUP], F32, tag="tanh", name="tanh", bufs=TANH_BUFS)
                     nc.scalar.activation(
-                        out=tanh[i][:, part], in_=product2[i][:, part], func=ACT.Tanh, bias=b3_cols[:, j : j + 1]
+                        out=tanh[g, j][:], in_=product2[g, j][:], func=ACT.Tanh, bias=b3_cols[:, j : j + 1]
                     )
 
-        def weigh(i):
-            if 0 <= i < len(order) and order[i] not in DIRECT:
-                covered.append((order[i], 0))
-                if order[i] not in HALF_DIRECT:
-                    covered.append((order[i], 1))
-                s, j = order[i]
-                g, c = streams[s]
-                if s not in weighted:
-                    weighted[s] = work.tile([P, c.stop - c.start], F32, tag="weighted", name="weighted", bufs=4)
-                    nc.vector.tensor_scalar(
-                        out=weighted[s][:], in0=tanh[i][:], scalar1=enc_cols[:, j : j + 1], scalar2=None, op0=ALU.mult
-                    )
-                else:
-                    n = c.stop - c.start
-                    parts = SPLIT if s >= LAST and j >= SPLIT_FROM else 1
-                    if order[i] in HALF_DIRECT:
-                        n, parts = n // 2, 1
+        def scaled_chunks(g):
+            return SCALED_LAST if g == LAST else SCALED
+
+        def weigh(n, k):
+            if 0 <= n < len(slots):
+                g, j = slots[n][k]
+                covered.append((g, j))
+                if j in scaled_chunks(g):
+                    scaled[g, j] = work.tile([P, GROUP], F32, tag="scaled", name="scaled", bufs=SCALED_BUFS)
+                    parts = 2 if (g, j) == slots[-1][-1] else 1
                     for a in range(parts):
-                        part = slice(a * n // parts, (a + 1) * n // parts)
-                        nc.vector.scalar_tensor_tensor(
-                            out=weighted[s][:, part],
-                            in0=tanh[i][:, part],
-                            scalar=enc_cols[:, j : j + 1],
-                            in1=weighted[s][:, part],
+                        part = slice(a * GROUP // parts, (a + 1) * GROUP // parts)
+                        nc.vector.tensor_scalar(
+                            out=scaled[g, j][:, part],
+                            in0=tanh[g, j][:, part],
+                            scalar1=enc_cols[:, j : j + 1],
+                            scalar2=None,
                             op0=ALU.mult,
-                            op1=ALU.add,
                         )
-
-        opened = []
-        pieces = [(0, GROUP)] if PIECES == 1 else [(0, FACES), (FACES, FACES)]
-
-        def add_to_sums(s, lhsT, rhs, final, cols_of=slice(0, GROUP)):
-            g, c = streams[s]
-            if s < LAST:
-                nc.tensor.matmul(out=sums[:, cols_of], lhsT=lhsT, rhs=rhs[:, cols_of], start=(0 not in opened), stop=final and s == LAST - 1)
-                opened.append(0)
-            else:
-                for a, n in pieces:
-                    fresh = a not in last_sums
-                    if fresh and a < GROUP - P:
-                        last_sums[a] = psum.tile([P, n], F32, tag="flip", name="last_sums", bufs=FLIP_BANKS)
-                    elif fresh:
-                        last_sums[a] = psum.tile([P, n], F32, tag="product", name="last_sums", bufs=PRODUCT_BANKS)
-                    nc.tensor.matmul(out=last_sums[a][:], lhsT=lhsT, rhs=rhs[:, a : a + n], start=fresh, stop=final)
-
-        def sum_direct(i):
-            if 0 <= i < len(order) and order[i] in DIRECT:
-                covered.extend([(order[i], 0), (order[i], 1)])
-                s, j = order[i]
-                g, c = streams[s]
-                n = direct_chunks.index(j) + 1
-                add_to_sums(s, pick_enc[:, n * P - g : (n + 1) * P - g], tanh[i][:], False)
-
-        def sum_half_direct(i):
-            if 0 <= i < len(order) and order[i] in HALF_DIRECT:
-                covered.append((order[i], 1))
-                s, j = order[i]
-                g, c = streams[s]
-                n = direct_chunks.index(j) + 1
-                add_to_sums(s, pick_enc[:, n * P - g : (n + 1) * P - g], tanh[i][:], False, slice(FACES, GROUP))
-
-        def sum_weighted(s, h=None):
-            g, c = streams[s]
-            summed.extend([(s, 0), (s, 1)] if h is None else [(s, h)])
-            if h is None:
-                add_to_sums(s, pick[:, P - g : 2 * P - g], weighted[s][:], True)
-            else:
-                add_to_sums(s, pick[:, P - g : 2 * P - g], weighted[s][:], h == 1, slice(h * FACES, (h + 1) * FACES))
-
-        def quarter(q):
-            def group_of(lag):
-                return (q - lag) // 4 if (q - lag) % 4 == 0 and q - lag > 3 else -1
-
-            if TORD == 1:
-                flip_edge_hid(2 * group_of(0))
-                flip_edge_hid(2 * group_of(FPOS) + 1)
-            if q - LAG_LAYER1 >= PACK:
-                layer1_product((q - LAG_LAYER1) // PACK, (q - LAG_LAYER1) % PACK, whole)
-            layer2_product(2 * (q - LAG_LAYER2))
-            layer2_product(2 * (q - LAG_LAYER2) + 1)
-            if TORD == 0:
-                flip_edge_hid(2 * group_of(0))
-                flip_edge_hid(2 * group_of(FPOS) + 1)
-            sum_direct(2 * (q - LAG_SUM_DIRECT))
-            sum_direct(2 * (q - LAG_SUM_DIRECT) + 1)
-            for s in range(LAST):
-                if s == LAST - 1:
-                    if last_place[s] // 2 == q - LAG_SUM_6:
-                        sum_weighted(s)
-                elif SUM_GAP == 0 or s == 0:
-                    if last_place[s] // 2 == q - LAG_SUM:
-                        sum_weighted(s)
+                elif g not in weighted:
+                    weighted[g] = work.tile([P, GROUP], F32, tag="weighted", name="weighted", bufs=5)
+                    nc.vector.tensor_scalar(
+                        out=weighted[g][:], in0=tanh[g, j][:], scalar1=enc_cols[:, j : j + 1], scalar2=None, op0=ALU.mult
+                    )
                 else:
-                    if last_place[s] // 2 == q - LAG_SUM:
-                        sum_weighted(s, 0)
-                    if last_place[s] // 2 == q - LAG_SUM - SUM_GAP:
-                        sum_weighted(s, 1)
-            sum_half_direct(2 * (q - DH_LAG))
-            sum_half_direct(2 * (q - DH_LAG) + 1)
+                    nc.vector.scalar_tensor_tensor(
+                        out=weighted[g][:],
+                        in0=tanh[g, j][:],
+                        scalar=enc_cols[:, j : j + 1],
+                        in1=weighted[g][:],
+                        op0=ALU.mult,
+                        op1=ALU.add,
+                    )
 
-            copies = [2 * group_of(LAG_COPY), 2 * group_of(LAG_COPY + FPOS) + 1]
-            copies_s = [2 * group_of(LAG_COPY_S), 2 * group_of(LAG_COPY_S + FPOS) + 1]
-            if CPOS == 1:
-                for b in copies_s:
-                    if b in S_SET:
-                        copy_edge_hid(b, nc.scalar.copy)
-            if q - LAG_GELU >= PACK:
-                gelu((q - LAG_GELU) // PACK, (q - LAG_GELU) % PACK, whole)
-            tanh_of(2 * (q - LAG_TANH))
-            tanh_of(2 * (q - LAG_TANH) + 1)
-            if CPOS == 0:
-                for b in copies_s:
-                    if b in S_SET:
-                        copy_edge_hid(b, nc.scalar.copy)
+        def add_transposed(bank, terms, blocks):
+            for a in blocks:
+                for i in range(len(terms)):
+                    nc.tensor.matmul(
+                        out=bank[:, a, :],
+                        lhsT=terms[i][:, a * P : (a + 1) * P],
+                        rhs=ident[:],
+                        is_transpose=True,
+                        start=(i == 0),
+                        stop=(i == len(terms) - 1),
+                    )
+
+        def add_group(g, blocks, chunks=SCALED):
+            if g not in acc:
+                acc[g] = psum.tile([P, BLOCKS, P], F32, tag="sums", name="acc", bufs=1)
+            add_transposed(acc[g], [weighted[g]] + [scaled[g, j] for j in chunks], blocks)
+
+        def reduce_channels(g, bank, cols, h0=0, h1=2):
+            nc.vector.tensor_reduce(
+                out=cols[:, 0:ROWS].rearrange("p (f b) -> p b f", f=2)[:, 2 * g + h0 : 2 * g + h1, :],
+                in_=bank[:].rearrange("p (h f) c -> p h f c", f=2)[:, h0:h1, :, :],
+                axis=ALONG_FREE,
+                op=ALU.add,
+            )
+
+        AT_FLIP, AT_COPY, AT_QE, AT_LAYER1, AT_INT, AT_QX = -15, -14, -12, -9, -5, -3
+
+        def slot(n):
+            def group_at(offset):
+                m = n - offset
+                return m // 4 if m % 4 == 0 else -1
+
+            def group_from(offset, first):
+                g = group_at(offset)
+                return g if g >= first else -1
+
+            m = n - AT_LAYER1
+            if m >= PACK:
+                layer1_product(m // PACK, m % PACK, whole)
+            layer2_product(n)
+            flip_edge_hid(2 * group_from(AT_FLIP, 2))
+            if group_from(AT_FLIP, 2) > 0:
+                flip_edge_hid(2 * group_from(AT_FLIP, 2) + 1)
+            for g in range(LAST):
+                if n == (RUN_6A if g == LAST - 1 else 4 * g + RUN_A):
+                    add_group(g, [0, 1])
+                if n == (RUN_6B if g == LAST - 1 else 4 * g + RUN_B):
+                    add_group(g, [2, 3])
+
+            g = group_from(AT_COPY, 2)
+            copies = [2 * g, 2 * g + 1] if g > 0 else []
+            for b in copies:
+                if b in COPIED_BY_SCALAR:
+                    copy_edge_hid(b, nc.scalar.copy)
+            if m >= PACK:
+                gelu(m // PACK, m % PACK, whole)
+            tanh_of(n)
 
             for b in copies:
-                if b not in S_SET:
+                if b not in COPIED_BY_SCALAR:
                     copy_edge_hid(b, nc.vector.tensor_copy)
-            if q >= INT_0:
-                interleave(2 * ((q - INT_0) // 4) if (q - INT_0) % 4 == 0 else -1)
-            if q >= INT_1:
-                interleave(2 * ((q - INT_1) // 4) + 1 if (q - INT_1) % 4 == 0 else -1)
-            weigh(2 * (q - LAG_WEIGH))
-            quantise_edge_hid(group_of(LAG_QE), whole)
-            if q >= LAG_QX and (q - LAG_QX) % 4 == 0:
-                quantise_x((q - LAG_QX) // 4)
-            weigh(2 * (q - LAG_WEIGH) + 1)
+            for g in range(LAST):
+                if n == (REDUCE_6 if g == LAST - 1 else 4 * g + REDUCE):
+                    reduce_channels(g, acc[g], w_cols)
+            if group_at(AT_INT) >= 0:
+                interleave(2 * group_at(AT_INT))
+            if group_at(AT_INT + 1) >= 0:
+                interleave(2 * group_at(AT_INT + 1) + 1)
+            weigh(n - 1, 0)
+            if group_from(AT_QE, 2) > 0:
+                quantise_edge_hid(group_from(AT_QE, 2), whole)
+            if group_at(AT_QX) >= 0:
+                quantise_x(group_at(AT_QX))
+            weigh(n - 1, 1)
 
         halves = [slice(0, FACES), slice(FACES, GROUP)]
         stir(WARM0)
@@ -427,19 +371,13 @@ def tile_fluxgnn1dlatent_pb_t_kernel(
         flip_edge_hid(1)
         stir(WARM2)
         quantise_edge_hid(0, halves[0])
-        copy_edge_hid(1, nc.scalar.copy if C1S else nc.vector.tensor_copy)
-        if HF == 1:
-            flip_edge_hid(2)
+        copy_edge_hid(1, nc.vector.tensor_copy)
         for t in range(PACK):
             layer1_product(0, t, halves[0])
             gelu(0, t, halves[0])
-        if HF == 0:
-            flip_edge_hid(2)
-        if HV == 0:
-            quantise_edge_hid(0, halves[1])
-        copy_edge_hid(2, nc.scalar.copy if HS2 else nc.vector.tensor_copy)
-        if HV == 1:
-            quantise_edge_hid(0, halves[1])
+        flip_edge_hid(2)
+        quantise_edge_hid(0, halves[1])
+        copy_edge_hid(2, nc.vector.tensor_copy)
         flip_edge_hid(3)
         copy_edge_hid(3, nc.vector.tensor_copy)
         for t in range(PACK):
@@ -451,8 +389,6 @@ def tile_fluxgnn1dlatent_pb_t_kernel(
         nc.vector.tensor_copy(out=cols[:], in_=cols_ps[:])
         enc_cols = cols[:, 0:CHUNKS]
         b3_cols = cols[:, CHUNKS : 2 * CHUNKS]
-        for n, j in enumerate(direct_chunks):
-            nc.vector.tensor_copy(out=pick_enc[:, (n + 1) * P : (n + 1) * P + 1], in_=enc_cols[:, j : j + 1])
 
         enc_sq = keep.tile([P, CHUNKS], F32, name="enc_sq")
         enc_sq_sum = keep.tile([P, 1], F32, name="enc_sq_sum")
@@ -460,93 +396,83 @@ def tile_fluxgnn1dlatent_pb_t_kernel(
         norm_eps = keep.tile([P, 1], F32, name="norm_eps")
         inv_norm = keep.tile([P, 1], F32, name="inv_norm")
         scale = keep.tile([P, 1], F32, name="scale")
-        u_gain = keep.tile([GROUPS, 2, FACES], F32, name="u_gain")
-        result = keep.tile([GROUPS, 2, CELLS], F32, name="result")
-        last_result = keep.tile([GROUPS, 2, FACES], F32, name="last_result")
-        by_group = out.rearrange("(g h) i -> g h i", h=2)
+        u_gain = keep.tile([ROWS, P], F32, name="u_gain")
+        right = keep.tile([ROWS, P], F32, name="right")
+        result = keep.tile([ROWS, P], F32, name="result")
         norm_bank = {}
 
-        def prepare(step):
-            if step == 0:
+        def prepare(step_number):
+            if step_number == 0:
                 nc.vector.tensor_tensor(out=enc_sq[:], in0=enc_cols, in1=enc_cols, op=ALU.mult)
-            if step == 1:
+            if step_number == 1:
                 nc.vector.tensor_reduce(out=enc_sq_sum[:], in_=enc_sq[:], axis=ALONG_FREE, op=ALU.add)
-            if step == 4:
+            if step_number == 4:
                 norm_bank[0] = psum.tile([P, P], F32, tag="product", name="enc_sq_all", bufs=PRODUCT_BANKS)
                 nc.tensor.matmul(
                     out=norm_bank[0][:], lhsT=enc_sq_sum[:, 0:1].to_broadcast([P, P]), rhs=ident[:], start=True, stop=True
                 )
-            if step == 5:
+            if step_number == 5:
                 nc.vector.tensor_reduce(out=norm[:], in_=norm_bank[0][:], axis=ALONG_FREE, op=ALU.add)
-            if step == 6:
+            if step_number == 6:
                 nc.vector.tensor_scalar_add(out=norm_eps[:], in0=norm[:], scalar1=1e-12)
-            if step == 7:
+            if step_number == 7:
                 nc.vector.reciprocal(out=inv_norm[:], in_=norm_eps[:])
-            if step == 8:
+            if step_number == 8:
                 nc.vector.tensor_scalar_mul(out=scale[:], in0=inv_norm[:], scalar1=0.125)
-            if step == 9:
+            if step_number == 9:
                 nc.vector.tensor_scalar(
-                    out=u_gain[:, :, 0:CELLS],
-                    in0=u_bf[:],
-                    scalar1=norm[0:GROUPS, 0:1],
-                    scalar2=inv_norm[0:GROUPS, 0:1],
+                    out=u_gain[:],
+                    in0=u_rows[:],
+                    scalar1=norm[0:ROWS, 0:1],
+                    scalar2=inv_norm[0:ROWS, 0:1],
                     op0=ALU.mult,
                     op1=ALU.mult,
                 )
 
-        def cells_right(w, h, a, n, to):
-            hs = slice(0, 2) if h is None else slice(h, h + 1)
+        for n in range(-7, len(slots) + 1):
+            prepare(n + 1)
+            slot(n)
+        assert sorted(covered) == [(g, j) for g in range(GROUPS) for j in range(CHUNKS)]
+
+        early_bank = psum.tile([P, BLOCKS, P], F32, tag="flip", name="early_bank", bufs=FLIP_BANKS)
+        late_bank = psum.tile([P, BLOCKS, P], F32, tag="flip", name="late_bank", bufs=FLIP_BANKS)
+        stir(WARM_END)
+        add_transposed(early_bank, [weighted[LAST]], range(BLOCKS))
+        reduce_channels(LAST, early_bank, w_cols)
+        add_transposed(late_bank, [scaled[LAST, j] for j in SCALED_LAST], range(BLOCKS))
+        reduce_channels(LAST, late_bank, w_late, 0, 1)
+        reduce_channels(LAST, late_bank, w_late, 1, 2)
+        faces = psum.tile([P, 2, P], F32, tag="product", name="faces", bufs=PRODUCT_BANKS)
+        for k in range(2):
+            for cols_of, first in ((w_cols, True), (w_late, False)):
+                nc.tensor.matmul(
+                    out=faces[:, k, :],
+                    lhsT=cols_of[:, k * GRIDS : k * GRIDS + P],
+                    rhs=ident[:],
+                    is_transpose=True,
+                    start=first,
+                    stop=not first,
+                )
+        row = faces[0:ROWS, :, :].rearrange("r k i -> r (k i)")
+        for a in range(2):
+            part = slice(a * P // 2, (a + 1) * P // 2)
             nc.vector.scalar_tensor_tensor(
-                out=to[:, hs, a : a + n],
-                in0=w.rearrange("g (h i) -> g h i", h=hs.stop - hs.start)[:, :, 1 : n + 1],
-                scalar=scale[0:GROUPS, 0:1],
-                in1=u_gain[:, hs, a : a + n],
+                out=right[:, part],
+                in0=row[:, part.start + 1 : part.stop + 1],
+                scalar=scale[0:ROWS, 0:1],
+                in1=u_gain[:, part],
                 op0=ALU.mult,
                 op1=ALU.subtract,
             )
-
-        def cells_left(w, h, a, n, right, to):
-            hs = slice(0, 2) if h is None else slice(h, h + 1)
+        for a in range(2):
+            part = slice(a * P // 2, (a + 1) * P // 2)
             nc.vector.scalar_tensor_tensor(
-                out=to[:, hs, a : a + n],
-                in0=w.rearrange("g (h i) -> g h i", h=hs.stop - hs.start)[:, :, 0:n],
-                scalar=scale[0:GROUPS, 0:1],
-                in1=right[:, hs, a : a + n],
+                out=result[:, part],
+                in0=row[:, part],
+                scalar=scale[0:ROWS, 0:1],
+                in1=right[:, part],
                 op0=ALU.mult,
                 op1=ALU.subtract,
             )
-
-        right = keep.tile([GROUPS, 2, CELLS], F32, name="right")
-        last_right = keep.tile([GROUPS, 2, FACES], F32, name="last_right")
-        end = (len(order) + 1) // 2 + LAG_WEIGH
-        for q in range(Q0, end):
-            prepare(q - NORM_Q)
-            quarter(q)
-        for i in range(2 * (end - LAG_SUM_DIRECT), len(order)):
-            sum_direct(i)
-        for i in range(2 * (end - DH_LAG), len(order)):
-            sum_half_direct(i)
-        sum_weighted(LAST)
-
-        todo = []
-        for a, n in pieces:
-            h, first = divmod(a, FACES)
-            if PIECES == 1:
-                for h in range(2):
-                    todo.append((last_sums[a][0:GROUPS, h * FACES : (h + 1) * FACES], h, 0, CELLS))
-            else:
-                todo.append((last_sums[a][0:GROUPS, 0 : n], h, first, n - 1))
-        rights = [lambda p=p: cells_right(*p, last_right) for p in todo]
-        lefts = [lambda p=p: cells_left(*p, last_right, last_result) for p in todo]
-        cells_right(sums[0:GROUPS, :], None, 0, CELLS, right)
-        if CORD == 0:
-            rights[0]()
-        cells_left(sums[0:GROUPS, :], None, 0, CELLS, right, result)
-        nc.sync.dma_start(out=by_group[0:LAST, :, :], in_=result[0:LAST, :, :])
-        if CORD == 1:
-            rights[0]()
-        for f in rights[1:] + lefts:
-            f()
-        assert sorted(covered) == sorted([(o, h) for o in order for h in range(2)])
-        assert sorted(summed) == [(s, h) for s in range(GROUPS) for h in range(2)]
-        nc.sync.dma_start(out=by_group[LAST:GROUPS, :, :], in_=last_result[LAST:GROUPS, :, 0:CELLS])
+        nc.sync.dma_start(out=out[:, 0:P], in_=result[0:GRIDS, :])
+        nc.scalar.dma_start(out=out[:, P:CELLS], in_=result[GRIDS:ROWS, 0 : CELLS - P])

@@ -32,16 +32,26 @@ PRODUCT_BANKS = 5
 
 SCALED = [4, 5, 6, 7]
 SCALED_LAST = [6, 7]
-RUN_A, RUN_B, REDUCE = 8, 9, 10
-RUN_6A, RUN_6B, REDUCE_6 = 31, 31, 32
-COPIED_BY_SCALAR = [5, 9, 13]
+REDUCE = 10
+RUN_6A, REDUCE_6 = 31, 32
+COPIED_BY_SCALAR = [5]
 TANH_BUFS = 12
-SCALED_BUFS = 12
-LOADS = ["0", "w2", "s2", "1", "2", "3", "w3", "s3", "4", "5", "6", "7", "8", "9", "10", "11", "12", "13", "14", "15"]
+SCALED_BUFS = 16
+SC = [4, 5, 6, 7]
+SC_LAST = [6, 7]
+FL_AFTER = 2
+ACT_6, LATE_6, N_LATE, ACT_7 = 0, 1, 2, 0
+SC_6 = [4, 5, 6, 7]
+FL_POS = 1
+RUNS = [(8, [0, 1]), (9, [2, 3])]
+CP_POS = 0
+BLOCK_TAG = ["flip", "flip", "product", "product"]
+HEAD = "w6 F0 A0 F1 w1 A1 R c Q0 B0 Q1 C B1 F2 p0 V2 F3 V3 p1 f2 s2 f3 Q2 B2 Q3 B3 v3 p4 q1 i0 p5"
+LOADS = ["b0", "b1", "w2", "s2", "bias", "1", "enc", "2", "3", "w3", "s3"] + [str(i) for i in range(4, 16)] + ["u"]
 WARM0 = 4
 WARM1 = 4
 WARM2 = 1
-WARM_END = 3
+WARM_END = 2
 R6_POS = 0
 
 FLOPS = 2 * GRIDS * FACES * HID * (HID + LATENT)
@@ -68,7 +78,7 @@ def tile_fluxgnn1dlatent_pb_t_kernel(
         w3_plane = keep.tile([P, LATENT], U8, name="w3_plane", align_bytes=64)
         rows_bf = keep.tile([P, P], BF16, name="rows_bf")
         rows = keep.tile([P, P], F32, name="rows")
-        cols = keep.tile([P, P], F32, name="cols")
+        cols = keep.tile([P, 2 * CHUNKS], F32, name="cols")
         ident = keep.tile([P, P], F32, name="ident")
         b2_bf = keep.tile([P, PACK], BF16, name="b2_bf")
         b2_cols = keep.tile([P, PACK], F32, name="b2_cols")
@@ -79,10 +89,10 @@ def tile_fluxgnn1dlatent_pb_t_kernel(
         warm_out = keep.tile([P, 1], F32, name="warm_out")
         noise = keep.tile([P, GROUP], BF16, name="noise")
 
-        nc.vector.memset(noise[:], 0.0)
         nc.vector.memset(w2_raw_plane[:].bitcast(I32), 0)
-        nc.vector.memset(warm[:], 0.0)
         nc.vector.memset(rows_bf[:], 0.0)
+        nc.vector.memset(warm[:], 0.0)
+        nc.vector.memset(noise[:], 0.0)
         nc.vector.memset(w3_plane[:].bitcast(I32), 0)
         make_identity(nc, ident[:])
         nc.vector.memset(u_rows[:], 0.0)
@@ -94,6 +104,9 @@ def tile_fluxgnn1dlatent_pb_t_kernel(
                 out=e_in[b][:],
                 in_=tokens[b * FACES : (b + 1) * FACES, :].rearrange("(n p) k -> p n k", p=P),
             )
+
+        def load_block(k, start):
+            start(out=e_in[k // 2][:, k % 2, :], in_=tokens[k * P : (k + 1) * P, :])
 
         def load_words(words_tile, words):
             nc.sync.dma_start(
@@ -108,13 +121,6 @@ def tile_fluxgnn1dlatent_pb_t_kernel(
                     in_=scales[0, 4 * quad : 4 * quad + 4, :].bitcast(I32),
                 )
 
-        nc.scalar.dma_start(out=b2_bf[:], in_=b2.rearrange("(p t) -> p t", t=PACK))
-        nc.scalar.dma_start(out=rows_bf[0:CHUNKS, :], in_=enc.rearrange("(j p) -> j p", p=P))
-        nc.scalar.dma_start(
-            out=rows_bf[CHUNKS : 2 * CHUNKS, :], in_=b3.rearrange("(j p) -> j p", p=P)
-        )
-        nc.scalar.dma_start(out=u_rows[0:GRIDS, :], in_=u[:, 0:P])
-        nc.scalar.dma_start(out=u_rows[GRIDS:ROWS, 0 : CELLS - P], in_=u[:, P:CELLS])
         for what in LOADS:
             if what == "w2":
                 load_words(w2_raw_words, W2_words)
@@ -124,21 +130,32 @@ def tile_fluxgnn1dlatent_pb_t_kernel(
                 load_words(w3_words, W3_words)
             elif what == "s3":
                 load_plane(w3_plane, W3_scales)
+            elif what == "bias":
+                nc.scalar.dma_start(out=b2_bf[:], in_=b2.rearrange("(p t) -> p t", t=PACK))
+            elif what == "enc":
+                nc.scalar.dma_start(out=rows_bf[0:CHUNKS, :], in_=enc.rearrange("(j p) -> j p", p=P))
+                nc.scalar.dma_start(
+                    out=rows_bf[CHUNKS : 2 * CHUNKS, :], in_=b3.rearrange("(j p) -> j p", p=P)
+                )
+            elif what == "u":
+                nc.sync.dma_start(out=u_rows[0:GRIDS, :], in_=u[:, 0:P])
+                nc.sync.dma_start(out=u_rows[GRIDS:ROWS, 0 : CELLS - P], in_=u[:, P:CELLS])
+            elif what[0] == "b":
+                load_block(int(what[1:]), nc.sync.dma_start)
             else:
                 load_grid(int(what))
 
         nc.scalar.activation(out=warm_out[:], in_=warm[:], func=ACT.Gelu)
 
-        nc.vector.tensor_copy(out=b2_cols[:], in_=b2_bf[:])
-        nc.vector.tensor_copy(out=rows[:], in_=rows_bf[:])
-        nc.vector.tensor_copy(
-            out=w2_words[:].bitcast(I32).rearrange("p (t m) -> p t m", t=PACK),
-            in_=w2_raw_words[:].bitcast(I32).rearrange("p (m t) -> p t m", t=PACK),
-        )
         for t in range(PACK):
             nc.vector.tensor_copy(
                 out=w2_plane[:, t * P : (t + 1) * P], in_=w2_raw_plane[:, t : HID : PACK]
             )
+        nc.vector.tensor_copy(
+            out=w2_words[:].bitcast(I32).rearrange("p (t m) -> p t m", t=PACK),
+            in_=w2_raw_words[:].bitcast(I32).rearrange("p (m t) -> p t m", t=PACK),
+        )
+        nc.vector.tensor_copy(out=b2_cols[:], in_=b2_bf[:])
 
         e_bank, e_grouped, e_codes, e_plane = {}, {}, {}, {}
         product1, x_raw = {}, {}
@@ -151,8 +168,16 @@ def tile_fluxgnn1dlatent_pb_t_kernel(
                 for i in range(n):
                     nc.tensor.matmul(out=bank[:], lhsT=noise[:, 0:P], rhs=noise[:], start=True, stop=True)
 
+        done = []
+
+        def first_time(*what):
+            if what in done:
+                return False
+            done.append(what)
+            return True
+
         def flip_edge_hid(b):
-            if 0 <= b < GRIDS:
+            if 0 <= b < GRIDS and first_time("f", b):
                 e_bank[b] = psum.tile([P, 2, FACES], F32, tag="flip", name="e_bank", bufs=FLIP_BANKS)
                 words = e_in[b][:].bitcast(F32)
                 for n in range(2):
@@ -162,7 +187,7 @@ def tile_fluxgnn1dlatent_pb_t_kernel(
                         )
 
         def copy_edge_hid(b, copy):
-            if 0 <= b < GRIDS:
+            if 0 <= b < GRIDS and first_time("c", b):
                 g, h = divmod(b, 2)
                 if g not in e_grouped:
                     e_grouped[g] = work.tile([P, GROUP, PACK], BF16, tag="e_grouped", name="e_grouped", align_bytes=64)
@@ -171,8 +196,47 @@ def tile_fluxgnn1dlatent_pb_t_kernel(
                     in_=e_bank[b][:].rearrange("p w r -> p r w"),
                 )
 
+        block_bank, block_product = {}, {}
+
+        def flip_block(k):
+            block_bank[k] = psum.tile([P, 2, P], F32, tag=BLOCK_TAG[k], name="block_bank", bufs=FLIP_BANKS if BLOCK_TAG[k] == "flip" else PRODUCT_BANKS)
+            words = e_in[k // 2][:].bitcast(F32)
+            for w in range(2):
+                nc.tensor.transpose(block_bank[k][:, w, :], words[:, k % 2, w : HID // 2 : 2], ident[:])
+
+        def copy_block(k, copy):
+            if 0 not in e_grouped:
+                e_grouped[0] = work.tile([P, GROUP, PACK], BF16, tag="e_grouped", name="e_grouped", align_bytes=64)
+            copy(
+                out=e_grouped[0][:, k * P : (k + 1) * P, :].rearrange("p r t -> p (r t)").bitcast(F32).rearrange("p (r w) -> p r w", w=2),
+                in_=block_bank[k][:].rearrange("p w r -> p r w"),
+            )
+
+        def block_layer1(k):
+            c = slice(k * P, (k + 1) * P)
+            bank = psum.tile([P, PACK, P], F32, tag="product", name="block_product", bufs=PRODUCT_BANKS)
+            block_product[k] = bank
+            for t in range(PACK):
+                nc.tensor.matmul_mx(
+                    out=bank[:, t, :],
+                    lhsT=w2_words[:, t * P : (t + 1) * P].bitcast(FP8X4),
+                    lhsT_scale=w2_plane[:, t * P : (t + 1) * P],
+                    rhs=e_codes[0][:, c].bitcast(FP8X4),
+                    rhs_scale=e_plane[0][:, c],
+                    start=True,
+                    stop=True,
+                )
+
+        def block_gelu(k):
+            if 0 not in x_raw:
+                x_raw[0] = work.tile([P, PACK, GROUP], BF16, tag="x_raw", name="x_raw", bufs=3)
+            for t in range(PACK):
+                nc.scalar.activation(
+                    out=x_raw[0][:, t, k * P : (k + 1) * P], in_=block_product[k][:, t, :], func=ACT.Gelu, bias=b2_cols[:, t : t + 1]
+                )
+
         def quantise_edge_hid(g, c):
-            if 0 <= g < GROUPS:
+            if 0 <= g < GROUPS and first_time("q", g, c.start, c.stop):
                 if g not in e_codes:
                     e_codes[g] = work.tile([P, GROUP], U32, tag="e_codes", name="e_codes", bufs=3, align_bytes=64)
                     e_plane[g] = work.tile([P, GROUP], U8, tag="e_plane", name="e_plane", bufs=3, align_bytes=64)
@@ -183,7 +247,7 @@ def tile_fluxgnn1dlatent_pb_t_kernel(
                 )
 
         def layer1_product(g, t, c):
-            if 0 <= g < GROUPS:
+            if 0 <= g < GROUPS and first_time("l", g, t, c.start):
                 product1[g, t, c.start] = psum.tile([P, c.stop - c.start], F32, tag="product", name="product1", bufs=PRODUCT_BANKS)
                 nc.tensor.matmul_mx(
                     out=product1[g, t, c.start][:],
@@ -196,7 +260,7 @@ def tile_fluxgnn1dlatent_pb_t_kernel(
                 )
 
         def gelu(g, t, c):
-            if 0 <= g < GROUPS:
+            if 0 <= g < GROUPS and first_time("g", g, t, c.start):
                 if g not in x_raw:
                     x_raw[g] = work.tile([P, PACK, GROUP], BF16, tag="x_raw", name="x_raw", bufs=3)
                 nc.scalar.activation(
@@ -204,7 +268,7 @@ def tile_fluxgnn1dlatent_pb_t_kernel(
                 )
 
         def interleave(b):
-            if 0 <= b < GRIDS:
+            if 0 <= b < GRIDS and first_time("i", b):
                 g, h = divmod(b, 2)
                 if h == 0:
                     x_grouped[g] = work.tile([P, GROUP, PACK], BF16, tag="x_grouped", name="x_grouped", align_bytes=64)
@@ -214,7 +278,7 @@ def tile_fluxgnn1dlatent_pb_t_kernel(
                 )
 
         def quantise_x(g):
-            if 0 <= g < GROUPS:
+            if 0 <= g < GROUPS and first_time("x", g):
                 x_codes[g] = work.tile([P, GROUP], U32, tag="x_codes", name="x_codes", bufs=4, align_bytes=64)
                 x_plane[g] = work.tile([P, GROUP], U8, tag="x_plane", name="x_plane", bufs=4, align_bytes=64)
                 nc.vector.quantize_mx(
@@ -255,7 +319,7 @@ def tile_fluxgnn1dlatent_pb_t_kernel(
                     )
 
         def scaled_chunks(g):
-            return SCALED_LAST if g == LAST else SCALED
+            return SC_LAST if g == LAST else SC_6 if g == LAST - 1 else SC
 
         def weigh(n, k):
             if 0 <= n < len(slots):
@@ -300,10 +364,11 @@ def tile_fluxgnn1dlatent_pb_t_kernel(
                         stop=(i == len(terms) - 1),
                     )
 
-        def add_group(g, blocks, chunks=SCALED):
+        def add_group(g, blocks):
             if g not in acc:
                 acc[g] = psum.tile([P, BLOCKS, P], F32, tag="sums", name="acc", bufs=1)
-            add_transposed(acc[g], [weighted[g]] + [scaled[g, j] for j in chunks], blocks)
+            terms = [weighted[g]] if g in weighted else []
+            add_transposed(acc[g], terms + [scaled[g, j] for j in scaled_chunks(g)], blocks)
 
         def reduce_channels(g, bank, cols, h0=0, h1=2):
             nc.vector.tensor_reduce(
@@ -312,6 +377,12 @@ def tile_fluxgnn1dlatent_pb_t_kernel(
                 axis=ALONG_FREE,
                 op=ALU.add,
             )
+
+        def reduce_on_scalar(g, bank, cols):
+            for a in range(BLOCKS):
+                n = GRIDS * (a % 2) + 2 * g + a // 2
+                spare = work.tile([P, P], F32, tag="spare", name="spare", bufs=4)
+                nc.scalar.activation(out=spare[:], in_=bank[:, a, :], func=ACT.Copy, accum_out=cols[:, n : n + 1])
 
         AT_FLIP, AT_COPY, AT_QE, AT_LAYER1, AT_INT, AT_QX = -15, -14, -12, -9, -5, -3
 
@@ -327,18 +398,27 @@ def tile_fluxgnn1dlatent_pb_t_kernel(
             m = n - AT_LAYER1
             if m >= PACK:
                 layer1_product(m // PACK, m % PACK, whole)
+            def flips():
+                flip_edge_hid(2 * group_from(AT_FLIP, 2))
+                if group_from(AT_FLIP + FL_POS, 2) > 0:
+                    flip_edge_hid(2 * group_from(AT_FLIP + FL_POS, 2) + 1)
+
+            if FL_AFTER == 0:
+                flips()
             layer2_product(n)
-            flip_edge_hid(2 * group_from(AT_FLIP, 2))
-            if group_from(AT_FLIP, 2) > 0:
-                flip_edge_hid(2 * group_from(AT_FLIP, 2) + 1)
+            if FL_AFTER == 1:
+                flips()
             for g in range(LAST):
-                if n == (RUN_6A if g == LAST - 1 else 4 * g + RUN_A):
-                    add_group(g, [0, 1])
-                if n == (RUN_6B if g == LAST - 1 else 4 * g + RUN_B):
-                    add_group(g, [2, 3])
+                for at, blocks in RUNS:
+                    if n == (RUN_6A if g == LAST - 1 else 4 * g + at):
+                        add_group(g, blocks)
+            if FL_AFTER == 2:
+                flips()
 
             g = group_from(AT_COPY, 2)
-            copies = [2 * g, 2 * g + 1] if g > 0 else []
+            copies = [2 * g] if g > 0 else []
+            g = group_from(AT_COPY + FL_POS, 2)
+            copies += [2 * g + 1] if g > 0 else []
             for b in copies:
                 if b in COPIED_BY_SCALAR:
                     copy_edge_hid(b, nc.scalar.copy)
@@ -349,9 +429,14 @@ def tile_fluxgnn1dlatent_pb_t_kernel(
             for b in copies:
                 if b not in COPIED_BY_SCALAR:
                     copy_edge_hid(b, nc.vector.tensor_copy)
-            for g in range(LAST):
-                if n == (REDUCE_6 if g == LAST - 1 else 4 * g + REDUCE):
+            for g in range(LAST - 1):
+                if n == 4 * g + REDUCE:
                     reduce_channels(g, acc[g], w_cols)
+            if n == REDUCE_6:
+                if ACT_6:
+                    reduce_on_scalar(LAST - 1, acc[LAST - 1], w_cols)
+                elif not LATE_6:
+                    reduce_channels(LAST - 1, acc[LAST - 1], w_cols)
             if group_at(AT_INT) >= 0:
                 interleave(2 * group_at(AT_INT))
             if group_at(AT_INT + 1) >= 0:
@@ -363,33 +448,8 @@ def tile_fluxgnn1dlatent_pb_t_kernel(
                 quantise_x(group_at(AT_QX))
             weigh(n - 1, 1)
 
-        halves = [slice(0, FACES), slice(FACES, GROUP)]
-        stir(WARM0)
-        flip_edge_hid(0)
-        copy_edge_hid(0, nc.scalar.copy)
-        stir(WARM1)
-        flip_edge_hid(1)
-        stir(WARM2)
-        quantise_edge_hid(0, halves[0])
-        copy_edge_hid(1, nc.vector.tensor_copy)
-        for t in range(PACK):
-            layer1_product(0, t, halves[0])
-            gelu(0, t, halves[0])
-        flip_edge_hid(2)
-        quantise_edge_hid(0, halves[1])
-        copy_edge_hid(2, nc.vector.tensor_copy)
-        flip_edge_hid(3)
-        copy_edge_hid(3, nc.vector.tensor_copy)
-        for t in range(PACK):
-            layer1_product(0, t, halves[1])
-            gelu(0, t, halves[1])
-        cols_ps = psum.tile([P, P], F32, tag="product", name="cols_ps", bufs=PRODUCT_BANKS)
-        nc.tensor.transpose(cols_ps[:], rows[:], ident[:])
-        quantise_edge_hid(1, whole)
-        nc.vector.tensor_copy(out=cols[:], in_=cols_ps[:])
         enc_cols = cols[:, 0:CHUNKS]
         b3_cols = cols[:, CHUNKS : 2 * CHUNKS]
-
         enc_sq = keep.tile([P, CHUNKS], F32, name="enc_sq")
         enc_sq_sum = keep.tile([P, 1], F32, name="enc_sq_sum")
         norm = keep.tile([P, 1], F32, name="norm")
@@ -402,6 +462,8 @@ def tile_fluxgnn1dlatent_pb_t_kernel(
         norm_bank = {}
 
         def prepare(step_number):
+            if not first_time("p", step_number):
+                return
             if step_number == 0:
                 nc.vector.tensor_tensor(out=enc_sq[:], in0=enc_cols, in1=enc_cols, op=ALU.mult)
             if step_number == 1:
@@ -429,6 +491,54 @@ def tile_fluxgnn1dlatent_pb_t_kernel(
                     op1=ALU.mult,
                 )
 
+        halves = [slice(0, FACES), slice(FACES, GROUP)]
+        on_vector, on_scalar = nc.vector.tensor_copy, nc.scalar.copy
+        for what in HEAD.split():
+            op, arg = what[0], what[1:]
+            if op == "w":
+                stir(int(arg))
+            if op == "f":
+                flip_edge_hid(int(arg))
+            if op == "v":
+                copy_edge_hid(int(arg), on_vector)
+            if op == "s":
+                copy_edge_hid(int(arg), on_scalar)
+            if op == "F":
+                flip_block(int(arg))
+            if op == "V":
+                copy_block(int(arg), on_vector)
+            if op == "A":
+                copy_block(int(arg), on_scalar)
+            if op == "Q":
+                quantise_edge_hid(0, slice(int(arg) * P, (int(arg) + 1) * P))
+            if op == "B":
+                block_layer1(int(arg))
+                block_gelu(int(arg))
+            if op == "p":
+                prepare(int(arg))
+            if op == "R":
+                nc.vector.tensor_copy(out=rows[:], in_=rows_bf[:])
+            if op == "h":
+                quantise_edge_hid(0, halves[int(arg)])
+            if op == "q":
+                quantise_edge_hid(int(arg), whole)
+            if op == "g":
+                for t in range(PACK):
+                    layer1_product(0, t, halves[int(arg)])
+                    gelu(0, t, halves[int(arg)])
+            if op == "G":
+                layer1_product(int(arg[0]), int(arg[1]), whole)
+                gelu(int(arg[0]), int(arg[1]), whole)
+            if op == "c":
+                cols_ps = psum.tile([P, P], F32, tag="product", name="cols_ps", bufs=PRODUCT_BANKS)
+                nc.tensor.transpose(cols_ps[:], rows[:], ident[:])
+            if op == "C":
+                nc.vector.tensor_copy(out=cols[:, 0 : 2 * CHUNKS], in_=cols_ps[:, 0 : 2 * CHUNKS])
+            if op == "i":
+                interleave(int(arg))
+            if op == "x":
+                quantise_x(int(arg))
+
         for n in range(-7, len(slots) + 1):
             prepare(n + 1)
             slot(n)
@@ -437,9 +547,15 @@ def tile_fluxgnn1dlatent_pb_t_kernel(
         early_bank = psum.tile([P, BLOCKS, P], F32, tag="flip", name="early_bank", bufs=FLIP_BANKS)
         late_bank = psum.tile([P, BLOCKS, P], F32, tag="flip", name="late_bank", bufs=FLIP_BANKS)
         stir(WARM_END)
-        add_transposed(early_bank, [weighted[LAST]], range(BLOCKS))
-        reduce_channels(LAST, early_bank, w_cols)
-        add_transposed(late_bank, [scaled[LAST, j] for j in SCALED_LAST], range(BLOCKS))
+        if LATE_6 and not ACT_6:
+            reduce_channels(LAST - 1, acc[LAST - 1], w_cols)
+        split = len(SC_LAST) - N_LATE
+        add_transposed(early_bank, [weighted[LAST]] + [scaled[LAST, j] for j in SC_LAST[:split]], range(BLOCKS))
+        if ACT_7:
+            reduce_on_scalar(LAST, early_bank, w_cols)
+        else:
+            reduce_channels(LAST, early_bank, w_cols)
+        add_transposed(late_bank, [scaled[LAST, j] for j in SC_LAST[split:]], range(BLOCKS))
         reduce_channels(LAST, late_bank, w_late, 0, 1)
         reduce_channels(LAST, late_bank, w_late, 1, 2)
         faces = psum.tile([P, 2, P], F32, tag="product", name="faces", bufs=PRODUCT_BANKS)

@@ -34,15 +34,16 @@ SCALED = [4, 5, 6, 7]
 SCALED_LAST = [6, 7]
 REDUCE = 10
 RUN_6A, REDUCE_6 = 31, 32
-COPIED_BY_SCALAR = [5]
+COPIED_BY_SCALAR = [5, 13]
 TANH_BUFS = 12
 SCALED_BUFS = 16
-SC = [4, 5, 6, 7]
-SC_LAST = [6, 7]
-FL_AFTER = 2
-ACT_6, LATE_6, N_LATE, ACT_7 = 0, 1, 2, 0
-SC_6 = [4, 5, 6, 7]
-FL_POS = 1
+SC = [3, 5, 7]
+SC_LAST = []
+LATE_CHUNKS = [5, 7]
+FL_AFTER = 1
+ACT_6, LATE_6, N_LATE, ACT_7 = 1, 1, 1, 1
+SC_6 = [3, 5, 7]
+FL_POS = 0
 RUNS = [(8, [0, 1]), (9, [2, 3])]
 CP_POS = 0
 BLOCK_TAG = ["flip", "flip", "product", "product"]
@@ -325,7 +326,24 @@ def tile_fluxgnn1dlatent_pb_t_kernel(
             if 0 <= n < len(slots):
                 g, j = slots[n][k]
                 covered.append((g, j))
-                if j in scaled_chunks(g):
+                if g == LAST and j in LATE_CHUNKS:
+                    if "late" not in weighted:
+                        weighted["late"] = work.tile([P, GROUP], F32, tag="weighted", name="weighted", bufs=5)
+                        nc.vector.tensor_scalar(
+                            out=weighted["late"][:], in0=tanh[g, j][:], scalar1=enc_cols[:, j : j + 1], scalar2=None, op0=ALU.mult
+                        )
+                    else:
+                        for a in range(2):
+                            part = slice(a * FACES, (a + 1) * FACES)
+                            nc.vector.scalar_tensor_tensor(
+                                out=weighted["late"][:, part],
+                                in0=tanh[g, j][:, part],
+                                scalar=enc_cols[:, j : j + 1],
+                                in1=weighted["late"][:, part],
+                                op0=ALU.mult,
+                                op1=ALU.add,
+                            )
+                elif j in scaled_chunks(g):
                     scaled[g, j] = work.tile([P, GROUP], F32, tag="scaled", name="scaled", bufs=SCALED_BUFS)
                     parts = 2 if (g, j) == slots[-1][-1] else 1
                     for a in range(parts):
@@ -549,13 +567,13 @@ def tile_fluxgnn1dlatent_pb_t_kernel(
         stir(WARM_END)
         if LATE_6 and not ACT_6:
             reduce_channels(LAST - 1, acc[LAST - 1], w_cols)
-        split = len(SC_LAST) - N_LATE
+        split = len(SC_LAST) if LATE_CHUNKS else len(SC_LAST) - N_LATE
         add_transposed(early_bank, [weighted[LAST]] + [scaled[LAST, j] for j in SC_LAST[:split]], range(BLOCKS))
         if ACT_7:
             reduce_on_scalar(LAST, early_bank, w_cols)
         else:
             reduce_channels(LAST, early_bank, w_cols)
-        add_transposed(late_bank, [scaled[LAST, j] for j in SC_LAST[split:]], range(BLOCKS))
+        add_transposed(late_bank, [weighted["late"]] if LATE_CHUNKS else [scaled[LAST, j] for j in SC_LAST[split:]], range(BLOCKS))
         reduce_channels(LAST, late_bank, w_late, 0, 1)
         reduce_channels(LAST, late_bank, w_late, 1, 2)
         faces = psum.tile([P, 2, P], F32, tag="product", name="faces", bufs=PRODUCT_BANKS)

@@ -47,8 +47,8 @@ FL_POS = 0
 RUNS = [(8, [0, 1]), (9, [2, 3])]
 CP_POS = 0
 BLOCK_TAG = ["flip", "flip", "product", "product"]
-HEAD = "w6 F0 A0 F1 w1 A1 R c Q0 B0 Q1 C B1 F2 p0 V2 F3 V3 p1 f2 s2 f3 Q2 B2 Q3 B3 v3 p4 q1 i0 p5"
-LOADS = ["b0", "b1", "w2", "s2", "bias", "1", "enc", "2", "3", "w3", "s3"] + [str(i) for i in range(4, 16)] + ["u"]
+HEAD = "w6 F0 A0 F1 w1 A1 Q0 B0 Q1 B1 F2 V2 F3 V3 f2 s2 f3 Q2 B2 Q3 B3 v3 R c q1 C i0"
+LOADS = ["0", "s2", "w2", "bias", "1", "2", "enc", "3", "w3", "s3"] + [str(i) for i in range(4, 16)] + ["u"]
 WARM0 = 4
 WARM1 = 4
 WARM2 = 1

@@ -48,7 +48,7 @@ RUNS = [(8, [0, 1]), (9, [2, 3])]
 CP_POS = 0
 BLOCK_TAG = ["flip", "flip", "product", "product"]
 HEAD = "w6 F0 A0 F1 w1 A1 Q0 B0 Q1 B1 F2 V2 F3 V3 f2 s2 f3 Q2 B2 Q3 B3 v3 R c q1 C i0"
-LOADS = ["0", "s2", "w2", "bias", "1", "2", "enc", "3", "w3", "s3"] + [str(i) for i in range(4, 16)] + ["u"]
+LOADS = ["s2", "a0", "bias", "w2", "1", "2", "3", "encs", "4", "5", "w3", "s3"] + [str(i) for i in range(6, 16)] + ["u"]
 WARM0 = 4
 WARM1 = 4
 WARM2 = 1
@@ -131,8 +131,19 @@ def tile_fluxgnn1dlatent_pb_t_kernel(
                 load_words(w3_words, W3_words)
             elif what == "s3":
                 load_plane(w3_plane, W3_scales)
+            elif what[0] == "a":
+                b = int(what[1:])
+                nc.scalar.dma_start(
+                    out=e_in[b][:],
+                    in_=tokens[b * FACES : (b + 1) * FACES, :].rearrange("(n p) k -> p n k", p=P),
+                )
             elif what == "bias":
                 nc.scalar.dma_start(out=b2_bf[:], in_=b2.rearrange("(p t) -> p t", t=PACK))
+            elif what == "encs":
+                nc.sync.dma_start(out=rows_bf[0:CHUNKS, :], in_=enc.rearrange("(j p) -> j p", p=P))
+                nc.sync.dma_start(
+                    out=rows_bf[CHUNKS : 2 * CHUNKS, :], in_=b3.rearrange("(j p) -> j p", p=P)
+                )
             elif what == "enc":
                 nc.scalar.dma_start(out=rows_bf[0:CHUNKS, :], in_=enc.rearrange("(j p) -> j p", p=P))
                 nc.scalar.dma_start(

@@ -30,30 +30,13 @@ ROWS = 2 * GRIDS
 FLIP_BANKS = 2
 PRODUCT_BANKS = 5
 
-SCALED = [4, 5, 6, 7]
-SCALED_LAST = [6, 7]
-REDUCE = 10
-RUN_6A, REDUCE_6 = 31, 32
-COPIED_BY_SCALAR = [5, 13]
-TANH_BUFS = 12
-SCALED_BUFS = 16
-SC = [3, 5, 7]
-SC_LAST = []
-LATE_CHUNKS = [5, 7]
-FL_AFTER = 1
-ACT_6, LATE_6, N_LATE, ACT_7 = 1, 1, 1, 1
-SC_6 = [3, 5, 7]
-FL_POS = 0
-RUNS = [(8, [0, 1]), (9, [2, 3])]
-CP_POS = 0
-BLOCK_TAG = ["flip", "flip", "product", "product"]
-HEAD = "w6 F0 A0 F1 w1 A1 Q0 B0 Q1 B1 F2 V2 F3 V3 f2 s2 f3 Q2 B2 Q3 B3 v3 R c q1 C i0"
-LOADS = ["s2", "a0", "bias", "w2", "1", "2", "3", "encs", "4", "5", "w3", "s3"] + [str(i) for i in range(6, 16)] + ["u"]
-WARM0 = 4
-WARM1 = 4
-WARM2 = 1
-WARM_END = 2
-R6_POS = 0
+SCALED = (3, 5, 7)
+LATE_CHUNKS = (5, 7)
+COPIED_BY_SCALAR = (5, 13)
+
+AT_FLIP, AT_COPY, AT_QUANTISE_EDGE, AT_LAYER1 = -15, -14, -12, -9
+AT_INTERLEAVE, AT_QUANTISE_X = -5, -3
+AT_TURN, AT_REDUCE = 8, 10
 
 FLOPS = 2 * GRIDS * FACES * HID * (HID + LATENT)
 
@@ -80,6 +63,8 @@ def tile_fluxgnn1dlatent_pb_t_kernel(
         rows_bf = keep.tile([P, P], BF16, name="rows_bf")
         rows = keep.tile([P, P], F32, name="rows")
         cols = keep.tile([P, 2 * CHUNKS], F32, name="cols")
+        enc_cols = cols[:, 0:CHUNKS]
+        b3_cols = cols[:, CHUNKS : 2 * CHUNKS]
         ident = keep.tile([P, P], F32, name="ident")
         b2_bf = keep.tile([P, PACK], BF16, name="b2_bf")
         b2_cols = keep.tile([P, PACK], F32, name="b2_cols")
@@ -100,14 +85,11 @@ def tile_fluxgnn1dlatent_pb_t_kernel(
         nc.vector.memset(w_cols[:], 0.0)
         nc.vector.memset(w_late[:], 0.0)
 
-        def load_grid(b):
-            nc.sync.dma_start(
+        def load_grid(b, start=nc.sync.dma_start):
+            start(
                 out=e_in[b][:],
                 in_=tokens[b * FACES : (b + 1) * FACES, :].rearrange("(n p) k -> p n k", p=P),
             )
-
-        def load_block(k, start):
-            start(out=e_in[k // 2][:, k % 2, :], in_=tokens[k * P : (k + 1) * P, :])
 
         def load_words(words_tile, words):
             nc.sync.dma_start(
@@ -122,40 +104,22 @@ def tile_fluxgnn1dlatent_pb_t_kernel(
                     in_=scales[0, 4 * quad : 4 * quad + 4, :].bitcast(I32),
                 )
 
-        for what in LOADS:
-            if what == "w2":
-                load_words(w2_raw_words, W2_words)
-            elif what == "s2":
-                load_plane(w2_raw_plane, W2_scales)
-            elif what == "w3":
-                load_words(w3_words, W3_words)
-            elif what == "s3":
-                load_plane(w3_plane, W3_scales)
-            elif what[0] == "a":
-                b = int(what[1:])
-                nc.scalar.dma_start(
-                    out=e_in[b][:],
-                    in_=tokens[b * FACES : (b + 1) * FACES, :].rearrange("(n p) k -> p n k", p=P),
-                )
-            elif what == "bias":
-                nc.scalar.dma_start(out=b2_bf[:], in_=b2.rearrange("(p t) -> p t", t=PACK))
-            elif what == "encs":
-                nc.sync.dma_start(out=rows_bf[0:CHUNKS, :], in_=enc.rearrange("(j p) -> j p", p=P))
-                nc.sync.dma_start(
-                    out=rows_bf[CHUNKS : 2 * CHUNKS, :], in_=b3.rearrange("(j p) -> j p", p=P)
-                )
-            elif what == "enc":
-                nc.scalar.dma_start(out=rows_bf[0:CHUNKS, :], in_=enc.rearrange("(j p) -> j p", p=P))
-                nc.scalar.dma_start(
-                    out=rows_bf[CHUNKS : 2 * CHUNKS, :], in_=b3.rearrange("(j p) -> j p", p=P)
-                )
-            elif what == "u":
-                nc.sync.dma_start(out=u_rows[0:GRIDS, :], in_=u[:, 0:P])
-                nc.sync.dma_start(out=u_rows[GRIDS:ROWS, 0 : CELLS - P], in_=u[:, P:CELLS])
-            elif what[0] == "b":
-                load_block(int(what[1:]), nc.sync.dma_start)
-            else:
-                load_grid(int(what))
+        load_plane(w2_raw_plane, W2_scales)
+        load_grid(0, nc.scalar.dma_start)
+        nc.scalar.dma_start(out=b2_bf[:], in_=b2.rearrange("(p t) -> p t", t=PACK))
+        load_words(w2_raw_words, W2_words)
+        for b in range(1, 4):
+            load_grid(b)
+        nc.sync.dma_start(out=rows_bf[0:CHUNKS, :], in_=enc.rearrange("(j p) -> j p", p=P))
+        nc.sync.dma_start(out=rows_bf[CHUNKS : 2 * CHUNKS, :], in_=b3.rearrange("(j p) -> j p", p=P))
+        for b in range(4, 6):
+            load_grid(b)
+        load_words(w3_words, W3_words)
+        load_plane(w3_plane, W3_scales)
+        for b in range(6, GRIDS):
+            load_grid(b)
+        nc.sync.dma_start(out=u_rows[0:GRIDS, :], in_=u[:, 0:P])
+        nc.sync.dma_start(out=u_rows[GRIDS:ROWS, 0 : CELLS - P], in_=u[:, P:CELLS])
 
         nc.scalar.activation(out=warm_out[:], in_=warm[:], func=ACT.Gelu)
 
@@ -170,315 +134,191 @@ def tile_fluxgnn1dlatent_pb_t_kernel(
         nc.vector.tensor_copy(out=b2_cols[:], in_=b2_bf[:])
 
         e_bank, e_grouped, e_codes, e_plane = {}, {}, {}, {}
-        product1, x_raw = {}, {}
-        x_grouped, x_codes, x_plane = {}, {}, {}
-        product2, tanh, weighted, scaled, acc = {}, {}, {}, {}, {}
+        product1, x_raw, x_grouped, x_codes, x_plane = {}, {}, {}, {}, {}
+        product2, tanh, weighted, scaled, turned = {}, {}, {}, {}, {}
+
+        def product_bank(shape, name):
+            return psum.tile(shape, F32, tag="product", name=name, bufs=PRODUCT_BANKS)
+
+        def flip_bank(shape, name):
+            return psum.tile(shape, F32, tag="flip", name=name, bufs=FLIP_BANKS)
 
         def stir(n):
-            if n > 0:
-                bank = psum.tile([P, GROUP], F32, tag="product", name="stirred", bufs=PRODUCT_BANKS)
-                for i in range(n):
-                    nc.tensor.matmul(out=bank[:], lhsT=noise[:, 0:P], rhs=noise[:], start=True, stop=True)
+            bank = product_bank([P, GROUP], "stirred")
+            for i in range(n):
+                nc.tensor.matmul(out=bank[:], lhsT=noise[:, 0:P], rhs=noise[:], start=True, stop=True)
 
-        done = []
-
-        def first_time(*what):
-            if what in done:
-                return False
-            done.append(what)
-            return True
-
-        def flip_edge_hid(b):
-            if 0 <= b < GRIDS and first_time("f", b):
-                e_bank[b] = psum.tile([P, 2, FACES], F32, tag="flip", name="e_bank", bufs=FLIP_BANKS)
-                words = e_in[b][:].bitcast(F32)
-                for n in range(2):
-                    for w in range(2):
-                        nc.tensor.transpose(
-                            e_bank[b][:, w, n * P : (n + 1) * P], words[:, n, w : HID // 2 : 2], ident[:]
-                        )
-
-        def copy_edge_hid(b, copy):
-            if 0 <= b < GRIDS and first_time("c", b):
-                g, h = divmod(b, 2)
-                if g not in e_grouped:
-                    e_grouped[g] = work.tile([P, GROUP, PACK], BF16, tag="e_grouped", name="e_grouped", align_bytes=64)
-                copy(
-                    out=e_grouped[g][:, h * FACES : (h + 1) * FACES, :].rearrange("p r t -> p (r t)").bitcast(F32).rearrange("p (r w) -> p r w", w=2),
-                    in_=e_bank[b][:].rearrange("p w r -> p r w"),
-                )
-
-        block_bank, block_product = {}, {}
-
-        def flip_block(k):
-            block_bank[k] = psum.tile([P, 2, P], F32, tag=BLOCK_TAG[k], name="block_bank", bufs=FLIP_BANKS if BLOCK_TAG[k] == "flip" else PRODUCT_BANKS)
-            words = e_in[k // 2][:].bitcast(F32)
+        def flip(bank, b, n, first):
+            words = e_in[b][:].bitcast(F32)
             for w in range(2):
-                nc.tensor.transpose(block_bank[k][:, w, :], words[:, k % 2, w : HID // 2 : 2], ident[:])
+                nc.tensor.transpose(bank[:, w, first : first + P], words[:, n, w : HID // 2 : 2], ident[:])
 
-        def copy_block(k, copy):
-            if 0 not in e_grouped:
-                e_grouped[0] = work.tile([P, GROUP, PACK], BF16, tag="e_grouped", name="e_grouped", align_bytes=64)
+        def copy_turned(bank, first, count, copy):
+            g, first = divmod(first, GROUP)
+            if g not in e_grouped:
+                e_grouped[g] = work.tile([P, GROUP, PACK], BF16, tag="e_grouped", name="e_grouped", align_bytes=64)
+            rows_of = e_grouped[g][:, first : first + count, :].rearrange("p r t -> p (r t)")
             copy(
-                out=e_grouped[0][:, k * P : (k + 1) * P, :].rearrange("p r t -> p (r t)").bitcast(F32).rearrange("p (r w) -> p r w", w=2),
-                in_=block_bank[k][:].rearrange("p w r -> p r w"),
+                out=rows_of.bitcast(F32).rearrange("p (r w) -> p r w", w=2),
+                in_=bank[:].rearrange("p w r -> p r w"),
             )
 
-        def block_layer1(k):
-            c = slice(k * P, (k + 1) * P)
-            bank = psum.tile([P, PACK, P], F32, tag="product", name="block_product", bufs=PRODUCT_BANKS)
-            block_product[k] = bank
-            for t in range(PACK):
-                nc.tensor.matmul_mx(
-                    out=bank[:, t, :],
-                    lhsT=w2_words[:, t * P : (t + 1) * P].bitcast(FP8X4),
-                    lhsT_scale=w2_plane[:, t * P : (t + 1) * P],
-                    rhs=e_codes[0][:, c].bitcast(FP8X4),
-                    rhs_scale=e_plane[0][:, c],
-                    start=True,
-                    stop=True,
-                )
+        def flip_grid(b):
+            e_bank[b] = flip_bank([P, 2, FACES], "e_bank")
+            for n in range(2):
+                flip(e_bank[b], b, n, n * P)
 
-        def block_gelu(k):
-            if 0 not in x_raw:
-                x_raw[0] = work.tile([P, PACK, GROUP], BF16, tag="x_raw", name="x_raw", bufs=3)
-            for t in range(PACK):
-                nc.scalar.activation(
-                    out=x_raw[0][:, t, k * P : (k + 1) * P], in_=block_product[k][:, t, :], func=ACT.Gelu, bias=b2_cols[:, t : t + 1]
-                )
+        def copy_grid(b, copy):
+            copy_turned(e_bank[b], b * FACES, FACES, copy)
+
+        def flip_block(k, bank):
+            e_bank["block", k] = bank
+            flip(bank, k // 2, k % 2, 0)
+
+        def copy_block(k, copy):
+            copy_turned(e_bank["block", k], k * P, P, copy)
 
         def quantise_edge_hid(g, c):
-            if 0 <= g < GROUPS and first_time("q", g, c.start, c.stop):
-                if g not in e_codes:
-                    e_codes[g] = work.tile([P, GROUP], U32, tag="e_codes", name="e_codes", bufs=3, align_bytes=64)
-                    e_plane[g] = work.tile([P, GROUP], U8, tag="e_plane", name="e_plane", bufs=3, align_bytes=64)
-                nc.vector.quantize_mx(
-                    out=e_codes[g][:, c].bitcast(FP8X4),
-                    scales=e_plane[g][:, c],
-                    in_=e_grouped[g][:, c, :].rearrange("p r t -> p (r t)"),
-                )
+            if g not in e_codes:
+                e_codes[g] = work.tile([P, GROUP], U32, tag="e_codes", name="e_codes", bufs=3, align_bytes=64)
+                e_plane[g] = work.tile([P, GROUP], U8, tag="e_plane", name="e_plane", bufs=3, align_bytes=64)
+            nc.vector.quantize_mx(
+                out=e_codes[g][:, c].bitcast(FP8X4),
+                scales=e_plane[g][:, c],
+                in_=e_grouped[g][:, c, :].rearrange("p r t -> p (r t)"),
+            )
 
-        def layer1_product(g, t, c):
-            if 0 <= g < GROUPS and first_time("l", g, t, c.start):
-                product1[g, t, c.start] = psum.tile([P, c.stop - c.start], F32, tag="product", name="product1", bufs=PRODUCT_BANKS)
-                nc.tensor.matmul_mx(
-                    out=product1[g, t, c.start][:],
-                    lhsT=w2_words[:, t * P : (t + 1) * P].bitcast(FP8X4),
-                    lhsT_scale=w2_plane[:, t * P : (t + 1) * P],
-                    rhs=e_codes[g][:, c].bitcast(FP8X4),
-                    rhs_scale=e_plane[g][:, c],
-                    start=True,
-                    stop=True,
-                )
+        def multiply_by_w2(product, g, t, c):
+            nc.tensor.matmul_mx(
+                out=product,
+                lhsT=w2_words[:, t * P : (t + 1) * P].bitcast(FP8X4),
+                lhsT_scale=w2_plane[:, t * P : (t + 1) * P],
+                rhs=e_codes[g][:, c].bitcast(FP8X4),
+                rhs_scale=e_plane[g][:, c],
+                start=True,
+                stop=True,
+            )
 
-        def gelu(g, t, c):
-            if 0 <= g < GROUPS and first_time("g", g, t, c.start):
-                if g not in x_raw:
-                    x_raw[g] = work.tile([P, PACK, GROUP], BF16, tag="x_raw", name="x_raw", bufs=3)
-                nc.scalar.activation(
-                    out=x_raw[g][:, t, c], in_=product1[g, t, c.start][:], func=ACT.Gelu, bias=b2_cols[:, t : t + 1]
-                )
+        def gelu(product, g, t, c):
+            if g not in x_raw:
+                x_raw[g] = work.tile([P, PACK, GROUP], BF16, tag="x_raw", name="x_raw", bufs=3)
+            nc.scalar.activation(out=x_raw[g][:, t, c], in_=product, func=ACT.Gelu, bias=b2_cols[:, t : t + 1])
 
-        def interleave(b):
-            if 0 <= b < GRIDS and first_time("i", b):
-                g, h = divmod(b, 2)
-                if h == 0:
-                    x_grouped[g] = work.tile([P, GROUP, PACK], BF16, tag="x_grouped", name="x_grouped", align_bytes=64)
-                nc.vector.tensor_copy(
-                    out=x_grouped[g][:, h * FACES : (h + 1) * FACES, :].rearrange("p (c i) t -> p c t i", i=4),
-                    in_=x_raw[g][:, :, h * FACES : (h + 1) * FACES].rearrange("p t (c i) -> p c t i", i=4),
-                )
-
-        def quantise_x(g):
-            if 0 <= g < GROUPS and first_time("x", g):
-                x_codes[g] = work.tile([P, GROUP], U32, tag="x_codes", name="x_codes", bufs=4, align_bytes=64)
-                x_plane[g] = work.tile([P, GROUP], U8, tag="x_plane", name="x_plane", bufs=4, align_bytes=64)
-                nc.vector.quantize_mx(
-                    out=x_codes[g][:].bitcast(FP8X4),
-                    scales=x_plane[g][:],
-                    in_=x_grouped[g][:].rearrange("p r t -> p (r t)"),
-                )
+        def layer1_of_block(k):
+            c = slice(k * P, (k + 1) * P)
+            bank = product_bank([P, PACK, P], "block_product")
+            for t in range(PACK):
+                multiply_by_w2(bank[:, t, :], 0, t, c)
+            for t in range(PACK):
+                gelu(bank[:, t, :], 0, t, c)
 
         whole = slice(0, GROUP)
+
+        def interleave(b):
+            g, h = divmod(b, 2)
+            c = slice(h * FACES, (h + 1) * FACES)
+            if h == 0:
+                x_grouped[g] = work.tile([P, GROUP, PACK], BF16, tag="x_grouped", name="x_grouped", align_bytes=64)
+            nc.vector.tensor_copy(
+                out=x_grouped[g][:, c, :].rearrange("p (c i) t -> p c t i", i=4),
+                in_=x_raw[g][:, :, c].rearrange("p t (c i) -> p c t i", i=4),
+            )
+
+        def quantise_x(g):
+            x_codes[g] = work.tile([P, GROUP], U32, tag="x_codes", name="x_codes", bufs=4, align_bytes=64)
+            x_plane[g] = work.tile([P, GROUP], U8, tag="x_plane", name="x_plane", bufs=4, align_bytes=64)
+            nc.vector.quantize_mx(
+                out=x_codes[g][:].bitcast(FP8X4),
+                scales=x_plane[g][:],
+                in_=x_grouped[g][:].rearrange("p r t -> p (r t)"),
+            )
 
         jobs = sorted(
             [(g, j) for g in range(GROUPS) for j in range(CHUNKS)],
             key=lambda job: (CHUNKS // 2 * job[0] + job[1], job[0]),
         )
         slots = [jobs[i : i + 2] for i in range(0, len(jobs), 2)]
-        covered = []
 
-        def layer2_product(n):
-            if 0 <= n < len(slots):
-                for g, j in slots[n]:
-                    product2[g, j] = psum.tile([P, GROUP], F32, tag="product", name="product2", bufs=PRODUCT_BANKS)
-                    nc.tensor.matmul_mx(
-                        out=product2[g, j][:],
-                        lhsT=w3_words[:, j * P : (j + 1) * P].bitcast(FP8X4),
-                        lhsT_scale=w3_plane[:, j * P : (j + 1) * P],
-                        rhs=x_codes[g][:].bitcast(FP8X4),
-                        rhs_scale=x_plane[g][:],
-                        start=True,
-                        stop=True,
-                    )
+        def layer2_product(g, j):
+            product2[g, j] = product_bank([P, GROUP], "product2")
+            nc.tensor.matmul_mx(
+                out=product2[g, j][:],
+                lhsT=w3_words[:, j * P : (j + 1) * P].bitcast(FP8X4),
+                lhsT_scale=w3_plane[:, j * P : (j + 1) * P],
+                rhs=x_codes[g][:].bitcast(FP8X4),
+                rhs_scale=x_plane[g][:],
+                start=True,
+                stop=True,
+            )
 
-        def tanh_of(n):
-            if 0 <= n < len(slots):
-                for g, j in slots[n]:
-                    tanh[g, j] = work.tile([P, GROUP], F32, tag="tanh", name="tanh", bufs=TANH_BUFS)
-                    nc.scalar.activation(
-                        out=tanh[g, j][:], in_=product2[g, j][:], func=ACT.Tanh, bias=b3_cols[:, j : j + 1]
-                    )
+        def tanh_of(g, j):
+            tanh[g, j] = work.tile([P, GROUP], F32, tag="tanh", name="tanh", bufs=12)
+            nc.scalar.activation(out=tanh[g, j][:], in_=product2[g, j][:], func=ACT.Tanh, bias=b3_cols[:, j : j + 1])
 
-        def scaled_chunks(g):
-            return SC_LAST if g == LAST else SC_6 if g == LAST - 1 else SC
+        def scale_by_enc(out, g, j):
+            nc.vector.tensor_scalar(
+                out=out, in0=tanh[g, j][:], scalar1=enc_cols[:, j : j + 1], scalar2=None, op0=ALU.mult
+            )
 
-        def weigh(n, k):
-            if 0 <= n < len(slots):
-                g, j = slots[n][k]
-                covered.append((g, j))
-                if g == LAST and j in LATE_CHUNKS:
-                    if "late" not in weighted:
-                        weighted["late"] = work.tile([P, GROUP], F32, tag="weighted", name="weighted", bufs=5)
-                        nc.vector.tensor_scalar(
-                            out=weighted["late"][:], in0=tanh[g, j][:], scalar1=enc_cols[:, j : j + 1], scalar2=None, op0=ALU.mult
-                        )
-                    else:
-                        for a in range(2):
-                            part = slice(a * FACES, (a + 1) * FACES)
-                            nc.vector.scalar_tensor_tensor(
-                                out=weighted["late"][:, part],
-                                in0=tanh[g, j][:, part],
-                                scalar=enc_cols[:, j : j + 1],
-                                in1=weighted["late"][:, part],
-                                op0=ALU.mult,
-                                op1=ALU.add,
-                            )
-                elif j in scaled_chunks(g):
-                    scaled[g, j] = work.tile([P, GROUP], F32, tag="scaled", name="scaled", bufs=SCALED_BUFS)
-                    parts = 2 if (g, j) == slots[-1][-1] else 1
-                    for a in range(parts):
-                        part = slice(a * GROUP // parts, (a + 1) * GROUP // parts)
-                        nc.vector.tensor_scalar(
-                            out=scaled[g, j][:, part],
-                            in0=tanh[g, j][:, part],
-                            scalar1=enc_cols[:, j : j + 1],
-                            scalar2=None,
-                            op0=ALU.mult,
-                        )
-                elif g not in weighted:
-                    weighted[g] = work.tile([P, GROUP], F32, tag="weighted", name="weighted", bufs=5)
-                    nc.vector.tensor_scalar(
-                        out=weighted[g][:], in0=tanh[g, j][:], scalar1=enc_cols[:, j : j + 1], scalar2=None, op0=ALU.mult
-                    )
-                else:
-                    nc.vector.scalar_tensor_tensor(
-                        out=weighted[g][:],
-                        in0=tanh[g, j][:],
-                        scalar=enc_cols[:, j : j + 1],
-                        in1=weighted[g][:],
-                        op0=ALU.mult,
-                        op1=ALU.add,
-                    )
+        def add_to(total, g, j, c):
+            nc.vector.scalar_tensor_tensor(
+                out=total[:, c],
+                in0=tanh[g, j][:, c],
+                scalar=enc_cols[:, j : j + 1],
+                in1=total[:, c],
+                op0=ALU.mult,
+                op1=ALU.add,
+            )
 
-        def add_transposed(bank, terms, blocks):
+        def weigh(g, j):
+            if g < LAST and j in SCALED:
+                scaled[g, j] = work.tile([P, GROUP], F32, tag="scaled", name="scaled", bufs=16)
+                scale_by_enc(scaled[g, j][:], g, j)
+                return
+            total = (g, "late") if g == LAST and j in LATE_CHUNKS else (g, "early")
+            if total not in weighted:
+                weighted[total] = work.tile([P, GROUP], F32, tag="weighted", name="weighted", bufs=5)
+                scale_by_enc(weighted[total][:], g, j)
+            elif total[1] == "late":
+                for h in range(2):
+                    add_to(weighted[total], g, j, slice(h * FACES, (h + 1) * FACES))
+            else:
+                add_to(weighted[total], g, j, whole)
+
+        def turn(bank, terms, a):
+            for i in range(len(terms)):
+                nc.tensor.matmul(
+                    out=bank,
+                    lhsT=terms[i][:, a * P : (a + 1) * P],
+                    rhs=ident[:],
+                    is_transpose=True,
+                    start=(i == 0),
+                    stop=(i == len(terms) - 1),
+                )
+
+        def turn_group(g, blocks):
+            if g not in turned:
+                turned[g] = psum.tile([P, BLOCKS, P], F32, tag="turned", name="turned", bufs=1)
+            terms = [weighted[g, "early"]] + [scaled[g, j] for j in SCALED]
             for a in blocks:
-                for i in range(len(terms)):
-                    nc.tensor.matmul(
-                        out=bank[:, a, :],
-                        lhsT=terms[i][:, a * P : (a + 1) * P],
-                        rhs=ident[:],
-                        is_transpose=True,
-                        start=(i == 0),
-                        stop=(i == len(terms) - 1),
-                    )
+                turn(turned[g][:, a, :], terms, a)
 
-        def add_group(g, blocks):
-            if g not in acc:
-                acc[g] = psum.tile([P, BLOCKS, P], F32, tag="sums", name="acc", bufs=1)
-            terms = [weighted[g]] if g in weighted else []
-            add_transposed(acc[g], terms + [scaled[g, j] for j in scaled_chunks(g)], blocks)
-
-        def reduce_channels(g, bank, cols, h0=0, h1=2):
+        def reduce_channels(g, bank, to, hs=slice(0, 2)):
+            by_grid = to[:, 0:ROWS].rearrange("p (half b) -> p b half", half=2)
             nc.vector.tensor_reduce(
-                out=cols[:, 0:ROWS].rearrange("p (f b) -> p b f", f=2)[:, 2 * g + h0 : 2 * g + h1, :],
-                in_=bank[:].rearrange("p (h f) c -> p h f c", f=2)[:, h0:h1, :, :],
+                out=by_grid[:, 2 * g + hs.start : 2 * g + hs.stop, :],
+                in_=bank[:].rearrange("p (h half) c -> p h half c", half=2)[:, hs, :, :],
                 axis=ALONG_FREE,
                 op=ALU.add,
             )
 
-        def reduce_on_scalar(g, bank, cols):
+        def reduce_on_scalar(g, bank, to):
             for a in range(BLOCKS):
-                n = GRIDS * (a % 2) + 2 * g + a // 2
+                h, half = divmod(a, 2)
+                n = GRIDS * half + 2 * g + h
                 spare = work.tile([P, P], F32, tag="spare", name="spare", bufs=4)
-                nc.scalar.activation(out=spare[:], in_=bank[:, a, :], func=ACT.Copy, accum_out=cols[:, n : n + 1])
+                nc.scalar.activation(out=spare[:], in_=bank[:, a, :], func=ACT.Copy, accum_out=to[:, n : n + 1])
 
-        AT_FLIP, AT_COPY, AT_QE, AT_LAYER1, AT_INT, AT_QX = -15, -14, -12, -9, -5, -3
-
-        def slot(n):
-            def group_at(offset):
-                m = n - offset
-                return m // 4 if m % 4 == 0 else -1
-
-            def group_from(offset, first):
-                g = group_at(offset)
-                return g if g >= first else -1
-
-            m = n - AT_LAYER1
-            if m >= PACK:
-                layer1_product(m // PACK, m % PACK, whole)
-            def flips():
-                flip_edge_hid(2 * group_from(AT_FLIP, 2))
-                if group_from(AT_FLIP + FL_POS, 2) > 0:
-                    flip_edge_hid(2 * group_from(AT_FLIP + FL_POS, 2) + 1)
-
-            if FL_AFTER == 0:
-                flips()
-            layer2_product(n)
-            if FL_AFTER == 1:
-                flips()
-            for g in range(LAST):
-                for at, blocks in RUNS:
-                    if n == (RUN_6A if g == LAST - 1 else 4 * g + at):
-                        add_group(g, blocks)
-            if FL_AFTER == 2:
-                flips()
-
-            g = group_from(AT_COPY, 2)
-            copies = [2 * g] if g > 0 else []
-            g = group_from(AT_COPY + FL_POS, 2)
-            copies += [2 * g + 1] if g > 0 else []
-            for b in copies:
-                if b in COPIED_BY_SCALAR:
-                    copy_edge_hid(b, nc.scalar.copy)
-            if m >= PACK:
-                gelu(m // PACK, m % PACK, whole)
-            tanh_of(n)
-
-            for b in copies:
-                if b not in COPIED_BY_SCALAR:
-                    copy_edge_hid(b, nc.vector.tensor_copy)
-            for g in range(LAST - 1):
-                if n == 4 * g + REDUCE:
-                    reduce_channels(g, acc[g], w_cols)
-            if n == REDUCE_6:
-                if ACT_6:
-                    reduce_on_scalar(LAST - 1, acc[LAST - 1], w_cols)
-                elif not LATE_6:
-                    reduce_channels(LAST - 1, acc[LAST - 1], w_cols)
-            if group_at(AT_INT) >= 0:
-                interleave(2 * group_at(AT_INT))
-            if group_at(AT_INT + 1) >= 0:
-                interleave(2 * group_at(AT_INT + 1) + 1)
-            weigh(n - 1, 0)
-            if group_from(AT_QE, 2) > 0:
-                quantise_edge_hid(group_from(AT_QE, 2), whole)
-            if group_at(AT_QX) >= 0:
-                quantise_x(group_at(AT_QX))
-            weigh(n - 1, 1)
-
-        enc_cols = cols[:, 0:CHUNKS]
-        b3_cols = cols[:, CHUNKS : 2 * CHUNKS]
         enc_sq = keep.tile([P, CHUNKS], F32, name="enc_sq")
         enc_sq_sum = keep.tile([P, 1], F32, name="enc_sq_sum")
         norm = keep.tile([P, 1], F32, name="norm")
@@ -488,29 +328,27 @@ def tile_fluxgnn1dlatent_pb_t_kernel(
         u_gain = keep.tile([ROWS, P], F32, name="u_gain")
         right = keep.tile([ROWS, P], F32, name="right")
         result = keep.tile([ROWS, P], F32, name="result")
-        norm_bank = {}
+        norm_bank = []
 
-        def prepare(step_number):
-            if not first_time("p", step_number):
-                return
-            if step_number == 0:
+        def prepare(n):
+            if n == -1:
                 nc.vector.tensor_tensor(out=enc_sq[:], in0=enc_cols, in1=enc_cols, op=ALU.mult)
-            if step_number == 1:
+            if n == 0:
                 nc.vector.tensor_reduce(out=enc_sq_sum[:], in_=enc_sq[:], axis=ALONG_FREE, op=ALU.add)
-            if step_number == 4:
-                norm_bank[0] = psum.tile([P, P], F32, tag="product", name="enc_sq_all", bufs=PRODUCT_BANKS)
+            if n == 3:
+                norm_bank.append(product_bank([P, P], "norm_bank"))
                 nc.tensor.matmul(
                     out=norm_bank[0][:], lhsT=enc_sq_sum[:, 0:1].to_broadcast([P, P]), rhs=ident[:], start=True, stop=True
                 )
-            if step_number == 5:
+            if n == 4:
                 nc.vector.tensor_reduce(out=norm[:], in_=norm_bank[0][:], axis=ALONG_FREE, op=ALU.add)
-            if step_number == 6:
+            if n == 5:
                 nc.vector.tensor_scalar_add(out=norm_eps[:], in0=norm[:], scalar1=1e-12)
-            if step_number == 7:
+            if n == 6:
                 nc.vector.reciprocal(out=inv_norm[:], in_=norm_eps[:])
-            if step_number == 8:
+            if n == 7:
                 nc.vector.tensor_scalar_mul(out=scale[:], in0=inv_norm[:], scalar1=0.125)
-            if step_number == 9:
+            if n == 8:
                 nc.vector.tensor_scalar(
                     out=u_gain[:],
                     in0=u_rows[:],
@@ -520,102 +358,135 @@ def tile_fluxgnn1dlatent_pb_t_kernel(
                     op1=ALU.mult,
                 )
 
-        halves = [slice(0, FACES), slice(FACES, GROUP)]
+        def slot(n):
+            def group_at(offset, first=0):
+                g, beside = divmod(n - offset, 4)
+                return g if beside == 0 and first <= g < GROUPS else -1
+
+            def in_slot(n):
+                return slots[n] if 0 <= n < len(slots) else []
+
+            g1, t1 = divmod(n - AT_LAYER1, PACK)
+            if 1 <= g1 < GROUPS:
+                product1[g1, t1] = product_bank([P, GROUP], "product1")
+                multiply_by_w2(product1[g1, t1][:], g1, t1, whole)
+            for g, j in in_slot(n):
+                layer2_product(g, j)
+            g = group_at(AT_FLIP, 2)
+            if g >= 0:
+                flip_grid(2 * g)
+                flip_grid(2 * g + 1)
+            for i in range(2):
+                g = group_at(AT_TURN + i)
+                if 0 <= g < LAST - 1:
+                    turn_group(g, (2 * i, 2 * i + 1))
+            if n == len(slots) - 1:
+                turn_group(LAST - 1, range(BLOCKS))
+
+            g = group_at(AT_COPY, 2)
+            copies = (2 * g, 2 * g + 1) if g >= 0 else ()
+            for b in copies:
+                if b in COPIED_BY_SCALAR:
+                    copy_grid(b, nc.scalar.copy)
+            if 1 <= g1 < GROUPS:
+                gelu(product1[g1, t1][:], g1, t1, whole)
+            for g, j in in_slot(n):
+                tanh_of(g, j)
+            if n == len(slots):
+                reduce_on_scalar(LAST - 1, turned[LAST - 1], w_cols)
+
+            for b in copies:
+                if b not in COPIED_BY_SCALAR:
+                    copy_grid(b, nc.vector.tensor_copy)
+            g = group_at(AT_REDUCE)
+            if 0 <= g < LAST - 1:
+                reduce_channels(g, turned[g], w_cols)
+            g = group_at(AT_INTERLEAVE)
+            if g > 0:
+                interleave(2 * g)
+            g = group_at(AT_INTERLEAVE + 1)
+            if g >= 0:
+                interleave(2 * g + 1)
+            for job in in_slot(n - 1)[:1]:
+                weigh(*job)
+            g = group_at(AT_QUANTISE_EDGE, 2)
+            if g >= 0:
+                quantise_edge_hid(g, whole)
+            g = group_at(AT_QUANTISE_X)
+            if g >= 0:
+                quantise_x(g)
+            for job in in_slot(n - 1)[1:]:
+                weigh(*job)
+
         on_vector, on_scalar = nc.vector.tensor_copy, nc.scalar.copy
-        for what in HEAD.split():
-            op, arg = what[0], what[1:]
-            if op == "w":
-                stir(int(arg))
-            if op == "f":
-                flip_edge_hid(int(arg))
-            if op == "v":
-                copy_edge_hid(int(arg), on_vector)
-            if op == "s":
-                copy_edge_hid(int(arg), on_scalar)
-            if op == "F":
-                flip_block(int(arg))
-            if op == "V":
-                copy_block(int(arg), on_vector)
-            if op == "A":
-                copy_block(int(arg), on_scalar)
-            if op == "Q":
-                quantise_edge_hid(0, slice(int(arg) * P, (int(arg) + 1) * P))
-            if op == "B":
-                block_layer1(int(arg))
-                block_gelu(int(arg))
-            if op == "p":
-                prepare(int(arg))
-            if op == "R":
-                nc.vector.tensor_copy(out=rows[:], in_=rows_bf[:])
-            if op == "h":
-                quantise_edge_hid(0, halves[int(arg)])
-            if op == "q":
-                quantise_edge_hid(int(arg), whole)
-            if op == "g":
-                for t in range(PACK):
-                    layer1_product(0, t, halves[int(arg)])
-                    gelu(0, t, halves[int(arg)])
-            if op == "G":
-                layer1_product(int(arg[0]), int(arg[1]), whole)
-                gelu(int(arg[0]), int(arg[1]), whole)
-            if op == "c":
-                cols_ps = psum.tile([P, P], F32, tag="product", name="cols_ps", bufs=PRODUCT_BANKS)
-                nc.tensor.transpose(cols_ps[:], rows[:], ident[:])
-            if op == "C":
-                nc.vector.tensor_copy(out=cols[:, 0 : 2 * CHUNKS], in_=cols_ps[:, 0 : 2 * CHUNKS])
-            if op == "i":
-                interleave(int(arg))
-            if op == "x":
-                quantise_x(int(arg))
 
-        for n in range(-7, len(slots) + 1):
-            prepare(n + 1)
+        def quantise_block(k):
+            quantise_edge_hid(0, slice(k * P, (k + 1) * P))
+
+        stir(6)
+        flip_block(0, flip_bank([P, 2, P], "e_block"))
+        copy_block(0, on_scalar)
+        flip_block(1, flip_bank([P, 2, P], "e_block"))
+        stir(1)
+        copy_block(1, on_scalar)
+        quantise_block(0)
+        flip_block(2, product_bank([P, 2, P], "e_block"))
+        flip_block(3, product_bank([P, 2, P], "e_block"))
+        layer1_of_block(0)
+        quantise_block(1)
+        copy_block(2, on_vector)
+        copy_block(3, on_vector)
+        layer1_of_block(1)
+        flip_grid(2)
+        copy_grid(2, on_scalar)
+        flip_grid(3)
+        quantise_block(2)
+        layer1_of_block(2)
+        quantise_block(3)
+        layer1_of_block(3)
+        copy_grid(3, on_vector)
+        nc.vector.tensor_copy(out=rows[:], in_=rows_bf[:])
+        cols_bank = product_bank([P, P], "cols_bank")
+        nc.tensor.transpose(cols_bank[:], rows[:], ident[:])
+        quantise_edge_hid(1, whole)
+        nc.vector.tensor_copy(out=cols[:], in_=cols_bank[:, 0 : 2 * CHUNKS])
+        interleave(0)
+
+        for n in range(4 * 2 + AT_FLIP, len(slots) + 1):
+            prepare(n)
             slot(n)
-        assert sorted(covered) == [(g, j) for g in range(GROUPS) for j in range(CHUNKS)]
 
-        early_bank = psum.tile([P, BLOCKS, P], F32, tag="flip", name="early_bank", bufs=FLIP_BANKS)
-        late_bank = psum.tile([P, BLOCKS, P], F32, tag="flip", name="late_bank", bufs=FLIP_BANKS)
-        stir(WARM_END)
-        if LATE_6 and not ACT_6:
-            reduce_channels(LAST - 1, acc[LAST - 1], w_cols)
-        split = len(SC_LAST) if LATE_CHUNKS else len(SC_LAST) - N_LATE
-        add_transposed(early_bank, [weighted[LAST]] + [scaled[LAST, j] for j in SC_LAST[:split]], range(BLOCKS))
-        if ACT_7:
-            reduce_on_scalar(LAST, early_bank, w_cols)
-        else:
-            reduce_channels(LAST, early_bank, w_cols)
-        add_transposed(late_bank, [weighted["late"]] if LATE_CHUNKS else [scaled[LAST, j] for j in SC_LAST[split:]], range(BLOCKS))
-        reduce_channels(LAST, late_bank, w_late, 0, 1)
-        reduce_channels(LAST, late_bank, w_late, 1, 2)
-        faces = psum.tile([P, 2, P], F32, tag="product", name="faces", bufs=PRODUCT_BANKS)
+        early_bank = flip_bank([P, BLOCKS, P], "early_bank")
+        late_bank = flip_bank([P, BLOCKS, P], "late_bank")
+        stir(2)
+        for a in range(BLOCKS):
+            turn(early_bank[:, a, :], [weighted[LAST, "early"]], a)
+        reduce_on_scalar(LAST, early_bank, w_cols)
+        for a in range(BLOCKS):
+            turn(late_bank[:, a, :], [weighted[LAST, "late"]], a)
+        for h in range(2):
+            reduce_channels(LAST, late_bank, w_late, slice(h, h + 1))
+        faces = product_bank([P, 2, P], "faces")
         for k in range(2):
-            for cols_of, first in ((w_cols, True), (w_late, False)):
-                nc.tensor.matmul(
-                    out=faces[:, k, :],
-                    lhsT=cols_of[:, k * GRIDS : k * GRIDS + P],
-                    rhs=ident[:],
-                    is_transpose=True,
-                    start=first,
-                    stop=not first,
-                )
+            shifted = slice(k * GRIDS, k * GRIDS + P)
+            turn(faces[:, k, :], [w_cols[:, shifted], w_late[:, shifted]], 0)
         row = faces[0:ROWS, :, :].rearrange("r k i -> r (k i)")
-        for a in range(2):
-            part = slice(a * P // 2, (a + 1) * P // 2)
+        halves = [slice(0, P // 2), slice(P // 2, P)]
+        for c in halves:
             nc.vector.scalar_tensor_tensor(
-                out=right[:, part],
-                in0=row[:, part.start + 1 : part.stop + 1],
+                out=right[:, c],
+                in0=row[:, c.start + 1 : c.stop + 1],
                 scalar=scale[0:ROWS, 0:1],
-                in1=u_gain[:, part],
+                in1=u_gain[:, c],
                 op0=ALU.mult,
                 op1=ALU.subtract,
             )
-        for a in range(2):
-            part = slice(a * P // 2, (a + 1) * P // 2)
+        for c in halves:
             nc.vector.scalar_tensor_tensor(
-                out=result[:, part],
-                in0=row[:, part],
+                out=result[:, c],
+                in0=row[:, c],
                 scalar=scale[0:ROWS, 0:1],
-                in1=right[:, part],
+                in1=right[:, c],
                 op0=ALU.mult,
                 op1=ALU.subtract,
             )

from contextlib import ExitStack

import concourse.mybir as mybir
from concourse.masks import make_identity

F32 = mybir.dt.float32
BF16 = mybir.dt.bfloat16
I32 = mybir.dt.int32
U32 = mybir.dt.uint32
U8 = mybir.dt.uint8
FP8X4 = mybir.dt.float8_e4m3fn_x4
ACT = mybir.ActivationFunctionType
ALU = mybir.AluOpType
ALONG_FREE = mybir.AxisListType.X

P = 128
GRIDS = 16
FACES = 256
CELLS = 255
HID = 512
LATENT = 1024
PACK = 4
GROUP = 2 * FACES
GROUPS = GRIDS // 2
LAST = GROUPS - 1
CHUNKS = LATENT // P
BLOCKS = GROUP // P
ROWS = 2 * GRIDS

FLIP_BANKS = 2
PRODUCT_BANKS = 5

SCALED = (3, 5, 7)
LATE_CHUNKS = (5, 7)
COPIED_BY_SCALAR = (5, 13)

AT_FLIP, AT_COPY, AT_QUANTISE_EDGE, AT_LAYER1 = -15, -14, -12, -9
AT_INTERLEAVE, AT_QUANTISE_X = -5, -3
AT_TURN, AT_REDUCE = 8, 10

FLOPS = 2 * GRIDS * FACES * HID * (HID + LATENT)


def tile_fluxgnn1dlatent_pb_t_kernel(
    tc, edge_hid, u, enc, W2_words, W2_scales, b2, W3_words, W3_scales, b3, out
):
    nc = tc.nc
    tokens = edge_hid.flatten_outer_dims()

    with ExitStack() as ctx:
        ctx.enter_context(tc.manual_schedule())
        keep = ctx.enter_context(tc.tile_pool(name="keep", bufs=1))
        work = ctx.enter_context(tc.tile_pool(name="work", bufs=2))
        psum = ctx.enter_context(tc.psum_pool(name="psum", bufs=1))

        e_in = [keep.tile([P, 2, HID], BF16, name="e_in%d" % b) for b in range(GRIDS)]
        w2_raw_words = keep.tile([P, HID], U32, name="w2_raw_words", align_bytes=64)
        w2_raw_plane = keep.tile([P, HID], U8, name="w2_raw_plane", align_bytes=64)
        w2_words = keep.tile([P, HID], U32, name="w2_words", align_bytes=64)
        w2_plane = keep.tile([P, HID], U8, name="w2_plane", align_bytes=64)
        w3_words = keep.tile([P, LATENT], U32, name="w3_words", align_bytes=64)
        w3_plane = keep.tile([P, LATENT], U8, name="w3_plane", align_bytes=64)
        rows_bf = keep.tile([P, P], BF16, name="rows_bf")
        rows = keep.tile([P, P], F32, name="rows")
        cols = keep.tile([P, 2 * CHUNKS], F32, name="cols")
        enc_cols = cols[:, 0:CHUNKS]
        b3_cols = cols[:, CHUNKS : 2 * CHUNKS]
        ident = keep.tile([P, P], F32, name="ident")
        b2_bf = keep.tile([P, PACK], BF16, name="b2_bf")
        b2_cols = keep.tile([P, PACK], F32, name="b2_cols")
        u_rows = keep.tile([ROWS, P], BF16, name="u_rows")
        w_cols = keep.tile([P, P + GRIDS], F32, name="w_cols")
        w_late = keep.tile([P, P + GRIDS], F32, name="w_late")
        warm = keep.tile([P, 1], F32, name="warm")
        warm_out = keep.tile([P, 1], F32, name="warm_out")
        noise = keep.tile([P, GROUP], BF16, name="noise")

        nc.vector.memset(w2_raw_plane[:].bitcast(I32), 0)
        nc.vector.memset(rows_bf[:], 0.0)
        nc.vector.memset(warm[:], 0.0)
        nc.vector.memset(noise[:], 0.0)
        nc.vector.memset(w3_plane[:].bitcast(I32), 0)
        make_identity(nc, ident[:])
        nc.vector.memset(u_rows[:], 0.0)
        nc.vector.memset(w_cols[:], 0.0)
        nc.vector.memset(w_late[:], 0.0)

        def load_grid(b, start=nc.sync.dma_start):
            start(
                out=e_in[b][:],
                in_=tokens[b * FACES : (b + 1) * FACES, :].rearrange("(n p) k -> p n k", p=P),
            )

        def load_words(words_tile, words):
            nc.sync.dma_start(
                out=words_tile[:].bitcast(I32),
                in_=words[0].rearrange("p n t -> p (n t)").bitcast(I32),
            )

        def load_plane(plane_tile, scales):
            for quad in range(4):
                nc.sync.dma_start(
                    out=plane_tile[32 * quad : 32 * quad + 4, :].bitcast(I32),
                    in_=scales[0, 4 * quad : 4 * quad + 4, :].bitcast(I32),
                )

        load_plane(w2_raw_plane, W2_scales)
        load_grid(0, nc.scalar.dma_start)
        nc.scalar.dma_start(out=b2_bf[:], in_=b2.rearrange("(p t) -> p t", t=PACK))
        load_words(w2_raw_words, W2_words)
        for b in range(1, 4):
            load_grid(b)
        nc.sync.dma_start(out=rows_bf[0:CHUNKS, :], in_=enc.rearrange("(j p) -> j p", p=P))
        nc.sync.dma_start(out=rows_bf[CHUNKS : 2 * CHUNKS, :], in_=b3.rearrange("(j p) -> j p", p=P))
        for b in range(4, 6):
            load_grid(b)
        load_words(w3_words, W3_words)
        load_plane(w3_plane, W3_scales)
        for b in range(6, GRIDS):
            load_grid(b)
        nc.sync.dma_start(out=u_rows[0:GRIDS, :], in_=u[:, 0:P])
        nc.sync.dma_start(out=u_rows[GRIDS:ROWS, 0 : CELLS - P], in_=u[:, P:CELLS])

        nc.scalar.activation(out=warm_out[:], in_=warm[:], func=ACT.Gelu)

        for t in range(PACK):
            nc.vector.tensor_copy(
                out=w2_plane[:, t * P : (t + 1) * P], in_=w2_raw_plane[:, t : HID : PACK]
            )
        nc.vector.tensor_copy(
            out=w2_words[:].bitcast(I32).rearrange("p (t m) -> p t m", t=PACK),
            in_=w2_raw_words[:].bitcast(I32).rearrange("p (m t) -> p t m", t=PACK),
        )
        nc.vector.tensor_copy(out=b2_cols[:], in_=b2_bf[:])

        e_bank, e_grouped, e_codes, e_plane = {}, {}, {}, {}
        product1, x_raw, x_grouped, x_codes, x_plane = {}, {}, {}, {}, {}
        product2, tanh, weighted, scaled, turned = {}, {}, {}, {}, {}

        def product_bank(shape, name):
            return psum.tile(shape, F32, tag="product", name=name, bufs=PRODUCT_BANKS)

        def flip_bank(shape, name):
            return psum.tile(shape, F32, tag="flip", name=name, bufs=FLIP_BANKS)

        def stir(n):
            bank = product_bank([P, GROUP], "stirred")
            for i in range(n):
                nc.tensor.matmul(out=bank[:], lhsT=noise[:, 0:P], rhs=noise[:], start=True, stop=True)

        def flip(bank, b, n, first):
            words = e_in[b][:].bitcast(F32)
            for w in range(2):
                nc.tensor.transpose(bank[:, w, first : first + P], words[:, n, w : HID // 2 : 2], ident[:])

        def copy_turned(bank, first, count, copy):
            g, first = divmod(first, GROUP)
            if g not in e_grouped:
                e_grouped[g] = work.tile([P, GROUP, PACK], BF16, tag="e_grouped", name="e_grouped", align_bytes=64)
            rows_of = e_grouped[g][:, first : first + count, :].rearrange("p r t -> p (r t)")
            copy(
                out=rows_of.bitcast(F32).rearrange("p (r w) -> p r w", w=2),
                in_=bank[:].rearrange("p w r -> p r w"),
            )

        def flip_grid(b):
            e_bank[b] = flip_bank([P, 2, FACES], "e_bank")
            for n in range(2):
                flip(e_bank[b], b, n, n * P)

        def copy_grid(b, copy):
            copy_turned(e_bank[b], b * FACES, FACES, copy)

        def flip_block(k, bank):
            e_bank["block", k] = bank
            flip(bank, k // 2, k % 2, 0)

        def copy_block(k, copy):
            copy_turned(e_bank["block", k], k * P, P, copy)

        def quantise_edge_hid(g, c):
            if g not in e_codes:
                e_codes[g] = work.tile([P, GROUP], U32, tag="e_codes", name="e_codes", bufs=3, align_bytes=64)
                e_plane[g] = work.tile([P, GROUP], U8, tag="e_plane", name="e_plane", bufs=3, align_bytes=64)
            nc.vector.quantize_mx(
                out=e_codes[g][:, c].bitcast(FP8X4),
                scales=e_plane[g][:, c],
                in_=e_grouped[g][:, c, :].rearrange("p r t -> p (r t)"),
            )

        def multiply_by_w2(product, g, t, c):
            nc.tensor.matmul_mx(
                out=product,
                lhsT=w2_words[:, t * P : (t + 1) * P].bitcast(FP8X4),
                lhsT_scale=w2_plane[:, t * P : (t + 1) * P],
                rhs=e_codes[g][:, c].bitcast(FP8X4),
                rhs_scale=e_plane[g][:, c],
                start=True,
                stop=True,
            )

        def gelu(product, g, t, c):
            if g not in x_raw:
                x_raw[g] = work.tile([P, PACK, GROUP], BF16, tag="x_raw", name="x_raw", bufs=3)
            nc.scalar.activation(out=x_raw[g][:, t, c], in_=product, func=ACT.Gelu, bias=b2_cols[:, t : t + 1])

        def layer1_of_block(k):
            c = slice(k * P, (k + 1) * P)
            bank = product_bank([P, PACK, P], "block_product")
            for t in range(PACK):
                multiply_by_w2(bank[:, t, :], 0, t, c)
            for t in range(PACK):
                gelu(bank[:, t, :], 0, t, c)

        whole = slice(0, GROUP)

        def interleave(b):
            g, h = divmod(b, 2)
            c = slice(h * FACES, (h + 1) * FACES)
            if h == 0:
                x_grouped[g] = work.tile([P, GROUP, PACK], BF16, tag="x_grouped", name="x_grouped", align_bytes=64)
            nc.vector.tensor_copy(
                out=x_grouped[g][:, c, :].rearrange("p (c i) t -> p c t i", i=4),
                in_=x_raw[g][:, :, c].rearrange("p t (c i) -> p c t i", i=4),
            )

        def quantise_x(g):
            x_codes[g] = work.tile([P, GROUP], U32, tag="x_codes", name="x_codes", bufs=4, align_bytes=64)
            x_plane[g] = work.tile([P, GROUP], U8, tag="x_plane", name="x_plane", bufs=4, align_bytes=64)
            nc.vector.quantize_mx(
                out=x_codes[g][:].bitcast(FP8X4),
                scales=x_plane[g][:],
                in_=x_grouped[g][:].rearrange("p r t -> p (r t)"),
            )

        jobs = sorted(
            [(g, j) for g in range(GROUPS) for j in range(CHUNKS)],
            key=lambda job: (CHUNKS // 2 * job[0] + job[1], job[0]),
        )
        slots = [jobs[i : i + 2] for i in range(0, len(jobs), 2)]

        def layer2_product(g, j):
            product2[g, j] = product_bank([P, GROUP], "product2")
            nc.tensor.matmul_mx(
                out=product2[g, j][:],
                lhsT=w3_words[:, j * P : (j + 1) * P].bitcast(FP8X4),
                lhsT_scale=w3_plane[:, j * P : (j + 1) * P],
                rhs=x_codes[g][:].bitcast(FP8X4),
                rhs_scale=x_plane[g][:],
                start=True,
                stop=True,
            )

        def tanh_of(g, j):
            tanh[g, j] = work.tile([P, GROUP], F32, tag="tanh", name="tanh", bufs=12)
            nc.scalar.activation(out=tanh[g, j][:], in_=product2[g, j][:], func=ACT.Tanh, bias=b3_cols[:, j : j + 1])

        def scale_by_enc(out, g, j):
            nc.vector.tensor_scalar(
                out=out, in0=tanh[g, j][:], scalar1=enc_cols[:, j : j + 1], scalar2=None, op0=ALU.mult
            )

        def add_to(total, g, j, c):
            nc.vector.scalar_tensor_tensor(
                out=total[:, c],
                in0=tanh[g, j][:, c],
                scalar=enc_cols[:, j : j + 1],
                in1=total[:, c],
                op0=ALU.mult,
                op1=ALU.add,
            )

        def weigh(g, j):
            if g < LAST and j in SCALED:
                scaled[g, j] = work.tile([P, GROUP], F32, tag="scaled", name="scaled", bufs=16)
                scale_by_enc(scaled[g, j][:], g, j)
                return
            total = (g, "late") if g == LAST and j in LATE_CHUNKS else (g, "early")
            if total not in weighted:
                weighted[total] = work.tile([P, GROUP], F32, tag="weighted", name="weighted", bufs=5)
                scale_by_enc(weighted[total][:], g, j)
            elif total[1] == "late":
                for h in range(2):
                    add_to(weighted[total], g, j, slice(h * FACES, (h + 1) * FACES))
            else:
                add_to(weighted[total], g, j, whole)

        def turn(bank, terms, a):
            for i in range(len(terms)):
                nc.tensor.matmul(
                    out=bank,
                    lhsT=terms[i][:, a * P : (a + 1) * P],
                    rhs=ident[:],
                    is_transpose=True,
                    start=(i == 0),
                    stop=(i == len(terms) - 1),
                )

        def turn_group(g, blocks):
            if g not in turned:
                turned[g] = psum.tile([P, BLOCKS, P], F32, tag="turned", name="turned", bufs=1)
            terms = [weighted[g, "early"]] + [scaled[g, j] for j in SCALED]
            for a in blocks:
                turn(turned[g][:, a, :], terms, a)

        def reduce_channels(g, bank, to, hs=slice(0, 2)):
            by_grid = to[:, 0:ROWS].rearrange("p (half b) -> p b half", half=2)
            nc.vector.tensor_reduce(
                out=by_grid[:, 2 * g + hs.start : 2 * g + hs.stop, :],
                in_=bank[:].rearrange("p (h half) c -> p h half c", half=2)[:, hs, :, :],
                axis=ALONG_FREE,
                op=ALU.add,
            )

        def reduce_on_scalar(g, bank, to):
            for a in range(BLOCKS):
                h, half = divmod(a, 2)
                n = GRIDS * half + 2 * g + h
                spare = work.tile([P, P], F32, tag="spare", name="spare", bufs=4)
                nc.scalar.activation(out=spare[:], in_=bank[:, a, :], func=ACT.Copy, accum_out=to[:, n : n + 1])

        enc_sq = keep.tile([P, CHUNKS], F32, name="enc_sq")
        enc_sq_sum = keep.tile([P, 1], F32, name="enc_sq_sum")
        norm = keep.tile([P, 1], F32, name="norm")
        norm_eps = keep.tile([P, 1], F32, name="norm_eps")
        inv_norm = keep.tile([P, 1], F32, name="inv_norm")
        scale = keep.tile([P, 1], F32, name="scale")
        u_gain = keep.tile([ROWS, P], F32, name="u_gain")
        right = keep.tile([ROWS, P], F32, name="right")
        result = keep.tile([ROWS, P], F32, name="result")
        norm_bank = []

        def prepare(n):
            if n == -1:
                nc.vector.tensor_tensor(out=enc_sq[:], in0=enc_cols, in1=enc_cols, op=ALU.mult)
            if n == 0:
                nc.vector.tensor_reduce(out=enc_sq_sum[:], in_=enc_sq[:], axis=ALONG_FREE, op=ALU.add)
            if n == 3:
                norm_bank.append(product_bank([P, P], "norm_bank"))
                nc.tensor.matmul(
                    out=norm_bank[0][:], lhsT=enc_sq_sum[:, 0:1].to_broadcast([P, P]), rhs=ident[:], start=True, stop=True
                )
            if n == 4:
                nc.vector.tensor_reduce(out=norm[:], in_=norm_bank[0][:], axis=ALONG_FREE, op=ALU.add)
            if n == 5:
                nc.vector.tensor_scalar_add(out=norm_eps[:], in0=norm[:], scalar1=1e-12)
            if n == 6:
                nc.vector.reciprocal(out=inv_norm[:], in_=norm_eps[:])
            if n == 7:
                nc.vector.tensor_scalar_mul(out=scale[:], in0=inv_norm[:], scalar1=0.125)
            if n == 8:
                nc.vector.tensor_scalar(
                    out=u_gain[:],
                    in0=u_rows[:],
                    scalar1=norm[0:ROWS, 0:1],
                    scalar2=inv_norm[0:ROWS, 0:1],
                    op0=ALU.mult,
                    op1=ALU.mult,
                )

        def slot(n):
            def group_at(offset, first=0):
                g, beside = divmod(n - offset, 4)
                return g if beside == 0 and first <= g < GROUPS else -1

            def in_slot(n):
                return slots[n] if 0 <= n < len(slots) else []

            g1, t1 = divmod(n - AT_LAYER1, PACK)
            if 1 <= g1 < GROUPS:
                product1[g1, t1] = product_bank([P, GROUP], "product1")
                multiply_by_w2(product1[g1, t1][:], g1, t1, whole)
            for g, j in in_slot(n):
                layer2_product(g, j)
            g = group_at(AT_FLIP, 2)
            if g >= 0:
                flip_grid(2 * g)
                flip_grid(2 * g + 1)
            for i in range(2):
                g = group_at(AT_TURN + i)
                if 0 <= g < LAST - 1:
                    turn_group(g, (2 * i, 2 * i + 1))
            if n == len(slots) - 1:
                turn_group(LAST - 1, range(BLOCKS))

            g = group_at(AT_COPY, 2)
            copies = (2 * g, 2 * g + 1) if g >= 0 else ()
            for b in copies:
                if b in COPIED_BY_SCALAR:
                    copy_grid(b, nc.scalar.copy)
            if 1 <= g1 < GROUPS:
                gelu(product1[g1, t1][:], g1, t1, whole)
            for g, j in in_slot(n):
                tanh_of(g, j)
            if n == len(slots):
                reduce_on_scalar(LAST - 1, turned[LAST - 1], w_cols)

            for b in copies:
                if b not in COPIED_BY_SCALAR:
                    copy_grid(b, nc.vector.tensor_copy)
            g = group_at(AT_REDUCE)
            if 0 <= g < LAST - 1:
                reduce_channels(g, turned[g], w_cols)
            g = group_at(AT_INTERLEAVE)
            if g > 0:
                interleave(2 * g)
            g = group_at(AT_INTERLEAVE + 1)
            if g >= 0:
                interleave(2 * g + 1)
            for job in in_slot(n - 1)[:1]:
                weigh(*job)
            g = group_at(AT_QUANTISE_EDGE, 2)
            if g >= 0:
                quantise_edge_hid(g, whole)
            g = group_at(AT_QUANTISE_X)
            if g >= 0:
                quantise_x(g)
            for job in in_slot(n - 1)[1:]:
                weigh(*job)

        on_vector, on_scalar = nc.vector.tensor_copy, nc.scalar.copy

        def quantise_block(k):
            quantise_edge_hid(0, slice(k * P, (k + 1) * P))

        stir(6)
        flip_block(0, flip_bank([P, 2, P], "e_block"))
        copy_block(0, on_scalar)
        flip_block(1, flip_bank([P, 2, P], "e_block"))
        stir(1)
        copy_block(1, on_scalar)
        quantise_block(0)
        flip_block(2, product_bank([P, 2, P], "e_block"))
        flip_block(3, product_bank([P, 2, P], "e_block"))
        layer1_of_block(0)
        quantise_block(1)
        copy_block(2, on_vector)
        copy_block(3, on_vector)
        layer1_of_block(1)
        flip_grid(2)
        copy_grid(2, on_scalar)
        flip_grid(3)
        quantise_block(2)
        layer1_of_block(2)
        quantise_block(3)
        layer1_of_block(3)
        copy_grid(3, on_vector)
        nc.vector.tensor_copy(out=rows[:], in_=rows_bf[:])
        cols_bank = product_bank([P, P], "cols_bank")
        nc.tensor.transpose(cols_bank[:], rows[:], ident[:])
        quantise_edge_hid(1, whole)
        nc.vector.tensor_copy(out=cols[:], in_=cols_bank[:, 0 : 2 * CHUNKS])
        interleave(0)

        for n in range(4 * 2 + AT_FLIP, len(slots) + 1):
            prepare(n)
            slot(n)

        early_bank = flip_bank([P, BLOCKS, P], "early_bank")
        late_bank = flip_bank([P, BLOCKS, P], "late_bank")
        stir(2)
        for a in range(BLOCKS):
            turn(early_bank[:, a, :], [weighted[LAST, "early"]], a)
        reduce_on_scalar(LAST, early_bank, w_cols)
        for a in range(BLOCKS):
            turn(late_bank[:, a, :], [weighted[LAST, "late"]], a)
        for h in range(2):
            reduce_channels(LAST, late_bank, w_late, slice(h, h + 1))
        faces = product_bank([P, 2, P], "faces")
        for k in range(2):
            shifted = slice(k * GRIDS, k * GRIDS + P)
            turn(faces[:, k, :], [w_cols[:, shifted], w_late[:, shifted]], 0)
        row = faces[0:ROWS, :, :].rearrange("r k i -> r (k i)")
        halves = [slice(0, P // 2), slice(P // 2, P)]
        for c in halves:
            nc.vector.scalar_tensor_tensor(
                out=right[:, c],
                in0=row[:, c.start + 1 : c.stop + 1],
                scalar=scale[0:ROWS, 0:1],
                in1=u_gain[:, c],
                op0=ALU.mult,
                op1=ALU.subtract,
            )
        for c in halves:
            nc.vector.scalar_tensor_tensor(
                out=result[:, c],
                in0=row[:, c],
                scalar=scale[0:ROWS, 0:1],
                in1=right[:, c],
                op0=ALU.mult,
                op1=ALU.subtract,
            )
        nc.sync.dma_start(out=out[:, 0:P], in_=result[0:GRIDS, :])
        nc.scalar.dma_start(out=out[:, P:CELLS], in_=result[GRIDS:ROWS, 0 : CELLS - P])
